import numpy as np
import ml_dtypes


def mxq(x, axis, fmt="e4m3"):
    dtype, down = {"e4m3": (ml_dtypes.float8_e4m3fn, 7), "e5m2": (ml_dtypes.float8_e5m2, 14)}[fmt]
    v = np.moveaxis(np.asarray(x, np.float32).astype(ml_dtypes.bfloat16).astype(np.float64), axis, -1)
    blocks = v.reshape(v.shape[:-1] + (-1, 32))
    amax = np.abs(blocks).max(-1, keepdims=True)
    byte = np.maximum(np.where(amax > 0, np.frexp(amax)[1] - 1 + 127, 0) - down, 1)
    scale = np.exp2(byte - 127.0)
    codes = (blocks / scale).astype(np.float32).astype(dtype).astype(np.float64)
    return np.moveaxis((codes * scale).reshape(v.shape), -1, axis)


WIDE = False


def mx_kscale(k):
    if not WIDE:
        return np.ones(k)
    levels = np.array([10, -10, 5, -5, 0])
    a = np.random.permutation(np.resize(levels, k // 512 * 4)).reshape(k // 512, 4)
    idx = np.arange(k)
    return np.exp2(a[idx // 512, idx % 128 // 32])


BF16 = ml_dtypes.bfloat16


def bf(x):
    return np.asarray(x, np.float32).astype(BF16)


def f64(x):
    return np.asarray(x).astype(np.float64)


B, R, U, HID, G = 1024, 1024, 512, 1024, 1024
F = 2 * R + U
GAMMA_MAX = 2.0


def sigmoid(v):
    return 1.0 / (1.0 + np.exp(-v))


def setup_inputs():
    s = mx_kscale(U)
    w1 = np.random.standard_normal((HID, F)) / np.sqrt(F)
    w1[:, 2 * R:] /= s
    return {"y_tilde": bf(np.random.standard_normal((B, R))),
            "z_tilde": bf(np.random.standard_normal((B, R))),
            "u": bf(np.random.standard_normal((B, U)) * s),
            "dt": bf(0.3 + 0.2 * np.random.random(1)),
            "omega_sq": bf(1.0 + 0.1 * np.random.standard_normal(R)),
            "alpha_lambda": bf(-np.random.random(R) * 0.5),
            "B_tilde": bf(np.random.standard_normal((R, U)) / np.sqrt(U) / s),
            "dmlp_w1": bf(w1),
            "dmlp_b1": bf(np.random.standard_normal(HID) * 0.3),
            "dmlp_w2": bf(np.random.standard_normal((R, HID)) * 2.0 / np.sqrt(HID)),
            "dmlp_b2": bf(np.random.standard_normal(R) * 0.5)}


def reference(y_tilde, z_tilde, u, dt, omega_sq, alpha_lambda, B_tilde, dmlp_w1, dmlp_b1, dmlp_w2, dmlp_b2):
    y, z, step = f64(y_tilde), f64(z_tilde), f64(dt)
    fq = mxq(np.concatenate([y, z, f64(u)], axis=-1), 1, "e4m3")
    b_dot_u = fq[:, 2 * R:] @ mxq(f64(B_tilde), 1, "e4m3").T
    h = np.tanh((fq @ mxq(f64(dmlp_w1), 1, "e4m3").T) + f64(dmlp_b1))
    gamma_tilde = GAMMA_MAX * sigmoid((mxq(h, 1, "e4m3") @ mxq(f64(dmlp_w2), 1, "e4m3").T) + f64(dmlp_b2))
    z_next = z + step * (b_dot_u - (f64(omega_sq) - f64(alpha_lambda)) * y - gamma_tilde * z)
    y_next = y + step * z_next
    return z_next, gamma_tilde, y_next

@@ -1,0 +1,324 @@
+from contextlib import ExitStack
+
+import concourse.mybir as mybir
+from concourse.masks import make_identity
+
+BF16 = mybir.dt.bfloat16
+F32 = mybir.dt.float32
+U32 = mybir.dt.uint32
+U8 = mybir.dt.uint8
+FP8X4 = mybir.dt.float8_e4m3fn_x4
+ALU = mybir.AluOpType
+ACT = mybir.ActivationFunctionType
+
+P = 128
+PACK = 4
+K_PASS = P * PACK
+WORDS = K_PASS // 2
+BANK = 512
+PAIR = 2 * P
+
+BATCH = 1024
+MODES = 1024
+DRIVE = 512
+HIDDEN = 1024
+FEATS = 2 * MODES + DRIVE
+ROW_TILES = BATCH // P
+CHUNKS = BATCH // PAIR
+FEAT_PASSES = FEATS // K_PASS
+HID_PASSES = HIDDEN // K_PASS
+W1_UNITS = HIDDEN // PAIR
+
+FLOPS = 2 * BATCH * (HIDDEN * FEATS + MODES * DRIVE + MODES * HIDDEN)
+
+
+def tile_instrumentedlocmblock_pa_kernel(
+    tc, y_tilde, z_tilde, u, dt, omega_sq, alpha_lambda, B_tilde, dmlp_w1, dmlp_b1, dmlp_w2, dmlp_b2,
+    out_0, out_1, out_2,
+):
+    nc = tc.nc
+    with ExitStack() as ctx:
+        keep = ctx.enter_context(tc.tile_pool(name="keep", bufs=1))
+        weights_in = ctx.enter_context(tc.tile_pool(name="weights_in", bufs=4))
+        stage = ctx.enter_context(tc.tile_pool(name="stage", bufs=6))
+        hidden = ctx.enter_context(tc.tile_pool(name="hidden", bufs=2))
+        update = ctx.enter_context(tc.tile_pool(name="update", bufs=2))
+        psum = ctx.enter_context(tc.psum_pool(name="psum", bufs=1))
+
+        y_rows = y_tilde.rearrange("(p j) r -> p j r", j=ROW_TILES)
+        z_rows = z_tilde.rearrange("(p j) r -> p j r", j=ROW_TILES)
+        u_rows = u.rearrange("(p j) k -> p j k", j=ROW_TILES)
+        z_next_rows = out_0.rearrange("(p j) r -> p j r", j=ROW_TILES)
+        gamma_rows = out_1.rearrange("(p j) r -> p j r", j=ROW_TILES)
+        y_next_rows = out_2.rearrange("(p j) r -> p j r", j=ROW_TILES)
+        y_sb = keep.tile([P, ROW_TILES, MODES], BF16)
+        z_sb = keep.tile([P, ROW_TILES, MODES], BF16)
+        u_sb = keep.tile([P, ROW_TILES, DRIVE], BF16)
+
+        def load_chunk(c):
+            tiles = slice(2 * c, 2 * c + 2)
+            nc.sync.dma_start(out=y_sb[:, tiles, :], in_=y_rows[:, tiles, :])
+            nc.sync.dma_start(out=z_sb[:, tiles, :], in_=z_rows[:, tiles, :])
+            nc.sync.dma_start(out=u_sb[:, tiles, :], in_=u_rows[:, tiles, :])
+
+        w1_rows = dmlp_w1.rearrange("(n p e) f -> n p e f", p=P, e=2)
+        b_rows = B_tilde.rearrange("(i p) k -> p i k", p=P)
+        w2_rows = dmlp_w2.rearrange("(i p) k -> p i k", p=P)
+
+        load_chunk(0)
+        w1_raw = []
+        for n in range(W1_UNITS):
+            raw = weights_in.tile([P, 2, FEATS], BF16, tag="raw", name="w1_raw%d" % n)
+            nc.sync.dma_start(out=raw[:], in_=w1_rows[n])
+            w1_raw.append(raw)
+        load_chunk(1)
+        b_raw = weights_in.tile([P, ROW_TILES, DRIVE], BF16, tag="raw")
+        nc.sync.dma_start(out=b_raw[:], in_=b_rows)
+        w2_raw = []
+        for half in range(2):
+            raw = weights_in.tile([P, 4, HIDDEN], BF16, tag="raw", name="w2_raw%d" % half)
+            nc.sync.dma_start(out=raw[:], in_=w2_rows[:, 4 * half : 4 * half + 4, :])
+            w2_raw.append(raw)
+        load_chunk(2)
+        load_chunk(3)
+
+        ident = keep.tile([P, P], F32)
+        make_identity(nc, ident[:])
+
+        dt_bf = keep.tile([P, 1], BF16)
+        nc.scalar.dma_start(out=dt_bf[:], in_=dt.partition_broadcast(P))
+        dt_col = keep.tile([P, 1], F32)
+        minus_dt = keep.tile([P, 1], F32)
+        one_minus_dt = keep.tile([P, 1], F32)
+        nc.vector.tensor_copy(out=dt_col[:], in_=dt_bf[:])
+        nc.vector.tensor_scalar(out=minus_dt[:], in0=dt_col[:], scalar1=-1.0, scalar2=None, op0=ALU.mult)
+        nc.vector.tensor_scalar(
+            out=one_minus_dt[:], in0=dt_col[:], scalar1=-1.0, scalar2=1.0, op0=ALU.mult, op1=ALU.add
+        )
+
+        b1_rows = keep.tile([P, 2 * P], BF16)
+        nc.vector.memset(b1_rows[:], 0.0)
+        nc.scalar.dma_start(out=b1_rows[0:W1_UNITS, :], in_=dmlp_b1.rearrange("(n w) -> n w", n=W1_UNITS))
+        b1_bank = psum.tile([P, P], F32, tag="bank", bufs=3)
+        nc.tensor.transpose(b1_bank[:], b1_rows[:].bitcast(F32), ident[:])
+        b1_words = keep.tile([P, W1_UNITS], F32)
+        nc.vector.tensor_copy(out=b1_words[:], in_=b1_bank[:, 0:W1_UNITS])
+        b1_col = keep.tile([P, 2 * W1_UNITS], F32)
+        nc.vector.tensor_copy(out=b1_col[:], in_=b1_words[:].bitcast(BF16))
+
+        vectors = keep.tile([P, MODES], BF16)
+        nc.vector.memset(vectors[:], 0.0)
+        nc.scalar.dma_start(out=vectors[0:1, :], in_=omega_sq.rearrange("(o r) -> o r", o=1))
+        nc.scalar.dma_start(out=vectors[32:33, :], in_=alpha_lambda.rearrange("(o r) -> o r", o=1))
+        nc.scalar.dma_start(out=vectors[64:65, :], in_=dmlp_b2.rearrange("(o r) -> o r", o=1))
+        pick_stiffness = keep.tile([P, P], BF16)
+        nc.vector.memset(pick_stiffness[:], 0.0)
+        nc.vector.memset(pick_stiffness[0:32, :], 1.0)
+        nc.vector.memset(pick_stiffness[32:64, :], -1.0)
+        pick_b2 = keep.tile([P, P], BF16)
+        nc.vector.memset(pick_b2[:], 0.0)
+        nc.vector.memset(pick_b2[64:96, :], 1.0)
+        pull = keep.tile([P, MODES], F32)
+        b2_all = keep.tile([P, MODES], F32)
+        for half in range(MODES // BANK):
+            cols = slice(half * BANK, (half + 1) * BANK)
+            stiff_bank = psum.tile([P, BANK], F32, tag="bank", bufs=3)
+            nc.tensor.matmul(out=stiff_bank[:], lhsT=pick_stiffness[:], rhs=vectors[:, cols], start=True, stop=True)
+            nc.vector.tensor_scalar(
+                out=pull[:, cols], in0=stiff_bank[:], scalar1=minus_dt[:, 0:1], scalar2=None, op0=ALU.mult
+            )
+            b2_bank = psum.tile([P, BANK], F32, tag="bank", bufs=3)
+            nc.tensor.matmul(out=b2_bank[:], lhsT=pick_b2[:], rhs=vectors[:, cols], start=True, stop=True)
+            nc.vector.tensor_copy(out=b2_all[:, cols], in_=b2_bank[:])
+
+        feat_codes = keep.tile([P, FEAT_PASSES, BATCH], U32, align_bytes=64)
+        feat_scales = keep.tile([P, FEAT_PASSES, BATCH], U8, align_bytes=64)
+        w1_codes = keep.tile([P, W1_UNITS, FEAT_PASSES, PAIR], U32, align_bytes=64)
+        w1_scales = keep.tile([P, W1_UNITS, FEAT_PASSES, PAIR], U8, align_bytes=64)
+        b_codes = keep.tile([P, MODES], U32, align_bytes=64)
+        b_scales = keep.tile([P, MODES], U8, align_bytes=64)
+        w2_codes = keep.tile([P, HID_PASSES, MODES], U32, align_bytes=64)
+        w2_scales = keep.tile([P, HID_PASSES, MODES], U8, align_bytes=64)
+        h_codes = keep.tile([P, HID_PASSES, BATCH], U32, align_bytes=64)
+        h_scales = keep.tile([P, HID_PASSES, BATCH], U8, align_bytes=64)
+
+        def transpose_and_group(rows_a, rows_b):
+            bank = psum.tile([P, 2, PAIR], F32, tag="bank", bufs=3)
+            for s, rows in enumerate((rows_a, rows_b)):
+                for h in range(2):
+                    nc.tensor.transpose(bank[:, h, s * P : (s + 1) * P], rows[:, h * P : (h + 1) * P], ident[:])
+            grouped = stage.tile([P, PAIR, PACK], BF16, align_bytes=64)
+            nc.scalar.copy(out=grouped[:].bitcast(F32), in_=bank[:].rearrange("p h c -> p c h"))
+            return grouped
+
+        def quantise(grouped, codes, scales):
+            nc.vector.quantize_mx(
+                out=codes.bitcast(FP8X4), scales=scales, in_=grouped[:].rearrange("p c t -> p (c t)")
+            )
+
+        y_words = y_sb[:].bitcast(F32)
+        z_words = z_sb[:].bitcast(F32)
+        u_words = u_sb[:].bitcast(F32)
+        feat_sources = ((y_words, 0), (y_words, 1), (z_words, 0), (z_words, 1), (u_words, 0))
+
+        def prepare_feats(c):
+            cols = slice(c * PAIR, (c + 1) * PAIR)
+            grouped = []
+            for words, part in feat_sources:
+                k_words = slice(part * WORDS, (part + 1) * WORDS)
+                grouped.append(transpose_and_group(words[:, 2 * c, k_words], words[:, 2 * c + 1, k_words]))
+            for g in range(FEAT_PASSES):
+                quantise(grouped[g], feat_codes[:, g, cols], feat_scales[:, g, cols])
+
+        def prepare_w1(n):
+            words = w1_raw[n][:].bitcast(F32)
+            grouped = []
+            for g in range(FEAT_PASSES):
+                k_words = slice(g * WORDS, (g + 1) * WORDS)
+                grouped.append(transpose_and_group(words[:, 0, k_words], words[:, 1, k_words]))
+            for g in range(FEAT_PASSES):
+                quantise(grouped[g], w1_codes[:, n, g, :], w1_scales[:, n, g, :])
+
+        def prepare_b():
+            words = b_raw[:].bitcast(F32)
+            grouped = []
+            for q in range(MODES // PAIR):
+                grouped.append(transpose_and_group(words[:, 2 * q, :], words[:, 2 * q + 1, :]))
+            for q in range(MODES // PAIR):
+                cols = slice(q * PAIR, (q + 1) * PAIR)
+                quantise(grouped[q], b_codes[:, cols], b_scales[:, cols])
+
+        def prepare_w2(half):
+            words = w2_raw[half][:].bitcast(F32)
+            grouped = []
+            for g in range(HID_PASSES):
+                k_words = slice(g * WORDS, (g + 1) * WORDS)
+                for q in range(2):
+                    grouped.append(transpose_and_group(words[:, 2 * q, k_words], words[:, 2 * q + 1, k_words]))
+            for g in range(HID_PASSES):
+                for q in range(2):
+                    cols = slice((2 * half + q) * PAIR, (2 * half + q + 1) * PAIR)
+                    quantise(grouped[2 * g + q], w2_codes[:, g, cols], w2_scales[:, g, cols])
+
+        def hidden_layer(c, n, h_planes):
+            cols = slice(c * PAIR, (c + 1) * PAIR)
+            for e in range(2):
+                units = slice(e * P, (e + 1) * P)
+                acc = psum.tile([P, PAIR], F32, tag="acc1", bufs=2)
+                for g in range(FEAT_PASSES):
+                    nc.tensor.matmul_mx(
+                        out=acc[:],
+                        lhsT=w1_codes[:, n, g, units].bitcast(FP8X4),
+                        lhsT_scale=w1_scales[:, n, g, units],
+                        rhs=feat_codes[:, g, cols].bitcast(FP8X4),
+                        rhs_scale=feat_scales[:, g, cols],
+                        start=(g == 0),
+                        stop=(g == FEAT_PASSES - 1),
+                    )
+                nc.scalar.activation(
+                    out=h_planes[:, 2 * (n % 2) + e, :], in_=acc[:], func=ACT.Tanh,
+                    bias=b1_col[:, 2 * n + e : 2 * n + e + 1], scale=1.0,
+                )
+
+        def quantise_hidden(c, g, h_planes):
+            cols = slice(c * PAIR, (c + 1) * PAIR)
+            h_grouped = hidden.tile([P, PAIR, PACK], BF16, align_bytes=64)
+            nc.vector.tensor_copy(
+                out=h_grouped[:].rearrange("p (c i) t -> p c t i", i=4),
+                in_=h_planes[:].rearrange("p t (c i) -> p c t i", i=4),
+            )
+            quantise(h_grouped, h_codes[:, g, cols], h_scales[:, g, cols])
+
+        def new_h_planes():
+            h_planes = hidden.tile([P, PACK, PAIR], BF16)
+            return h_planes
+
+        def drive_and_spring(c):
+            forced = []
+            for j in (2 * c, 2 * c + 1):
+                z_next = update.tile([P, MODES], F32, tag="z_next", bufs=4, name="z_next%d" % j)
+                nc.vector.tensor_tensor(out=z_next[:], in0=pull[:], in1=y_sb[:, j, :], op=ALU.mult)
+                for half in range(MODES // BANK):
+                    cols = slice(half * BANK, (half + 1) * BANK)
+                    acc = psum.tile([P, BANK], F32, tag="acc2", bufs=1)
+                    nc.tensor.matmul_mx(
+                        out=acc[:],
+                        lhsT=feat_codes[:, FEAT_PASSES - 1, j * P : (j + 1) * P].bitcast(FP8X4),
+                        lhsT_scale=feat_scales[:, FEAT_PASSES - 1, j * P : (j + 1) * P],
+                        rhs=b_codes[:, cols].bitcast(FP8X4),
+                        rhs_scale=b_scales[:, cols],
+                        start=True,
+                        stop=True,
+                    )
+                    nc.vector.scalar_tensor_tensor(
+                        out=z_next[:, cols], in0=acc[:], scalar=dt_col[:, 0:1], in1=z_next[:, cols],
+                        op0=ALU.mult, op1=ALU.add,
+                    )
+                forced.append(z_next)
+            return forced
+
+        def damp_and_step(c, forced):
+            pair = (2 * c, 2 * c + 1)
+            work = []
+            for j in pair:
+                t_half = update.tile([P, MODES], F32, tag="t_half", name="t_half%d" % j)
+                for half in range(MODES // BANK):
+                    cols = slice(half * BANK, (half + 1) * BANK)
+                    acc = psum.tile([P, BANK], F32, tag="acc3", bufs=2)
+                    for g in range(HID_PASSES):
+                        nc.tensor.matmul_mx(
+                            out=acc[:],
+                            lhsT=h_codes[:, g, j * P : (j + 1) * P].bitcast(FP8X4),
+                            lhsT_scale=h_scales[:, g, j * P : (j + 1) * P],
+                            rhs=w2_codes[:, g, cols].bitcast(FP8X4),
+                            rhs_scale=w2_scales[:, g, cols],
+                            start=(g == 0),
+                            stop=(g == HID_PASSES - 1),
+                        )
+                    nc.vector.tensor_tensor(out=t_half[:, cols], in0=acc[:], in1=b2_all[:, cols], op=ALU.add)
+                work.append(t_half)
+            for t_half in work:
+                nc.scalar.activation(out=t_half[:], in_=t_half[:], func=ACT.Tanh, scale=0.5)
+            for t_half, j in zip(work, pair):
+                gamma = update.tile([P, MODES], F32, tag="gamma", name="gamma%d" % j)
+                nc.scalar.activation(out=gamma[:], in_=t_half[:], func=ACT.Identity, bias=1.0, scale=1.0)
+                nc.sync.dma_start(out=gamma_rows[:, j, :], in_=gamma[:])
+            for t_half in work:
+                nc.scalar.activation(
+                    out=t_half[:], in_=t_half[:], func=ACT.Identity, bias=one_minus_dt[:, 0:1], scale=minus_dt[:, 0:1]
+                )
+            for t_half, j in zip(work, pair):
+                nc.vector.tensor_tensor(out=t_half[:], in0=t_half[:], in1=z_sb[:, j, :], op=ALU.mult)
+            for t_half, z_next, j in zip(work, forced, pair):
+                nc.vector.tensor_tensor(out=z_next[:], in0=t_half[:], in1=z_next[:], op=ALU.add)
+                nc.sync.dma_start(out=z_next_rows[:, j, :], in_=z_next[:])
+            for z_next, j in zip(forced, pair):
+                y_next = update.tile([P, MODES], F32, tag="y_next", name="y_next%d" % j)
+                nc.vector.scalar_tensor_tensor(
+                    out=y_next[:], in0=z_next[:], scalar=dt_col[:, 0:1], in1=y_sb[:, j, :], op0=ALU.mult, op1=ALU.add
+                )
+                nc.sync.dma_start(out=y_next_rows[:, j, :], in_=y_next[:])
+
+        prepare_feats(0)
+        for g in range(HID_PASSES):
+            h_planes = new_h_planes()
+            for n in (2 * g, 2 * g + 1):
+                prepare_w1(n)
+                hidden_layer(0, n, h_planes)
+            quantise_hidden(0, g, h_planes)
+        prepare_feats(1)
+        prepare_b()
+        forced = drive_and_spring(0)
+        prepare_w2(0)
+        prepare_w2(1)
+        damp_and_step(0, forced)
+        for c in range(1, CHUNKS):
+            for g in range(HID_PASSES):
+                h_planes = new_h_planes()
+                for n in (2 * g, 2 * g + 1):
+                    hidden_layer(c, n, h_planes)
+                quantise_hidden(c, g, h_planes)
+            if c + 1 < CHUNKS:
+                prepare_feats(c + 1)
+            forced = drive_and_spring(c)
+            damp_and_step(c, forced)

@@ -237,7 +237,7 @@ def tile_instrumentedlocmblock_pa_kernel(
             forced = []
             for j in (2 * c, 2 * c + 1):
                 z_next = update.tile([P, MODES], F32, tag="z_next", bufs=4, name="z_next%d" % j)
-                nc.vector.tensor_tensor(out=z_next[:], in0=pull[:], in1=y_sb[:, j, :], op=ALU.mult)
+                nc.gpsimd.tensor_tensor(out=z_next[:], in0=pull[:], in1=y_sb[:, j, :], op=ALU.mult)
                 for half in range(MODES // BANK):
                     cols = slice(half * BANK, (half + 1) * BANK)
                     acc = psum.tile([P, BANK], F32, tag="acc2", bufs=1)

@@ -24,10 +24,12 @@ DRIVE = 512
 HIDDEN = 1024
 FEATS = 2 * MODES + DRIVE
 ROW_TILES = BATCH // P
+MODE_TILES = MODES // P
 CHUNKS = BATCH // PAIR
 FEAT_PASSES = FEATS // K_PASS
 HID_PASSES = HIDDEN // K_PASS
 W1_UNITS = HIDDEN // PAIR
+HALVES = MODES // BANK
 
 FLOPS = 2 * BATCH * (HIDDEN * FEATS + MODES * DRIVE + MODES * HIDDEN)
 
@@ -39,11 +41,12 @@ def tile_instrumentedlocmblock_pa_kernel(
     nc = tc.nc
     with ExitStack() as ctx:
         keep = ctx.enter_context(tc.tile_pool(name="keep", bufs=1))
-        weights_in = ctx.enter_context(tc.tile_pool(name="weights_in", bufs=4))
-        stage = ctx.enter_context(tc.tile_pool(name="stage", bufs=6))
+        weights_in = ctx.enter_context(tc.tile_pool(name="weights_in", bufs=3))
+        stage = ctx.enter_context(tc.tile_pool(name="stage", bufs=10))
         hidden = ctx.enter_context(tc.tile_pool(name="hidden", bufs=2))
         update = ctx.enter_context(tc.tile_pool(name="update", bufs=2))
-        psum = ctx.enter_context(tc.psum_pool(name="psum", bufs=1))
+        psum = ctx.enter_context(tc.psum_pool(name="psum", bufs=8))
+        ctx.enter_context(tc.manual_schedule())
 
         y_rows = y_tilde.rearrange("(p j) r -> p j r", j=ROW_TILES)
         z_rows = z_tilde.rearrange("(p j) r -> p j r", j=ROW_TILES)
@@ -65,71 +68,72 @@ def tile_instrumentedlocmblock_pa_kernel(
         b_rows = B_tilde.rearrange("(i p) k -> p i k", p=P)
         w2_rows = dmlp_w2.rearrange("(i p) k -> p i k", p=P)
 
+        dt_bf = keep.tile([P, 1], BF16)
+        nc.scalar.dma_start(out=dt_bf[:], in_=dt.partition_broadcast(P))
+        b1_rows = keep.tile([P, 2 * P], BF16)
+        nc.vector.memset(b1_rows[:], 0.0)
+        nc.scalar.dma_start(out=b1_rows[0:W1_UNITS, :], in_=dmlp_b1.rearrange("(n w) -> n w", n=W1_UNITS))
+        b2_rows = keep.tile([P, P], BF16)
+        nc.vector.memset(b2_rows[:], 0.0)
+        nc.scalar.dma_start(out=b2_rows[0:MODE_TILES, :], in_=dmlp_b2.rearrange("(i p) -> i p", p=P))
+        vectors = keep.tile([P, MODES], BF16)
+        nc.vector.memset(vectors[:], 0.0)
+        nc.scalar.dma_start(out=vectors[0:1, :], in_=omega_sq.rearrange("(o r) -> o r", o=1))
+        nc.scalar.dma_start(out=vectors[32:33, :], in_=alpha_lambda.rearrange("(o r) -> o r", o=1))
+
         load_chunk(0)
         w1_raw = []
         for n in range(W1_UNITS):
             raw = weights_in.tile([P, 2, FEATS], BF16, tag="raw", name="w1_raw%d" % n)
             nc.sync.dma_start(out=raw[:], in_=w1_rows[n])
             w1_raw.append(raw)
-        load_chunk(1)
-        b_raw = weights_in.tile([P, ROW_TILES, DRIVE], BF16, tag="raw")
-        nc.sync.dma_start(out=b_raw[:], in_=b_rows)
         w2_raw = []
         for half in range(2):
             raw = weights_in.tile([P, 4, HIDDEN], BF16, tag="raw", name="w2_raw%d" % half)
             nc.sync.dma_start(out=raw[:], in_=w2_rows[:, 4 * half : 4 * half + 4, :])
             w2_raw.append(raw)
-        load_chunk(2)
-        load_chunk(3)
+        b_raw = weights_in.tile([P, MODE_TILES, DRIVE], BF16, tag="raw")
+        nc.sync.dma_start(out=b_raw[:], in_=b_rows)
+        for c in range(1, CHUNKS):
+            load_chunk(c)
 
         ident = keep.tile([P, P], F32)
         make_identity(nc, ident[:])
 
-        dt_bf = keep.tile([P, 1], BF16)
-        nc.scalar.dma_start(out=dt_bf[:], in_=dt.partition_broadcast(P))
+        pick_stiffness = keep.tile([P, P], BF16)
+        nc.vector.memset(pick_stiffness[:], 0.0)
+        nc.vector.memset(pick_stiffness[0:32, :], 1.0)
+        nc.vector.memset(pick_stiffness[32:64, :], -1.0)
+
         dt_col = keep.tile([P, 1], F32)
         minus_dt = keep.tile([P, 1], F32)
-        one_minus_dt = keep.tile([P, 1], F32)
         nc.vector.tensor_copy(out=dt_col[:], in_=dt_bf[:])
         nc.vector.tensor_scalar(out=minus_dt[:], in0=dt_col[:], scalar1=-1.0, scalar2=None, op0=ALU.mult)
-        nc.vector.tensor_scalar(
-            out=one_minus_dt[:], in0=dt_col[:], scalar1=-1.0, scalar2=1.0, op0=ALU.mult, op1=ALU.add
-        )
 
-        b1_rows = keep.tile([P, 2 * P], BF16)
-        nc.vector.memset(b1_rows[:], 0.0)
-        nc.scalar.dma_start(out=b1_rows[0:W1_UNITS, :], in_=dmlp_b1.rearrange("(n w) -> n w", n=W1_UNITS))
-        b1_bank = psum.tile([P, P], F32, tag="bank", bufs=3)
+        b1_bank = psum.tile([P, P], F32, tag="ring")
         nc.tensor.transpose(b1_bank[:], b1_rows[:].bitcast(F32), ident[:])
         b1_words = keep.tile([P, W1_UNITS], F32)
         nc.vector.tensor_copy(out=b1_words[:], in_=b1_bank[:, 0:W1_UNITS])
         b1_col = keep.tile([P, 2 * W1_UNITS], F32)
         nc.vector.tensor_copy(out=b1_col[:], in_=b1_words[:].bitcast(BF16))
 
-        vectors = keep.tile([P, MODES], BF16)
-        nc.vector.memset(vectors[:], 0.0)
-        nc.scalar.dma_start(out=vectors[0:1, :], in_=omega_sq.rearrange("(o r) -> o r", o=1))
-        nc.scalar.dma_start(out=vectors[32:33, :], in_=alpha_lambda.rearrange("(o r) -> o r", o=1))
-        nc.scalar.dma_start(out=vectors[64:65, :], in_=dmlp_b2.rearrange("(o r) -> o r", o=1))
-        pick_stiffness = keep.tile([P, P], BF16)
-        nc.vector.memset(pick_stiffness[:], 0.0)
-        nc.vector.memset(pick_stiffness[0:32, :], 1.0)
-        nc.vector.memset(pick_stiffness[32:64, :], -1.0)
-        pick_b2 = keep.tile([P, P], BF16)
-        nc.vector.memset(pick_b2[:], 0.0)
-        nc.vector.memset(pick_b2[64:96, :], 1.0)
+        b2_rows_f32 = keep.tile([P, P], F32)
+        nc.vector.tensor_copy(out=b2_rows_f32[:], in_=b2_rows[:])
+        b2_bank = psum.tile([P, P], F32, tag="ring")
+        nc.tensor.transpose(b2_bank[:], b2_rows_f32[:], ident[:])
+        half_b2_col = keep.tile([P, MODE_TILES], F32)
+        nc.vector.tensor_scalar(
+            out=half_b2_col[:], in0=b2_bank[:, 0:MODE_TILES], scalar1=0.5, scalar2=None, op0=ALU.mult
+        )
+
         pull = keep.tile([P, MODES], F32)
-        b2_all = keep.tile([P, MODES], F32)
-        for half in range(MODES // BANK):
+        for half in range(HALVES):
             cols = slice(half * BANK, (half + 1) * BANK)
-            stiff_bank = psum.tile([P, BANK], F32, tag="bank", bufs=3)
+            stiff_bank = psum.tile([P, BANK], F32, tag="ring")
             nc.tensor.matmul(out=stiff_bank[:], lhsT=pick_stiffness[:], rhs=vectors[:, cols], start=True, stop=True)
             nc.vector.tensor_scalar(
                 out=pull[:, cols], in0=stiff_bank[:], scalar1=minus_dt[:, 0:1], scalar2=None, op0=ALU.mult
             )
-            b2_bank = psum.tile([P, BANK], F32, tag="bank", bufs=3)
-            nc.tensor.matmul(out=b2_bank[:], lhsT=pick_b2[:], rhs=vectors[:, cols], start=True, stop=True)
-            nc.vector.tensor_copy(out=b2_all[:, cols], in_=b2_bank[:])
 
         feat_codes = keep.tile([P, FEAT_PASSES, BATCH], U32, align_bytes=64)
         feat_scales = keep.tile([P, FEAT_PASSES, BATCH], U8, align_bytes=64)
@@ -142,13 +146,16 @@ def tile_instrumentedlocmblock_pa_kernel(
         h_codes = keep.tile([P, HID_PASSES, BATCH], U32, align_bytes=64)
         h_scales = keep.tile([P, HID_PASSES, BATCH], U8, align_bytes=64)
 
-        def transpose_and_group(rows_a, rows_b):
-            bank = psum.tile([P, 2, PAIR], F32, tag="bank", bufs=3)
+        def transpose_and_group(rows_a, rows_b, on_vector=False):
+            bank = psum.tile([P, 2, PAIR], F32, tag="ring")
             for s, rows in enumerate((rows_a, rows_b)):
                 for h in range(2):
                     nc.tensor.transpose(bank[:, h, s * P : (s + 1) * P], rows[:, h * P : (h + 1) * P], ident[:])
             grouped = stage.tile([P, PAIR, PACK], BF16, align_bytes=64)
-            nc.scalar.copy(out=grouped[:].bitcast(F32), in_=bank[:].rearrange("p h c -> p c h"))
+            if on_vector:
+                nc.vector.tensor_copy(out=grouped[:].bitcast(F32), in_=bank[:].rearrange("p h c -> p c h"))
+            else:
+                nc.scalar.copy(out=grouped[:].bitcast(F32), in_=bank[:].rearrange("p h c -> p c h"))
             return grouped
 
         def quantise(grouped, codes, scales):
@@ -161,40 +168,54 @@ def tile_instrumentedlocmblock_pa_kernel(
         u_words = u_sb[:].bitcast(F32)
         feat_sources = ((y_words, 0), (y_words, 1), (z_words, 0), (z_words, 1), (u_words, 0))
 
-        def prepare_feats(c):
-            cols = slice(c * PAIR, (c + 1) * PAIR)
+        def group_feats(c):
             grouped = []
             for words, part in feat_sources:
                 k_words = slice(part * WORDS, (part + 1) * WORDS)
                 grouped.append(transpose_and_group(words[:, 2 * c, k_words], words[:, 2 * c + 1, k_words]))
+            return grouped
+
+        def quantise_feats(c, grouped):
+            cols = slice(c * PAIR, (c + 1) * PAIR)
             for g in range(FEAT_PASSES):
                 quantise(grouped[g], feat_codes[:, g, cols], feat_scales[:, g, cols])
 
-        def prepare_w1(n):
+        def group_w1(n):
             words = w1_raw[n][:].bitcast(F32)
             grouped = []
             for g in range(FEAT_PASSES):
                 k_words = slice(g * WORDS, (g + 1) * WORDS)
-                grouped.append(transpose_and_group(words[:, 0, k_words], words[:, 1, k_words]))
+                grouped.append(
+                    transpose_and_group(words[:, 0, k_words], words[:, 1, k_words], on_vector=(g == FEAT_PASSES - 1))
+                )
+            return grouped
+
+        def quantise_w1(n, grouped):
             for g in range(FEAT_PASSES):
                 quantise(grouped[g], w1_codes[:, n, g, :], w1_scales[:, n, g, :])
 
-        def prepare_b():
+        def group_b():
             words = b_raw[:].bitcast(F32)
             grouped = []
             for q in range(MODES // PAIR):
                 grouped.append(transpose_and_group(words[:, 2 * q, :], words[:, 2 * q + 1, :]))
+            return grouped
+
+        def quantise_b(grouped):
             for q in range(MODES // PAIR):
                 cols = slice(q * PAIR, (q + 1) * PAIR)
                 quantise(grouped[q], b_codes[:, cols], b_scales[:, cols])
 
-        def prepare_w2(half):
+        def group_w2(half):
             words = w2_raw[half][:].bitcast(F32)
             grouped = []
             for g in range(HID_PASSES):
                 k_words = slice(g * WORDS, (g + 1) * WORDS)
                 for q in range(2):
                     grouped.append(transpose_and_group(words[:, 2 * q, k_words], words[:, 2 * q + 1, k_words]))
+            return grouped
+
+        def quantise_w2(half, grouped):
             for g in range(HID_PASSES):
                 for q in range(2):
                     cols = slice((2 * half + q) * PAIR, (2 * half + q + 1) * PAIR)
@@ -204,7 +225,7 @@ def tile_instrumentedlocmblock_pa_kernel(
             cols = slice(c * PAIR, (c + 1) * PAIR)
             for e in range(2):
                 units = slice(e * P, (e + 1) * P)
-                acc = psum.tile([P, PAIR], F32, tag="acc1", bufs=2)
+                acc = psum.tile([P, PAIR], F32, tag="ring")
                 for g in range(FEAT_PASSES):
                     nc.tensor.matmul_mx(
                         out=acc[:],
@@ -220,105 +241,166 @@ def tile_instrumentedlocmblock_pa_kernel(
                     bias=b1_col[:, 2 * n + e : 2 * n + e + 1], scale=1.0,
                 )
 
-        def quantise_hidden(c, g, h_planes):
-            cols = slice(c * PAIR, (c + 1) * PAIR)
+        def new_h_planes():
+            h_planes = hidden.tile([P, PACK, PAIR], BF16)
+            return h_planes
+
+        def regroup_hidden(h_planes):
             h_grouped = hidden.tile([P, PAIR, PACK], BF16, align_bytes=64)
             nc.vector.tensor_copy(
                 out=h_grouped[:].rearrange("p (c i) t -> p c t i", i=4),
                 in_=h_planes[:].rearrange("p t (c i) -> p c t i", i=4),
             )
+            return h_grouped
+
+        def quantise_hidden(c, g, h_grouped):
+            cols = slice(c * PAIR, (c + 1) * PAIR)
             quantise(h_grouped, h_codes[:, g, cols], h_scales[:, g, cols])
 
-        def new_h_planes():
-            h_planes = hidden.tile([P, PACK, PAIR], BF16)
-            return h_planes
+        def spring(j):
+            z_next = update.tile([P, MODES], F32, tag="z_next", bufs=4, name="z_next%d" % j)
+            nc.vector.tensor_tensor(out=z_next[:], in0=pull[:], in1=y_sb[:, j, :], op=ALU.mult)
+            return z_next
 
-        def drive_and_spring(c):
-            forced = []
-            for j in (2 * c, 2 * c + 1):
-                z_next = update.tile([P, MODES], F32, tag="z_next", bufs=4, name="z_next%d" % j)
-                nc.gpsimd.tensor_tensor(out=z_next[:], in0=pull[:], in1=y_sb[:, j, :], op=ALU.mult)
-                for half in range(MODES // BANK):
-                    cols = slice(half * BANK, (half + 1) * BANK)
-                    acc = psum.tile([P, BANK], F32, tag="acc2", bufs=1)
+        def drive(j, z_next):
+            rows = slice(j * P, (j + 1) * P)
+            for half in range(HALVES):
+                cols = slice(half * BANK, (half + 1) * BANK)
+                acc = psum.tile([P, BANK], F32, tag="ring")
+                nc.tensor.matmul_mx(
+                    out=acc[:],
+                    lhsT=feat_codes[:, FEAT_PASSES - 1, rows].bitcast(FP8X4),
+                    lhsT_scale=feat_scales[:, FEAT_PASSES - 1, rows],
+                    rhs=b_codes[:, cols].bitcast(FP8X4),
+                    rhs_scale=b_scales[:, cols],
+                    start=True,
+                    stop=True,
+                )
+                nc.vector.scalar_tensor_tensor(
+                    out=z_next[:, cols], in0=acc[:], scalar=dt_col[:, 0:1], in1=z_next[:, cols],
+                    op0=ALU.mult, op1=ALU.add,
+                )
+
+        def damping_net(c):
+            cols = slice(c * PAIR, (c + 1) * PAIR)
+            t_cols = update.tile([P, MODE_TILES, PAIR], F32, tag="t_cols", bufs=1, name="t_cols%d" % c)
+            for i in range(MODE_TILES):
+                modes = slice(i * P, (i + 1) * P)
+                acc = psum.tile([P, PAIR], F32, tag="ring")
+                for g in range(HID_PASSES):
                     nc.tensor.matmul_mx(
                         out=acc[:],
-                        lhsT=feat_codes[:, FEAT_PASSES - 1, j * P : (j + 1) * P].bitcast(FP8X4),
-                        lhsT_scale=feat_scales[:, FEAT_PASSES - 1, j * P : (j + 1) * P],
-                        rhs=b_codes[:, cols].bitcast(FP8X4),
-                        rhs_scale=b_scales[:, cols],
-                        start=True,
-                        stop=True,
+                        lhsT=w2_codes[:, g, modes].bitcast(FP8X4),
+                        lhsT_scale=w2_scales[:, g, modes],
+                        rhs=h_codes[:, g, cols].bitcast(FP8X4),
+                        rhs_scale=h_scales[:, g, cols],
+                        start=(g == 0),
+                        stop=(g == HID_PASSES - 1),
                     )
-                    nc.vector.scalar_tensor_tensor(
-                        out=z_next[:, cols], in0=acc[:], scalar=dt_col[:, 0:1], in1=z_next[:, cols],
-                        op0=ALU.mult, op1=ALU.add,
-                    )
-                forced.append(z_next)
-            return forced
-
-        def damp_and_step(c, forced):
-            pair = (2 * c, 2 * c + 1)
-            work = []
-            for j in pair:
-                t_half = update.tile([P, MODES], F32, tag="t_half", name="t_half%d" % j)
-                for half in range(MODES // BANK):
-                    cols = slice(half * BANK, (half + 1) * BANK)
-                    acc = psum.tile([P, BANK], F32, tag="acc3", bufs=2)
-                    for g in range(HID_PASSES):
-                        nc.tensor.matmul_mx(
-                            out=acc[:],
-                            lhsT=h_codes[:, g, j * P : (j + 1) * P].bitcast(FP8X4),
-                            lhsT_scale=h_scales[:, g, j * P : (j + 1) * P],
-                            rhs=w2_codes[:, g, cols].bitcast(FP8X4),
-                            rhs_scale=w2_scales[:, g, cols],
-                            start=(g == 0),
-                            stop=(g == HID_PASSES - 1),
-                        )
-                    nc.vector.tensor_tensor(out=t_half[:, cols], in0=acc[:], in1=b2_all[:, cols], op=ALU.add)
-                work.append(t_half)
-            for t_half in work:
-                nc.scalar.activation(out=t_half[:], in_=t_half[:], func=ACT.Tanh, scale=0.5)
-            for t_half, j in zip(work, pair):
-                gamma = update.tile([P, MODES], F32, tag="gamma", name="gamma%d" % j)
-                nc.scalar.activation(out=gamma[:], in_=t_half[:], func=ACT.Identity, bias=1.0, scale=1.0)
-                nc.sync.dma_start(out=gamma_rows[:, j, :], in_=gamma[:])
-            for t_half in work:
                 nc.scalar.activation(
-                    out=t_half[:], in_=t_half[:], func=ACT.Identity, bias=one_minus_dt[:, 0:1], scale=minus_dt[:, 0:1]
+                    out=t_cols[:, i, :], in_=acc[:], func=ACT.Tanh, bias=half_b2_col[:, i : i + 1], scale=0.5
                 )
-            for t_half, j in zip(work, pair):
-                nc.vector.tensor_tensor(out=t_half[:], in0=t_half[:], in1=z_sb[:, j, :], op=ALU.mult)
-            for t_half, z_next, j in zip(work, forced, pair):
-                nc.vector.tensor_tensor(out=z_next[:], in0=t_half[:], in1=z_next[:], op=ALU.add)
-                nc.sync.dma_start(out=z_next_rows[:, j, :], in_=z_next[:])
-            for z_next, j in zip(forced, pair):
-                y_next = update.tile([P, MODES], F32, tag="y_next", name="y_next%d" % j)
-                nc.vector.scalar_tensor_tensor(
-                    out=y_next[:], in0=z_next[:], scalar=dt_col[:, 0:1], in1=y_sb[:, j, :], op0=ALU.mult, op1=ALU.add
-                )
-                nc.sync.dma_start(out=y_next_rows[:, j, :], in_=y_next[:])
+            return t_cols
 
-        prepare_feats(0)
-        for g in range(HID_PASSES):
-            h_planes = new_h_planes()
-            for n in (2 * g, 2 * g + 1):
-                prepare_w1(n)
-                hidden_layer(0, n, h_planes)
-            quantise_hidden(0, g, h_planes)
-        prepare_feats(1)
-        prepare_b()
-        forced = drive_and_spring(0)
-        prepare_w2(0)
-        prepare_w2(1)
-        damp_and_step(0, forced)
+        def gamma_of(j, t_cols):
+            rows = slice((j % 2) * P, (j % 2 + 1) * P)
+            gamma = update.tile([P, MODES], F32, tag="gamma", name="gamma%d" % j)
+            for half in range(HALVES):
+                bank = psum.tile([P, BANK // P, P], F32, tag="ring")
+                for q in range(BANK // P):
+                    nc.tensor.transpose(bank[:, q, :], t_cols[:, half * (BANK // P) + q, rows], ident[:])
+                nc.scalar.activation(
+                    out=gamma[:, half * BANK : (half + 1) * BANK], in_=bank[:].rearrange("p q r -> p (q r)"),
+                    func=ACT.Identity, bias=1.0, scale=1.0,
+                )
+            nc.sync.dma_start(out=gamma_rows[:, j, :], in_=gamma[:])
+            kept = update.tile([P, MODES], F32, tag="kept", name="kept%d" % j)
+            nc.scalar.activation(out=kept[:], in_=gamma[:], func=ACT.Identity, bias=1.0, scale=minus_dt[:, 0:1])
+            return kept
+
+        def damp(j, kept):
+            nc.vector.tensor_tensor(out=kept[:], in0=kept[:], in1=z_sb[:, j, :], op=ALU.mult)
+
+        def new_velocity(j, kept, z_next):
+            nc.vector.tensor_tensor(out=z_next[:], in0=kept[:], in1=z_next[:], op=ALU.add)
+            nc.sync.dma_start(out=z_next_rows[:, j, :], in_=z_next[:])
+
+        def new_position(j, z_next):
+            y_next = update.tile([P, MODES], F32, tag="y_next", name="y_next%d" % j)
+            nc.vector.scalar_tensor_tensor(
+                out=y_next[:], in0=z_next[:], scalar=dt_col[:, 0:1], in1=y_sb[:, j, :], op0=ALU.mult, op1=ALU.add
+            )
+            nc.sync.dma_start(out=y_next_rows[:, j, :], in_=y_next[:])
+
+        forces = {}
+        quantise_feats(0, group_feats(0))
+        forces[0] = spring(0)
+        forces[1] = spring(1)
+        grouped_w1 = group_w1(0)
+        planes = {}
+        for n in range(W1_UNITS):
+            quantise_w1(n, grouped_w1)
+            if n + 1 < W1_UNITS:
+                grouped_w1 = group_w1(n + 1)
+            else:
+                grouped_w2 = group_w2(0)
+            if n == 2:
+                quantise_hidden(0, 0, regroup_hidden(planes[0]))
+            if n % 2 == 0:
+                planes[n // 2] = new_h_planes()
+            hidden_layer(0, n, planes[n // 2])
+        quantise_w2(0, grouped_w2)
+        grouped_w2 = group_w2(1)
+        quantise_hidden(0, 1, regroup_hidden(planes[1]))
+        quantise_w2(1, grouped_w2)
+        grouped_b = group_b()
+        t_cols = damping_net(0)
+        quantise_b(grouped_b)
+        next_feats = group_feats(1)
+        drive(0, forces[0])
+        drive(1, forces[1])
+        quantise_feats(1, next_feats)
+
         for c in range(1, CHUNKS):
-            for g in range(HID_PASSES):
-                h_planes = new_h_planes()
-                for n in (2 * g, 2 * g + 1):
-                    hidden_layer(c, n, h_planes)
-                quantise_hidden(c, g, h_planes)
+            old_a, old_b = 2 * c - 2, 2 * c - 1
+            new_a, new_b = 2 * c, 2 * c + 1
+
+            kept_a = gamma_of(old_a, t_cols)
+            forces[new_a] = spring(new_a)
+            forces[new_b] = spring(new_b)
+            drive(new_a, forces[new_a])
+            drive(new_b, forces[new_b])
+            planes_a = new_h_planes()
+            hidden_layer(c, 0, planes_a)
+            hidden_layer(c, 1, planes_a)
+            damp(old_a, kept_a)
+            grouped_a = regroup_hidden(planes_a)
+            new_velocity(old_a, kept_a, forces[old_a])
+            quantise_hidden(c, 0, grouped_a)
+            new_position(old_a, forces[old_a])
+
+            kept_b = gamma_of(old_b, t_cols)
+            planes_b = new_h_planes()
+            hidden_layer(c, 2, planes_b)
+            hidden_layer(c, 3, planes_b)
+            grouped_b = regroup_hidden(planes_b)
+            damp(old_b, kept_b)
+            quantise_hidden(c, 1, grouped_b)
+
             if c + 1 < CHUNKS:
-                prepare_feats(c + 1)
-            forced = drive_and_spring(c)
-            damp_and_step(c, forced)
+                next_feats = group_feats(c + 1)
+            t_cols = damping_net(c)
+            new_velocity(old_b, kept_b, forces[old_b])
+            if c + 1 < CHUNKS:
+                quantise_feats(c + 1, next_feats)
+            new_position(old_b, forces[old_b])
+
+        last_a, last_b = ROW_TILES - 2, ROW_TILES - 1
+        kept_a = gamma_of(last_a, t_cols)
+        damp(last_a, kept_a)
+        kept_b = gamma_of(last_b, t_cols)
+        new_velocity(last_a, kept_a, forces[last_a])
+        damp(last_b, kept_b)
+        new_position(last_a, forces[last_a])
+        new_velocity(last_b, kept_b, forces[last_b])
+        new_position(last_b, forces[last_b])

@@ -100,6 +100,10 @@ def tile_instrumentedlocmblock_pa_kernel(
         ident = keep.tile([P, P], F32)
         make_identity(nc, ident[:])
 
+        warm = keep.tile([P, 1], F32)
+        nc.vector.memset(warm[:], 0.0)
+        nc.scalar.activation(out=warm[:], in_=warm[:], func=ACT.Tanh)
+
         pick_stiffness = keep.tile([P, P], BF16)
         nc.vector.memset(pick_stiffness[:], 0.0)
         nc.vector.memset(pick_stiffness[0:32, :], 1.0)
@@ -356,10 +360,9 @@ def tile_instrumentedlocmblock_pa_kernel(
         grouped_b = group_b()
         t_cols = damping_net(0)
         quantise_b(grouped_b)
-        next_feats = group_feats(1)
         drive(0, forces[0])
         drive(1, forces[1])
-        quantise_feats(1, next_feats)
+        quantise_feats(1, group_feats(1))
 
         for c in range(1, CHUNKS):
             old_a, old_b = 2 * c - 2, 2 * c - 1
@@ -383,9 +386,8 @@ def tile_instrumentedlocmblock_pa_kernel(
             planes_b = new_h_planes()
             hidden_layer(c, 2, planes_b)
             hidden_layer(c, 3, planes_b)
-            grouped_b = regroup_hidden(planes_b)
+            quantise_hidden(c, 1, regroup_hidden(planes_b))
             damp(old_b, kept_b)
-            quantise_hidden(c, 1, grouped_b)
 
             if c + 1 < CHUNKS:
                 next_feats = group_feats(c + 1)

@@ -16,6 +16,7 @@ PACK = 4
 K_PASS = P * PACK
 WORDS = K_PASS // 2
 BANK = 512
+PSUM_BANKS = 8
 PAIR = 2 * P
 
 BATCH = 1024
@@ -29,7 +30,14 @@ CHUNKS = BATCH // PAIR
 FEAT_PASSES = FEATS // K_PASS
 HID_PASSES = HIDDEN // K_PASS
 W1_UNITS = HIDDEN // PAIR
+W2_PARTS = 2
+PART_TILES = MODE_TILES // W2_PARTS
 HALVES = MODES // BANK
+TILES_IN_BANK = BANK // P
+
+RAW_SLOTS = 3
+STAGE_SLOTS = 2 * FEAT_PASSES
+FORCE_SLOTS = 4
 
 FLOPS = 2 * BATCH * (HIDDEN * FEATS + MODES * DRIVE + MODES * HIDDEN)
 
@@ -40,12 +48,12 @@ def tile_instrumentedlocmblock_pa_kernel(
 ):
     nc = tc.nc
     with ExitStack() as ctx:
-        keep = ctx.enter_context(tc.tile_pool(name="keep", bufs=1))
-        weights_in = ctx.enter_context(tc.tile_pool(name="weights_in", bufs=3))
-        stage = ctx.enter_context(tc.tile_pool(name="stage", bufs=10))
+        resident = ctx.enter_context(tc.tile_pool(name="resident", bufs=1))
+        weights_in = ctx.enter_context(tc.tile_pool(name="weights_in", bufs=RAW_SLOTS))
+        stage = ctx.enter_context(tc.tile_pool(name="stage", bufs=STAGE_SLOTS))
         hidden = ctx.enter_context(tc.tile_pool(name="hidden", bufs=2))
         update = ctx.enter_context(tc.tile_pool(name="update", bufs=2))
-        psum = ctx.enter_context(tc.psum_pool(name="psum", bufs=8))
+        psum = ctx.enter_context(tc.psum_pool(name="psum", bufs=PSUM_BANKS))
         ctx.enter_context(tc.manual_schedule())
 
         y_rows = y_tilde.rearrange("(p j) r -> p j r", j=ROW_TILES)
@@ -54,9 +62,9 @@ def tile_instrumentedlocmblock_pa_kernel(
         z_next_rows = out_0.rearrange("(p j) r -> p j r", j=ROW_TILES)
         gamma_rows = out_1.rearrange("(p j) r -> p j r", j=ROW_TILES)
         y_next_rows = out_2.rearrange("(p j) r -> p j r", j=ROW_TILES)
-        y_sb = keep.tile([P, ROW_TILES, MODES], BF16)
-        z_sb = keep.tile([P, ROW_TILES, MODES], BF16)
-        u_sb = keep.tile([P, ROW_TILES, DRIVE], BF16)
+        y_sb = resident.tile([P, ROW_TILES, MODES], BF16)
+        z_sb = resident.tile([P, ROW_TILES, MODES], BF16)
+        u_sb = resident.tile([P, ROW_TILES, DRIVE], BF16)
 
         def load_chunk(c):
             tiles = slice(2 * c, 2 * c + 2)
@@ -68,18 +76,18 @@ def tile_instrumentedlocmblock_pa_kernel(
         b_rows = B_tilde.rearrange("(i p) k -> p i k", p=P)
         w2_rows = dmlp_w2.rearrange("(i p) k -> p i k", p=P)
 
-        dt_bf = keep.tile([P, 1], BF16)
+        dt_bf = resident.tile([P, 1], BF16)
         nc.scalar.dma_start(out=dt_bf[:], in_=dt.partition_broadcast(P))
-        b1_rows = keep.tile([P, 2 * P], BF16)
+        b1_rows = resident.tile([P, 2 * P], BF16)
         nc.vector.memset(b1_rows[:], 0.0)
         nc.scalar.dma_start(out=b1_rows[0:W1_UNITS, :], in_=dmlp_b1.rearrange("(n w) -> n w", n=W1_UNITS))
-        b2_rows = keep.tile([P, P], BF16)
+        b2_rows = resident.tile([P, P], BF16)
         nc.vector.memset(b2_rows[:], 0.0)
         nc.scalar.dma_start(out=b2_rows[0:MODE_TILES, :], in_=dmlp_b2.rearrange("(i p) -> i p", p=P))
-        vectors = keep.tile([P, MODES], BF16)
-        nc.vector.memset(vectors[:], 0.0)
-        nc.scalar.dma_start(out=vectors[0:1, :], in_=omega_sq.rearrange("(o r) -> o r", o=1))
-        nc.scalar.dma_start(out=vectors[32:33, :], in_=alpha_lambda.rearrange("(o r) -> o r", o=1))
+        stiffness_rows = resident.tile([P, MODES], BF16)
+        nc.vector.memset(stiffness_rows[:], 0.0)
+        nc.scalar.dma_start(out=stiffness_rows[0:1, :], in_=omega_sq.rearrange("(o r) -> o r", o=1))
+        nc.scalar.dma_start(out=stiffness_rows[32:33, :], in_=alpha_lambda.rearrange("(o r) -> o r", o=1))
 
         load_chunk(0)
         w1_raw = []
@@ -87,79 +95,79 @@ def tile_instrumentedlocmblock_pa_kernel(
             raw = weights_in.tile([P, 2, FEATS], BF16, tag="raw", name="w1_raw%d" % n)
             nc.sync.dma_start(out=raw[:], in_=w1_rows[n])
             w1_raw.append(raw)
-        w2_raw = []
-        for half in range(2):
-            raw = weights_in.tile([P, 4, HIDDEN], BF16, tag="raw", name="w2_raw%d" % half)
-            nc.sync.dma_start(out=raw[:], in_=w2_rows[:, 4 * half : 4 * half + 4, :])
-            w2_raw.append(raw)
         b_raw = weights_in.tile([P, MODE_TILES, DRIVE], BF16, tag="raw")
         nc.sync.dma_start(out=b_raw[:], in_=b_rows)
-        for c in range(1, CHUNKS):
+        load_chunk(1)
+        w2_raw = []
+        for part in range(W2_PARTS):
+            raw = weights_in.tile([P, PART_TILES, HIDDEN], BF16, tag="raw", name="w2_raw%d" % part)
+            nc.sync.dma_start(out=raw[:], in_=w2_rows[:, part * PART_TILES : (part + 1) * PART_TILES, :])
+            w2_raw.append(raw)
+        for c in range(2, CHUNKS):
             load_chunk(c)
 
-        ident = keep.tile([P, P], F32)
+        ident = resident.tile([P, P], F32)
         make_identity(nc, ident[:])
 
-        warm = keep.tile([P, 1], F32)
+        warm = resident.tile([P, 1], F32)
         nc.vector.memset(warm[:], 0.0)
         nc.scalar.activation(out=warm[:], in_=warm[:], func=ACT.Tanh)
 
-        pick_stiffness = keep.tile([P, P], BF16)
+        pick_stiffness = resident.tile([P, P], BF16)
         nc.vector.memset(pick_stiffness[:], 0.0)
         nc.vector.memset(pick_stiffness[0:32, :], 1.0)
         nc.vector.memset(pick_stiffness[32:64, :], -1.0)
 
-        dt_col = keep.tile([P, 1], F32)
-        minus_dt = keep.tile([P, 1], F32)
+        dt_col = resident.tile([P, 1], F32)
+        minus_dt = resident.tile([P, 1], F32)
         nc.vector.tensor_copy(out=dt_col[:], in_=dt_bf[:])
         nc.vector.tensor_scalar(out=minus_dt[:], in0=dt_col[:], scalar1=-1.0, scalar2=None, op0=ALU.mult)
 
-        b1_bank = psum.tile([P, P], F32, tag="ring")
+        b1_bank = psum.tile([P, P], F32, tag="bank")
         nc.tensor.transpose(b1_bank[:], b1_rows[:].bitcast(F32), ident[:])
-        b1_words = keep.tile([P, W1_UNITS], F32)
+        b1_words = resident.tile([P, W1_UNITS], F32)
         nc.vector.tensor_copy(out=b1_words[:], in_=b1_bank[:, 0:W1_UNITS])
-        b1_col = keep.tile([P, 2 * W1_UNITS], F32)
+        b1_col = resident.tile([P, 2 * W1_UNITS], F32)
         nc.vector.tensor_copy(out=b1_col[:], in_=b1_words[:].bitcast(BF16))
 
-        b2_rows_f32 = keep.tile([P, P], F32)
+        b2_rows_f32 = resident.tile([P, P], F32)
         nc.vector.tensor_copy(out=b2_rows_f32[:], in_=b2_rows[:])
-        b2_bank = psum.tile([P, P], F32, tag="ring")
+        b2_bank = psum.tile([P, P], F32, tag="bank")
         nc.tensor.transpose(b2_bank[:], b2_rows_f32[:], ident[:])
-        half_b2_col = keep.tile([P, MODE_TILES], F32)
+        half_b2_col = resident.tile([P, MODE_TILES], F32)
         nc.vector.tensor_scalar(
             out=half_b2_col[:], in0=b2_bank[:, 0:MODE_TILES], scalar1=0.5, scalar2=None, op0=ALU.mult
         )
 
-        pull = keep.tile([P, MODES], F32)
+        pull = resident.tile([P, MODES], F32)
         for half in range(HALVES):
             cols = slice(half * BANK, (half + 1) * BANK)
-            stiff_bank = psum.tile([P, BANK], F32, tag="ring")
-            nc.tensor.matmul(out=stiff_bank[:], lhsT=pick_stiffness[:], rhs=vectors[:, cols], start=True, stop=True)
+            stiffness_bank = psum.tile([P, BANK], F32, tag="bank")
+            nc.tensor.matmul(
+                out=stiffness_bank[:], lhsT=pick_stiffness[:], rhs=stiffness_rows[:, cols], start=True, stop=True
+            )
             nc.vector.tensor_scalar(
-                out=pull[:, cols], in0=stiff_bank[:], scalar1=minus_dt[:, 0:1], scalar2=None, op0=ALU.mult
+                out=pull[:, cols], in0=stiffness_bank[:], scalar1=minus_dt[:, 0:1], scalar2=None, op0=ALU.mult
             )
 
-        feat_codes = keep.tile([P, FEAT_PASSES, BATCH], U32, align_bytes=64)
-        feat_scales = keep.tile([P, FEAT_PASSES, BATCH], U8, align_bytes=64)
-        w1_codes = keep.tile([P, W1_UNITS, FEAT_PASSES, PAIR], U32, align_bytes=64)
-        w1_scales = keep.tile([P, W1_UNITS, FEAT_PASSES, PAIR], U8, align_bytes=64)
-        b_codes = keep.tile([P, MODES], U32, align_bytes=64)
-        b_scales = keep.tile([P, MODES], U8, align_bytes=64)
-        w2_codes = keep.tile([P, HID_PASSES, MODES], U32, align_bytes=64)
-        w2_scales = keep.tile([P, HID_PASSES, MODES], U8, align_bytes=64)
-        h_codes = keep.tile([P, HID_PASSES, BATCH], U32, align_bytes=64)
-        h_scales = keep.tile([P, HID_PASSES, BATCH], U8, align_bytes=64)
+        feat_codes = resident.tile([P, FEAT_PASSES, BATCH], U32, align_bytes=64)
+        feat_scales = resident.tile([P, FEAT_PASSES, BATCH], U8, align_bytes=64)
+        w1_codes = resident.tile([P, W1_UNITS, FEAT_PASSES, PAIR], U32, align_bytes=64)
+        w1_scales = resident.tile([P, W1_UNITS, FEAT_PASSES, PAIR], U8, align_bytes=64)
+        b_codes = resident.tile([P, MODES], U32, align_bytes=64)
+        b_scales = resident.tile([P, MODES], U8, align_bytes=64)
+        w2_codes = resident.tile([P, HID_PASSES, MODES], U32, align_bytes=64)
+        w2_scales = resident.tile([P, HID_PASSES, MODES], U8, align_bytes=64)
+        h_codes = resident.tile([P, HID_PASSES, BATCH], U32, align_bytes=64)
+        h_scales = resident.tile([P, HID_PASSES, BATCH], U8, align_bytes=64)
 
-        def transpose_and_group(rows_a, rows_b, on_vector=False):
-            bank = psum.tile([P, 2, PAIR], F32, tag="ring")
+        def transpose_and_group(rows_a, rows_b):
+            bank = psum.tile([P, 2, PAIR], F32, tag="bank")
             for s, rows in enumerate((rows_a, rows_b)):
-                for h in range(2):
-                    nc.tensor.transpose(bank[:, h, s * P : (s + 1) * P], rows[:, h * P : (h + 1) * P], ident[:])
+                for w in range(2):
+                    nc.tensor.transpose(bank[:, w, s * P : (s + 1) * P], rows[:, w * P : (w + 1) * P], ident[:])
             grouped = stage.tile([P, PAIR, PACK], BF16, align_bytes=64)
-            if on_vector:
-                nc.vector.tensor_copy(out=grouped[:].bitcast(F32), in_=bank[:].rearrange("p h c -> p c h"))
-            else:
-                nc.scalar.copy(out=grouped[:].bitcast(F32), in_=bank[:].rearrange("p h c -> p c h"))
+            nc.scalar.copy(out=grouped[:].bitcast(F32), in_=bank[:].rearrange("p w c -> p c w"))
             return grouped
 
         def quantise(grouped, codes, scales):
@@ -189,9 +197,7 @@ def tile_instrumentedlocmblock_pa_kernel(
             grouped = []
             for g in range(FEAT_PASSES):
                 k_words = slice(g * WORDS, (g + 1) * WORDS)
-                grouped.append(
-                    transpose_and_group(words[:, 0, k_words], words[:, 1, k_words], on_vector=(g == FEAT_PASSES - 1))
-                )
+                grouped.append(transpose_and_group(words[:, 0, k_words], words[:, 1, k_words]))
             return grouped
 
         def quantise_w1(n, grouped):
@@ -210,26 +216,31 @@ def tile_instrumentedlocmblock_pa_kernel(
                 cols = slice(q * PAIR, (q + 1) * PAIR)
                 quantise(grouped[q], b_codes[:, cols], b_scales[:, cols])
 
-        def group_w2(half):
-            words = w2_raw[half][:].bitcast(F32)
+        def group_w2(part):
+            words = w2_raw[part][:].bitcast(F32)
             grouped = []
             for g in range(HID_PASSES):
                 k_words = slice(g * WORDS, (g + 1) * WORDS)
-                for q in range(2):
+                for q in range(PART_TILES // 2):
                     grouped.append(transpose_and_group(words[:, 2 * q, k_words], words[:, 2 * q + 1, k_words]))
             return grouped
 
-        def quantise_w2(half, grouped):
+        def quantise_w2(part, grouped):
+            pairs = PART_TILES // 2
             for g in range(HID_PASSES):
-                for q in range(2):
-                    cols = slice((2 * half + q) * PAIR, (2 * half + q + 1) * PAIR)
-                    quantise(grouped[2 * g + q], w2_codes[:, g, cols], w2_scales[:, g, cols])
+                for q in range(pairs):
+                    cols = slice((pairs * part + q) * PAIR, (pairs * part + q + 1) * PAIR)
+                    quantise(grouped[pairs * g + q], w2_codes[:, g, cols], w2_scales[:, g, cols])
+
+        def new_h_planes():
+            h_planes = hidden.tile([P, PACK, PAIR], BF16)
+            return h_planes
 
         def hidden_layer(c, n, h_planes):
             cols = slice(c * PAIR, (c + 1) * PAIR)
             for e in range(2):
                 units = slice(e * P, (e + 1) * P)
-                acc = psum.tile([P, PAIR], F32, tag="ring")
+                acc = psum.tile([P, PAIR], F32, tag="bank")
                 for g in range(FEAT_PASSES):
                     nc.tensor.matmul_mx(
                         out=acc[:],
@@ -245,10 +256,6 @@ def tile_instrumentedlocmblock_pa_kernel(
                     bias=b1_col[:, 2 * n + e : 2 * n + e + 1], scale=1.0,
                 )
 
-        def new_h_planes():
-            h_planes = hidden.tile([P, PACK, PAIR], BF16)
-            return h_planes
-
         def regroup_hidden(h_planes):
             h_grouped = hidden.tile([P, PAIR, PACK], BF16, align_bytes=64)
             nc.vector.tensor_copy(
@@ -262,7 +269,7 @@ def tile_instrumentedlocmblock_pa_kernel(
             quantise(h_grouped, h_codes[:, g, cols], h_scales[:, g, cols])
 
         def spring(j):
-            z_next = update.tile([P, MODES], F32, tag="z_next", bufs=4, name="z_next%d" % j)
+            z_next = update.tile([P, MODES], F32, tag="z_next", bufs=FORCE_SLOTS, name="z_next%d" % j)
             nc.vector.tensor_tensor(out=z_next[:], in0=pull[:], in1=y_sb[:, j, :], op=ALU.mult)
             return z_next
 
@@ -270,7 +277,7 @@ def tile_instrumentedlocmblock_pa_kernel(
             rows = slice(j * P, (j + 1) * P)
             for half in range(HALVES):
                 cols = slice(half * BANK, (half + 1) * BANK)
-                acc = psum.tile([P, BANK], F32, tag="ring")
+                acc = psum.tile([P, BANK], F32, tag="bank")
                 nc.tensor.matmul_mx(
                     out=acc[:],
                     lhsT=feat_codes[:, FEAT_PASSES - 1, rows].bitcast(FP8X4),
@@ -290,7 +297,7 @@ def tile_instrumentedlocmblock_pa_kernel(
             t_cols = update.tile([P, MODE_TILES, PAIR], F32, tag="t_cols", bufs=1, name="t_cols%d" % c)
             for i in range(MODE_TILES):
                 modes = slice(i * P, (i + 1) * P)
-                acc = psum.tile([P, PAIR], F32, tag="ring")
+                acc = psum.tile([P, PAIR], F32, tag="bank")
                 for g in range(HID_PASSES):
                     nc.tensor.matmul_mx(
                         out=acc[:],
@@ -306,13 +313,13 @@ def tile_instrumentedlocmblock_pa_kernel(
                 )
             return t_cols
 
-        def gamma_of(j, t_cols):
+        def damping_of(j, t_cols):
             rows = slice((j % 2) * P, (j % 2 + 1) * P)
             gamma = update.tile([P, MODES], F32, tag="gamma", name="gamma%d" % j)
             for half in range(HALVES):
-                bank = psum.tile([P, BANK // P, P], F32, tag="ring")
-                for q in range(BANK // P):
-                    nc.tensor.transpose(bank[:, q, :], t_cols[:, half * (BANK // P) + q, rows], ident[:])
+                bank = psum.tile([P, TILES_IN_BANK, P], F32, tag="bank")
+                for q in range(TILES_IN_BANK):
+                    nc.tensor.transpose(bank[:, q, :], t_cols[:, half * TILES_IN_BANK + q, rows], ident[:])
                 nc.scalar.activation(
                     out=gamma[:, half * BANK : (half + 1) * BANK], in_=bank[:].rearrange("p q r -> p (q r)"),
                     func=ACT.Identity, bias=1.0, scale=1.0,
@@ -337,52 +344,50 @@ def tile_instrumentedlocmblock_pa_kernel(
             nc.sync.dma_start(out=y_next_rows[:, j, :], in_=y_next[:])
 
         forces = {}
+
+        def gather_forces(c):
+            for j in (2 * c, 2 * c + 1):
+                forces[j] = spring(j)
+                drive(j, forces[j])
+
         quantise_feats(0, group_feats(0))
         forces[0] = spring(0)
         forces[1] = spring(1)
+        planes = [new_h_planes(), new_h_planes()]
         grouped_w1 = group_w1(0)
-        planes = {}
         for n in range(W1_UNITS):
             quantise_w1(n, grouped_w1)
             if n + 1 < W1_UNITS:
                 grouped_w1 = group_w1(n + 1)
             else:
-                grouped_w2 = group_w2(0)
-            if n == 2:
-                quantise_hidden(0, 0, regroup_hidden(planes[0]))
-            if n % 2 == 0:
-                planes[n // 2] = new_h_planes()
+                grouped_drive = group_b()
             hidden_layer(0, n, planes[n // 2])
-        quantise_w2(0, grouped_w2)
-        grouped_w2 = group_w2(1)
+        quantise_hidden(0, 0, regroup_hidden(planes[0]))
+        quantise_b(grouped_drive)
+        grouped_feats = group_feats(1)
         quantise_hidden(0, 1, regroup_hidden(planes[1]))
-        quantise_w2(1, grouped_w2)
-        grouped_b = group_b()
-        t_cols = damping_net(0)
-        quantise_b(grouped_b)
         drive(0, forces[0])
         drive(1, forces[1])
-        quantise_feats(1, group_feats(1))
+        quantise_feats(1, grouped_feats)
+        quantise_w2(0, group_w2(0))
+        quantise_w2(1, group_w2(1))
+        t_cols = damping_net(0)
+        gather_forces(1)
 
         for c in range(1, CHUNKS):
             old_a, old_b = 2 * c - 2, 2 * c - 1
-            new_a, new_b = 2 * c, 2 * c + 1
 
-            kept_a = gamma_of(old_a, t_cols)
-            forces[new_a] = spring(new_a)
-            forces[new_b] = spring(new_b)
-            drive(new_a, forces[new_a])
-            drive(new_b, forces[new_b])
+            kept_a = damping_of(old_a, t_cols)
             planes_a = new_h_planes()
             hidden_layer(c, 0, planes_a)
             hidden_layer(c, 1, planes_a)
             damp(old_a, kept_a)
-            grouped_a = regroup_hidden(planes_a)
+            h_grouped_a = regroup_hidden(planes_a)
             new_velocity(old_a, kept_a, forces[old_a])
-            quantise_hidden(c, 0, grouped_a)
+            quantise_hidden(c, 0, h_grouped_a)
             new_position(old_a, forces[old_a])
 
-            kept_b = gamma_of(old_b, t_cols)
+            kept_b = damping_of(old_b, t_cols)
             planes_b = new_h_planes()
             hidden_layer(c, 2, planes_b)
             hidden_layer(c, 3, planes_b)
@@ -390,17 +395,19 @@ def tile_instrumentedlocmblock_pa_kernel(
             damp(old_b, kept_b)
 
             if c + 1 < CHUNKS:
-                next_feats = group_feats(c + 1)
+                grouped_feats = group_feats(c + 1)
             t_cols = damping_net(c)
             new_velocity(old_b, kept_b, forces[old_b])
             if c + 1 < CHUNKS:
-                quantise_feats(c + 1, next_feats)
+                quantise_feats(c + 1, grouped_feats)
             new_position(old_b, forces[old_b])
+            if c + 1 < CHUNKS:
+                gather_forces(c + 1)
 
         last_a, last_b = ROW_TILES - 2, ROW_TILES - 1
-        kept_a = gamma_of(last_a, t_cols)
+        kept_a = damping_of(last_a, t_cols)
         damp(last_a, kept_a)
-        kept_b = gamma_of(last_b, t_cols)
+        kept_b = damping_of(last_b, t_cols)
         new_velocity(last_a, kept_a, forces[last_a])
         damp(last_b, kept_b)
         new_position(last_a, forces[last_a])

@@ -120,8 +120,18 @@ def tile_instrumentedlocmblock_pa_kernel(
 
         dt_col = resident.tile([P, 1], F32)
         minus_dt = resident.tile([P, 1], F32)
+        dt_size = resident.tile([P, 1], F32)
+        tiny_step = resident.tile([P, 1], F32)
+        minus_step = resident.tile([P, 1], F32)
+        minus_rate = resident.tile([P, 1], F32)
         nc.vector.tensor_copy(out=dt_col[:], in_=dt_bf[:])
         nc.vector.tensor_scalar(out=minus_dt[:], in0=dt_col[:], scalar1=-1.0, scalar2=None, op0=ALU.mult)
+        nc.vector.tensor_tensor(out=dt_size[:], in0=dt_col[:], in1=minus_dt[:], op=ALU.max)
+        nc.vector.tensor_scalar(
+            out=tiny_step[:], in0=dt_size[:], scalar1=1e-20, scalar2=1e-20, op0=ALU.is_lt, op1=ALU.mult
+        )
+        nc.vector.tensor_tensor(out=minus_step[:], in0=minus_dt[:], in1=tiny_step[:], op=ALU.subtract)
+        nc.vector.reciprocal(out=minus_rate[:], in_=minus_step[:])
 
         b1_bank = psum.tile([P, P], F32, tag="bank")
         nc.tensor.transpose(b1_bank[:], b1_rows[:].bitcast(F32), ident[:])
@@ -325,15 +335,19 @@ def tile_instrumentedlocmblock_pa_kernel(
                     func=ACT.Identity, bias=1.0, scale=1.0,
                 )
             nc.sync.dma_start(out=gamma_rows[:, j, :], in_=gamma[:])
+            return gamma
+
+        def damp(j, gamma):
             kept = update.tile([P, MODES], F32, tag="kept", name="kept%d" % j)
-            nc.scalar.activation(out=kept[:], in_=gamma[:], func=ACT.Identity, bias=1.0, scale=minus_dt[:, 0:1])
+            nc.vector.scalar_tensor_tensor(
+                out=kept[:], in0=gamma[:], scalar=minus_rate[:, 0:1], in1=z_sb[:, j, :], op0=ALU.add, op1=ALU.mult
+            )
             return kept
 
-        def damp(j, kept):
-            nc.vector.tensor_tensor(out=kept[:], in0=kept[:], in1=z_sb[:, j, :], op=ALU.mult)
-
         def new_velocity(j, kept, z_next):
-            nc.vector.tensor_tensor(out=z_next[:], in0=kept[:], in1=z_next[:], op=ALU.add)
+            nc.vector.scalar_tensor_tensor(
+                out=z_next[:], in0=kept[:], scalar=minus_step[:, 0:1], in1=z_next[:], op0=ALU.mult, op1=ALU.add
+            )
             nc.sync.dma_start(out=z_next_rows[:, j, :], in_=z_next[:])
 
         def new_position(j, z_next):
@@ -377,22 +391,22 @@ def tile_instrumentedlocmblock_pa_kernel(
         for c in range(1, CHUNKS):
             old_a, old_b = 2 * c - 2, 2 * c - 1
 
-            kept_a = damping_of(old_a, t_cols)
+            gamma_a = damping_of(old_a, t_cols)
             planes_a = new_h_planes()
             hidden_layer(c, 0, planes_a)
             hidden_layer(c, 1, planes_a)
-            damp(old_a, kept_a)
+            kept_a = damp(old_a, gamma_a)
             h_grouped_a = regroup_hidden(planes_a)
             new_velocity(old_a, kept_a, forces[old_a])
             quantise_hidden(c, 0, h_grouped_a)
             new_position(old_a, forces[old_a])
 
-            kept_b = damping_of(old_b, t_cols)
+            gamma_b = damping_of(old_b, t_cols)
             planes_b = new_h_planes()
             hidden_layer(c, 2, planes_b)
             hidden_layer(c, 3, planes_b)
             quantise_hidden(c, 1, regroup_hidden(planes_b))
-            damp(old_b, kept_b)
+            kept_b = damp(old_b, gamma_b)
 
             if c + 1 < CHUNKS:
                 grouped_feats = group_feats(c + 1)
@@ -405,11 +419,11 @@ def tile_instrumentedlocmblock_pa_kernel(
                 gather_forces(c + 1)
 
         last_a, last_b = ROW_TILES - 2, ROW_TILES - 1
-        kept_a = damping_of(last_a, t_cols)
-        damp(last_a, kept_a)
-        kept_b = damping_of(last_b, t_cols)
+        gamma_a = damping_of(last_a, t_cols)
+        kept_a = damp(last_a, gamma_a)
+        gamma_b = damping_of(last_b, t_cols)
         new_velocity(last_a, kept_a, forces[last_a])
-        damp(last_b, kept_b)
+        kept_b = damp(last_b, gamma_b)
         new_position(last_a, forces[last_a])
         new_velocity(last_b, kept_b, forces[last_b])
         new_position(last_b, forces[last_b])

@@ -17,6 +17,7 @@ K_PASS = P * PACK
 WORDS = K_PASS // 2
 BANK = 512
 PSUM_BANKS = 8
+DRIVE_BANKS = 2
 PAIR = 2 * P
 
 BATCH = 1024
@@ -37,7 +38,7 @@ TILES_IN_BANK = BANK // P
 
 RAW_SLOTS = 3
 STAGE_SLOTS = 2 * FEAT_PASSES
-FORCE_SLOTS = 4
+FORCE_SLOTS = 7
 
 FLOPS = 2 * BATCH * (HIDDEN * FEATS + MODES * DRIVE + MODES * HIDDEN)
 
@@ -53,7 +54,8 @@ def tile_instrumentedlocmblock_pa_kernel(
         stage = ctx.enter_context(tc.tile_pool(name="stage", bufs=STAGE_SLOTS))
         hidden = ctx.enter_context(tc.tile_pool(name="hidden", bufs=2))
         update = ctx.enter_context(tc.tile_pool(name="update", bufs=2))
-        psum = ctx.enter_context(tc.psum_pool(name="psum", bufs=PSUM_BANKS))
+        psum = ctx.enter_context(tc.psum_pool(name="psum", bufs=PSUM_BANKS - DRIVE_BANKS))
+        drive_psum = ctx.enter_context(tc.psum_pool(name="drive_psum", bufs=DRIVE_BANKS))
         ctx.enter_context(tc.manual_schedule())
 
         y_rows = y_tilde.rearrange("(p j) r -> p j r", j=ROW_TILES)
@@ -89,7 +91,11 @@ def tile_instrumentedlocmblock_pa_kernel(
         nc.scalar.dma_start(out=stiffness_rows[0:1, :], in_=omega_sq.rearrange("(o r) -> o r", o=1))
         nc.scalar.dma_start(out=stiffness_rows[32:33, :], in_=alpha_lambda.rearrange("(o r) -> o r", o=1))
 
-        load_chunk(0)
+        for half in range(HALVES):
+            cols = slice(half * BANK, (half + 1) * BANK)
+            nc.sync.dma_start(out=y_sb[:, 0:2, cols], in_=y_rows[:, 0:2, cols])
+        nc.sync.dma_start(out=z_sb[:, 0:2, :], in_=z_rows[:, 0:2, :])
+        nc.sync.dma_start(out=u_sb[:, 0:2, :], in_=u_rows[:, 0:2, :])
         w1_raw = []
         for n in range(W1_UNITS):
             raw = weights_in.tile([P, 2, FEATS], BF16, tag="raw", name="w1_raw%d" % n)
@@ -168,16 +174,20 @@ def tile_instrumentedlocmblock_pa_kernel(
         b_scales = resident.tile([P, MODES], U8, align_bytes=64)
         w2_codes = resident.tile([P, HID_PASSES, MODES], U32, align_bytes=64)
         w2_scales = resident.tile([P, HID_PASSES, MODES], U8, align_bytes=64)
-        h_codes = resident.tile([P, HID_PASSES, BATCH], U32, align_bytes=64)
-        h_scales = resident.tile([P, HID_PASSES, BATCH], U8, align_bytes=64)
+        h_codes = {}
+        h_scales = {}
 
-        def transpose_and_group(rows_a, rows_b):
+        def transpose_and_group(rows_a, rows_b, on_vector=False):
             bank = psum.tile([P, 2, PAIR], F32, tag="bank")
             for s, rows in enumerate((rows_a, rows_b)):
                 for w in range(2):
                     nc.tensor.transpose(bank[:, w, s * P : (s + 1) * P], rows[:, w * P : (w + 1) * P], ident[:])
             grouped = stage.tile([P, PAIR, PACK], BF16, align_bytes=64)
-            nc.scalar.copy(out=grouped[:].bitcast(F32), in_=bank[:].rearrange("p w c -> p c w"))
+            words = bank[:].rearrange("p w c -> p c w")
+            if on_vector:
+                nc.vector.tensor_copy(out=grouped[:].bitcast(F32), in_=words)
+            else:
+                nc.scalar.copy(out=grouped[:].bitcast(F32), in_=words)
             return grouped
 
         def quantise(grouped, codes, scales):
@@ -207,7 +217,9 @@ def tile_instrumentedlocmblock_pa_kernel(
             grouped = []
             for g in range(FEAT_PASSES):
                 k_words = slice(g * WORDS, (g + 1) * WORDS)
-                grouped.append(transpose_and_group(words[:, 0, k_words], words[:, 1, k_words]))
+                grouped.append(
+                    transpose_and_group(words[:, 0, k_words], words[:, 1, k_words], on_vector=(g == FEAT_PASSES - 1))
+                )
             return grouped
 
         def quantise_w1(n, grouped):
@@ -232,7 +244,8 @@ def tile_instrumentedlocmblock_pa_kernel(
             for g in range(HID_PASSES):
                 k_words = slice(g * WORDS, (g + 1) * WORDS)
                 for q in range(PART_TILES // 2):
-                    grouped.append(transpose_and_group(words[:, 2 * q, k_words], words[:, 2 * q + 1, k_words]))
+                    last = g == HID_PASSES - 1 and q == PART_TILES // 2 - 1
+                    grouped.append(transpose_and_group(words[:, 2 * q, k_words], words[:, 2 * q + 1, k_words], on_vector=last))
             return grouped
 
         def quantise_w2(part, grouped):
@@ -266,17 +279,19 @@ def tile_instrumentedlocmblock_pa_kernel(
                     bias=b1_col[:, 2 * n + e : 2 * n + e + 1], scale=1.0,
                 )
 
-        def regroup_hidden(h_planes):
-            h_grouped = hidden.tile([P, PAIR, PACK], BF16, align_bytes=64)
-            nc.vector.tensor_copy(
+        def regroup_hidden(h_planes, copy):
+            h_grouped = hidden.tile([P, PAIR, PACK], BF16, tag="h_grouped", bufs=2, align_bytes=64)
+            copy(
                 out=h_grouped[:].rearrange("p (c i) t -> p c t i", i=4),
                 in_=h_planes[:].rearrange("p t (c i) -> p c t i", i=4),
             )
             return h_grouped
 
         def quantise_hidden(c, g, h_grouped):
-            cols = slice(c * PAIR, (c + 1) * PAIR)
-            quantise(h_grouped, h_codes[:, g, cols], h_scales[:, g, cols])
+            if g == 0:
+                h_codes[c] = hidden.tile([P, HID_PASSES, PAIR], U32, tag="h_codes", bufs=2, align_bytes=64, name="h_codes%d" % c)
+                h_scales[c] = hidden.tile([P, HID_PASSES, PAIR], U8, tag="h_scales", bufs=2, align_bytes=64, name="h_scales%d" % c)
+            quantise(h_grouped, h_codes[c][:, g, :], h_scales[c][:, g, :])
 
         def spring(j):
             z_next = update.tile([P, MODES], F32, tag="z_next", bufs=FORCE_SLOTS, name="z_next%d" % j)
@@ -287,7 +302,7 @@ def tile_instrumentedlocmblock_pa_kernel(
             rows = slice(j * P, (j + 1) * P)
             for half in range(HALVES):
                 cols = slice(half * BANK, (half + 1) * BANK)
-                acc = psum.tile([P, BANK], F32, tag="bank")
+                acc = drive_psum.tile([P, BANK], F32, tag="drive")
                 nc.tensor.matmul_mx(
                     out=acc[:],
                     lhsT=feat_codes[:, FEAT_PASSES - 1, rows].bitcast(FP8X4),
@@ -303,8 +318,7 @@ def tile_instrumentedlocmblock_pa_kernel(
                 )
 
         def damping_net(c):
-            cols = slice(c * PAIR, (c + 1) * PAIR)
-            t_cols = update.tile([P, MODE_TILES, PAIR], F32, tag="t_cols", bufs=1, name="t_cols%d" % c)
+            t_cols = weights_in.tile([P, MODE_TILES, PAIR], F32, tag="raw", name="t_cols%d" % c)
             for i in range(MODE_TILES):
                 modes = slice(i * P, (i + 1) * P)
                 acc = psum.tile([P, PAIR], F32, tag="bank")
@@ -313,8 +327,8 @@ def tile_instrumentedlocmblock_pa_kernel(
                         out=acc[:],
                         lhsT=w2_codes[:, g, modes].bitcast(FP8X4),
                         lhsT_scale=w2_scales[:, g, modes],
-                        rhs=h_codes[:, g, cols].bitcast(FP8X4),
-                        rhs_scale=h_scales[:, g, cols],
+                        rhs=h_codes[c][:, g, :].bitcast(FP8X4),
+                        rhs_scale=h_scales[c][:, g, :],
                         start=(g == 0),
                         stop=(g == HID_PASSES - 1),
                     )
@@ -334,11 +348,11 @@ def tile_instrumentedlocmblock_pa_kernel(
                     out=gamma[:, half * BANK : (half + 1) * BANK], in_=bank[:].rearrange("p q r -> p (q r)"),
                     func=ACT.Identity, bias=1.0, scale=1.0,
                 )
-            nc.sync.dma_start(out=gamma_rows[:, j, :], in_=gamma[:])
+            nc.scalar.dma_start(out=gamma_rows[:, j, :], in_=gamma[:])
             return gamma
 
         def damp(j, gamma):
-            kept = update.tile([P, MODES], F32, tag="kept", name="kept%d" % j)
+            kept = update.tile([P, MODES], F32, tag="kept", bufs=4, name="kept%d" % j)
             nc.vector.scalar_tensor_tensor(
                 out=kept[:], in0=gamma[:], scalar=minus_rate[:, 0:1], in1=z_sb[:, j, :], op0=ALU.add, op1=ALU.mult
             )
@@ -350,24 +364,38 @@ def tile_instrumentedlocmblock_pa_kernel(
             )
             nc.sync.dma_start(out=z_next_rows[:, j, :], in_=z_next[:])
 
-        def new_position(j, z_next):
-            y_next = update.tile([P, MODES], F32, tag="y_next", name="y_next%d" % j)
+        def new_position(j, kept, z_next):
+            y_next = kept
             nc.vector.scalar_tensor_tensor(
                 out=y_next[:], in0=z_next[:], scalar=dt_col[:, 0:1], in1=y_sb[:, j, :], op0=ALU.mult, op1=ALU.add
             )
             nc.sync.dma_start(out=y_next_rows[:, j, :], in_=y_next[:])
 
         forces = {}
-
-        def gather_forces(c):
-            for j in (2 * c, 2 * c + 1):
-                forces[j] = spring(j)
-                drive(j, forces[j])
+        planes = {}
+        kept = {}
+        gamma = {}
+        VC = nc.vector.tensor_copy
+        SC = nc.scalar.copy
+        def new_planes(c):
+            planes[c] = [new_h_planes(), new_h_planes()]
+        def SP(j): forces[j] = spring(j)
+        def DR(j): drive(j, forces[j])
+        def W(j): kept[j] = damp(j, gamma[j])
+        def Z(j): new_velocity(j, kept[j], forces[j])
+        def Y(j): new_position(j, kept[j], forces[j])
+        def G(j, t): gamma[j] = damping_of(j, t)
+        def HID(c, n): hidden_layer(c, n, planes[c][n // 2])
+        hg = {}
+        f = {}
+        v = {}
+        def RG(c, g, e): hg[c, g] = regroup_hidden(planes[c][g], e)
+        def QH(c, g): quantise_hidden(c, g, hg[c, g])
 
         quantise_feats(0, group_feats(0))
-        forces[0] = spring(0)
-        forces[1] = spring(1)
-        planes = [new_h_planes(), new_h_planes()]
+        SP(0)
+        SP(1)
+        new_planes(0)
         grouped_w1 = group_w1(0)
         for n in range(W1_UNITS):
             quantise_w1(n, grouped_w1)
@@ -375,55 +403,97 @@ def tile_instrumentedlocmblock_pa_kernel(
                 grouped_w1 = group_w1(n + 1)
             else:
                 grouped_drive = group_b()
-            hidden_layer(0, n, planes[n // 2])
-        quantise_hidden(0, 0, regroup_hidden(planes[0]))
+            HID(0, n)
+            if n == 2:
+                RG(0, 0, VC)
+        f[1] = group_feats(1)
+        QH(0, 0)
         quantise_b(grouped_drive)
-        grouped_feats = group_feats(1)
-        quantise_hidden(0, 1, regroup_hidden(planes[1]))
-        drive(0, forces[0])
-        drive(1, forces[1])
-        quantise_feats(1, grouped_feats)
-        quantise_w2(0, group_w2(0))
-        quantise_w2(1, group_w2(1))
+        RG(0, 1, SC)
+        DR(0)
+        quantise_feats(1, f[1])
+        v[0] = group_w2(0)
+        DR(1)
+        new_planes(1)
+        HID(1, 0)
+        QH(0, 1)
+        v[1] = group_w2(1)
+        quantise_w2(0, v[0])
+        HID(1, 1)
+        SP(2)
+        RG(1, 0, SC)
+        quantise_w2(1, v[1])
         t_cols = damping_net(0)
-        gather_forces(1)
-
-        for c in range(1, CHUNKS):
-            old_a, old_b = 2 * c - 2, 2 * c - 1
-
-            gamma_a = damping_of(old_a, t_cols)
-            planes_a = new_h_planes()
-            hidden_layer(c, 0, planes_a)
-            hidden_layer(c, 1, planes_a)
-            kept_a = damp(old_a, gamma_a)
-            h_grouped_a = regroup_hidden(planes_a)
-            new_velocity(old_a, kept_a, forces[old_a])
-            quantise_hidden(c, 0, h_grouped_a)
-            new_position(old_a, forces[old_a])
-
-            gamma_b = damping_of(old_b, t_cols)
-            planes_b = new_h_planes()
-            hidden_layer(c, 2, planes_b)
-            hidden_layer(c, 3, planes_b)
-            quantise_hidden(c, 1, regroup_hidden(planes_b))
-            kept_b = damp(old_b, gamma_b)
-
-            if c + 1 < CHUNKS:
-                grouped_feats = group_feats(c + 1)
-            t_cols = damping_net(c)
-            new_velocity(old_b, kept_b, forces[old_b])
-            if c + 1 < CHUNKS:
-                quantise_feats(c + 1, grouped_feats)
-            new_position(old_b, forces[old_b])
-            if c + 1 < CHUNKS:
-                gather_forces(c + 1)
-
-        last_a, last_b = ROW_TILES - 2, ROW_TILES - 1
-        gamma_a = damping_of(last_a, t_cols)
-        kept_a = damp(last_a, gamma_a)
-        gamma_b = damping_of(last_b, t_cols)
-        new_velocity(last_a, kept_a, forces[last_a])
-        kept_b = damp(last_b, gamma_b)
-        new_position(last_a, forces[last_a])
-        new_velocity(last_b, kept_b, forces[last_b])
-        new_position(last_b, forces[last_b])
+        SP(3)
+        HID(1, 2)
+        DR(2)
+        f[2] = group_feats(2)
+        HID(1, 3)
+        DR(3)
+        QH(1, 0)
+        G(0, t_cols)
+        RG(1, 1, SC)
+        G(1, t_cols)
+        quantise_feats(2, f[2])
+        QH(1, 1)
+        new_planes(2)
+        W(0)
+        W(1)
+        HID(2, 0)
+        SP(4)
+        Z(0)
+        Z(1)
+        HID(2, 1)
+        RG(2, 0, SC)
+        DR(4)
+        Y(0)
+        Y(1)
+        t_cols = damping_net(1)
+        QH(2, 0)
+        f[3] = group_feats(3)
+        HID(2, 2)
+        SP(5)
+        DR(5)
+        HID(2, 3)
+        RG(2, 1, SC)
+        G(2, t_cols)
+        quantise_feats(3, f[3])
+        QH(2, 1)
+        G(3, t_cols)
+        W(2)
+        W(3)
+        new_planes(3)
+        HID(3, 0)
+        SP(6)
+        Z(2)
+        Z(3)
+        HID(3, 1)
+        RG(3, 0, SC)
+        DR(6)
+        Y(2)
+        Y(3)
+        t_cols = damping_net(2)
+        QH(3, 0)
+        HID(3, 2)
+        SP(7)
+        HID(3, 3)
+        RG(3, 1, SC)
+        DR(7)
+        G(4, t_cols)
+        QH(3, 1)
+        G(5, t_cols)
+        W(4)
+        W(5)
+        t_cols = damping_net(3)
+        Z(4)
+        Z(5)
+        Y(4)
+        Y(5)
+        G(6, t_cols)
+        G(7, t_cols)
+        W(6)
+        W(7)
+        Z(6)
+        Z(7)
+        Y(6)
+        Y(7)

@@ -38,7 +38,7 @@ TILES_IN_BANK = BANK // P
 
 RAW_SLOTS = 3
 STAGE_SLOTS = 2 * FEAT_PASSES
-FORCE_SLOTS = 7
+FORCE_SLOTS = 8
 
 FLOPS = 2 * BATCH * (HIDDEN * FEATS + MODES * DRIVE + MODES * HIDDEN)
 
@@ -68,9 +68,12 @@ def tile_instrumentedlocmblock_pa_kernel(
         z_sb = resident.tile([P, ROW_TILES, MODES], BF16)
         u_sb = resident.tile([P, ROW_TILES, DRIVE], BF16)
 
-        def load_chunk(c):
+        def load_y(c):
             tiles = slice(2 * c, 2 * c + 2)
             nc.sync.dma_start(out=y_sb[:, tiles, :], in_=y_rows[:, tiles, :])
+
+        def load_zu(c):
+            tiles = slice(2 * c, 2 * c + 2)
             nc.sync.dma_start(out=z_sb[:, tiles, :], in_=z_rows[:, tiles, :])
             nc.sync.dma_start(out=u_sb[:, tiles, :], in_=u_rows[:, tiles, :])
 
@@ -91,27 +94,33 @@ def tile_instrumentedlocmblock_pa_kernel(
         nc.scalar.dma_start(out=stiffness_rows[0:1, :], in_=omega_sq.rearrange("(o r) -> o r", o=1))
         nc.scalar.dma_start(out=stiffness_rows[32:33, :], in_=alpha_lambda.rearrange("(o r) -> o r", o=1))
 
-        for half in range(HALVES):
-            cols = slice(half * BANK, (half + 1) * BANK)
-            nc.sync.dma_start(out=y_sb[:, 0:2, cols], in_=y_rows[:, 0:2, cols])
-        nc.sync.dma_start(out=z_sb[:, 0:2, :], in_=z_rows[:, 0:2, :])
-        nc.sync.dma_start(out=u_sb[:, 0:2, :], in_=u_rows[:, 0:2, :])
         w1_raw = []
-        for n in range(W1_UNITS):
+
+        def load_w1(n):
             raw = weights_in.tile([P, 2, FEATS], BF16, tag="raw", name="w1_raw%d" % n)
             nc.sync.dma_start(out=raw[:], in_=w1_rows[n])
             w1_raw.append(raw)
-        b_raw = weights_in.tile([P, MODE_TILES, DRIVE], BF16, tag="raw")
-        nc.sync.dma_start(out=b_raw[:], in_=b_rows)
-        load_chunk(1)
+
         w2_raw = []
-        for part in range(W2_PARTS):
+
+        def load_w2(part):
             raw = weights_in.tile([P, PART_TILES, HIDDEN], BF16, tag="raw", name="w2_raw%d" % part)
             nc.sync.dma_start(out=raw[:], in_=w2_rows[:, part * PART_TILES : (part + 1) * PART_TILES, :])
             w2_raw.append(raw)
-        for c in range(2, CHUNKS):
-            load_chunk(c)
 
+        for half in range(HALVES):
+            cols = slice(half * BANK, (half + 1) * BANK)
+            nc.sync.dma_start(out=y_sb[:, 0:2, cols], in_=y_rows[:, 0:2, cols])
+        load_zu(0)
+        for n in range(W1_UNITS):
+            load_w1(n)
+        b_raw = weights_in.tile([P, MODE_TILES, DRIVE], BF16, tag="raw")
+        nc.sync.dma_start(out=b_raw[:], in_=b_rows)
+        load_w2(0)
+        load_w2(1)
+        for c in range(1, CHUNKS):
+            load_y(c)
+            load_zu(c)
         ident = resident.tile([P, P], F32)
         make_identity(nc, ident[:])
 
@@ -138,33 +147,6 @@ def tile_instrumentedlocmblock_pa_kernel(
         )
         nc.vector.tensor_tensor(out=minus_step[:], in0=minus_dt[:], in1=tiny_step[:], op=ALU.subtract)
         nc.vector.reciprocal(out=minus_rate[:], in_=minus_step[:])
-
-        b1_bank = psum.tile([P, P], F32, tag="bank")
-        nc.tensor.transpose(b1_bank[:], b1_rows[:].bitcast(F32), ident[:])
-        b1_words = resident.tile([P, W1_UNITS], F32)
-        nc.vector.tensor_copy(out=b1_words[:], in_=b1_bank[:, 0:W1_UNITS])
-        b1_col = resident.tile([P, 2 * W1_UNITS], F32)
-        nc.vector.tensor_copy(out=b1_col[:], in_=b1_words[:].bitcast(BF16))
-
-        b2_rows_f32 = resident.tile([P, P], F32)
-        nc.vector.tensor_copy(out=b2_rows_f32[:], in_=b2_rows[:])
-        b2_bank = psum.tile([P, P], F32, tag="bank")
-        nc.tensor.transpose(b2_bank[:], b2_rows_f32[:], ident[:])
-        half_b2_col = resident.tile([P, MODE_TILES], F32)
-        nc.vector.tensor_scalar(
-            out=half_b2_col[:], in0=b2_bank[:, 0:MODE_TILES], scalar1=0.5, scalar2=None, op0=ALU.mult
-        )
-
-        pull = resident.tile([P, MODES], F32)
-        for half in range(HALVES):
-            cols = slice(half * BANK, (half + 1) * BANK)
-            stiffness_bank = psum.tile([P, BANK], F32, tag="bank")
-            nc.tensor.matmul(
-                out=stiffness_bank[:], lhsT=pick_stiffness[:], rhs=stiffness_rows[:, cols], start=True, stop=True
-            )
-            nc.vector.tensor_scalar(
-                out=pull[:, cols], in0=stiffness_bank[:], scalar1=minus_dt[:, 0:1], scalar2=None, op0=ALU.mult
-            )
 
         feat_codes = resident.tile([P, FEAT_PASSES, BATCH], U32, align_bytes=64)
         feat_scales = resident.tile([P, FEAT_PASSES, BATCH], U8, align_bytes=64)
@@ -200,11 +182,11 @@ def tile_instrumentedlocmblock_pa_kernel(
         u_words = u_sb[:].bitcast(F32)
         feat_sources = ((y_words, 0), (y_words, 1), (z_words, 0), (z_words, 1), (u_words, 0))
 
-        def group_feats(c):
+        def group_feats(c, k):
             grouped = []
-            for words, part in feat_sources:
+            for g, (words, part) in enumerate(feat_sources):
                 k_words = slice(part * WORDS, (part + 1) * WORDS)
-                grouped.append(transpose_and_group(words[:, 2 * c, k_words], words[:, 2 * c + 1, k_words]))
+                grouped.append(transpose_and_group(words[:, 2 * c, k_words], words[:, 2 * c + 1, k_words], on_vector=(g >= FEAT_PASSES - k)))
             return grouped
 
         def quantise_feats(c, grouped):
@@ -212,13 +194,13 @@ def tile_instrumentedlocmblock_pa_kernel(
             for g in range(FEAT_PASSES):
                 quantise(grouped[g], feat_codes[:, g, cols], feat_scales[:, g, cols])
 
-        def group_w1(n):
+        def group_w1(n, k):
             words = w1_raw[n][:].bitcast(F32)
             grouped = []
             for g in range(FEAT_PASSES):
                 k_words = slice(g * WORDS, (g + 1) * WORDS)
                 grouped.append(
-                    transpose_and_group(words[:, 0, k_words], words[:, 1, k_words], on_vector=(g == FEAT_PASSES - 1))
+                    transpose_and_group(words[:, 0, k_words], words[:, 1, k_words], on_vector=(g >= FEAT_PASSES - k))
                 )
             return grouped
 
@@ -226,11 +208,11 @@ def tile_instrumentedlocmblock_pa_kernel(
             for g in range(FEAT_PASSES):
                 quantise(grouped[g], w1_codes[:, n, g, :], w1_scales[:, n, g, :])
 
-        def group_b():
+        def group_b(k):
             words = b_raw[:].bitcast(F32)
             grouped = []
             for q in range(MODES // PAIR):
-                grouped.append(transpose_and_group(words[:, 2 * q, :], words[:, 2 * q + 1, :]))
+                grouped.append(transpose_and_group(words[:, 2 * q, :], words[:, 2 * q + 1, :], on_vector=(q >= 4 - k)))
             return grouped
 
         def quantise_b(grouped):
@@ -238,13 +220,13 @@ def tile_instrumentedlocmblock_pa_kernel(
                 cols = slice(q * PAIR, (q + 1) * PAIR)
                 quantise(grouped[q], b_codes[:, cols], b_scales[:, cols])
 
-        def group_w2(part):
+        def group_w2(part, k):
             words = w2_raw[part][:].bitcast(F32)
             grouped = []
             for g in range(HID_PASSES):
                 k_words = slice(g * WORDS, (g + 1) * WORDS)
                 for q in range(PART_TILES // 2):
-                    last = g == HID_PASSES - 1 and q == PART_TILES // 2 - 1
+                    last = 2 * g + q >= 4 - k
                     grouped.append(transpose_and_group(words[:, 2 * q, k_words], words[:, 2 * q + 1, k_words], on_vector=last))
             return grouped
 
@@ -276,7 +258,7 @@ def tile_instrumentedlocmblock_pa_kernel(
                     )
                 nc.scalar.activation(
                     out=h_planes[:, 2 * (n % 2) + e, :], in_=acc[:], func=ACT.Tanh,
-                    bias=b1_col[:, 2 * n + e : 2 * n + e + 1], scale=1.0,
+                    bias=S_['b1_col'][:, 2 * n + e : 2 * n + e + 1], scale=1.0,
                 )
 
         def regroup_hidden(h_planes, copy):
@@ -295,7 +277,7 @@ def tile_instrumentedlocmblock_pa_kernel(
 
         def spring(j):
             z_next = update.tile([P, MODES], F32, tag="z_next", bufs=FORCE_SLOTS, name="z_next%d" % j)
-            nc.vector.tensor_tensor(out=z_next[:], in0=pull[:], in1=y_sb[:, j, :], op=ALU.mult)
+            nc.vector.tensor_tensor(out=z_next[:], in0=S_['pull'][:], in1=y_sb[:, j, :], op=ALU.mult)
             return z_next
 
         def drive(j, z_next):
@@ -333,7 +315,7 @@ def tile_instrumentedlocmblock_pa_kernel(
                         stop=(g == HID_PASSES - 1),
                     )
                 nc.scalar.activation(
-                    out=t_cols[:, i, :], in_=acc[:], func=ACT.Tanh, bias=half_b2_col[:, i : i + 1], scale=0.5
+                    out=t_cols[:, i, :], in_=acc[:], func=ACT.Tanh, bias=S_['half_b2_col'][:, i : i + 1], scale=0.5
                 )
             return t_cols
 
@@ -371,126 +353,172 @@ def tile_instrumentedlocmblock_pa_kernel(
             )
             nc.sync.dma_start(out=y_next_rows[:, j, :], in_=y_next[:])
 
+
         forces = {}
         planes = {}
         kept = {}
         gamma = {}
+        hg = {}
+        f = {}
+        w = {}
+        v = {}
+        t_cols = {}
+        bb = {}
         VC = nc.vector.tensor_copy
         SC = nc.scalar.copy
-        def new_planes(c):
-            planes[c] = [new_h_planes(), new_h_planes()]
+        def F(c, k): f[c] = group_feats(c, k)
+        def QF(c): quantise_feats(c, f[c])
+        def W1(n, k): w[n] = group_w1(n, k)
+        def QW1(n): quantise_w1(n, w[n])
+        def B(i, k): bb[0] = group_b(k)
+        def QB(i): quantise_b(bb[0])
+        def V(i, k): v[i] = group_w2(i, k)
+        def QV(i): quantise_w2(i, v[i])
         def SP(j): forces[j] = spring(j)
         def DR(j): drive(j, forces[j])
+        def DM(c): t_cols[c] = damping_net(c)
+        def G(j): gamma[j] = damping_of(j, t_cols[j // 2])
         def W(j): kept[j] = damp(j, gamma[j])
         def Z(j): new_velocity(j, kept[j], forces[j])
         def Y(j): new_position(j, kept[j], forces[j])
-        def G(j, t): gamma[j] = damping_of(j, t)
-        def HID(c, n): hidden_layer(c, n, planes[c][n // 2])
-        hg = {}
-        f = {}
-        v = {}
-        def RG(c, g, e): hg[c, g] = regroup_hidden(planes[c][g], e)
+        def HID(c, n):
+            if (c, n // 2) not in planes:
+                planes[c, n // 2] = new_h_planes()
+            hidden_layer(c, n, planes[c, n // 2])
+        def RG(c, g, e): hg[c, g] = regroup_hidden(planes[c, g], e)
         def QH(c, g): quantise_hidden(c, g, hg[c, g])
+        S_ = {}
+        def CONST(i):
+            b1_bank = psum.tile([P, P], F32, tag="bank")
+            nc.tensor.transpose(b1_bank[:], b1_rows[:].bitcast(F32), ident[:])
+            b1_words = resident.tile([P, W1_UNITS], F32)
+            nc.vector.tensor_copy(out=b1_words[:], in_=b1_bank[:, 0:W1_UNITS])
+            b1_col = resident.tile([P, 2 * W1_UNITS], F32)
+            nc.vector.tensor_copy(out=b1_col[:], in_=b1_words[:].bitcast(BF16))
 
-        quantise_feats(0, group_feats(0))
+            b2_rows_f32 = resident.tile([P, P], F32)
+            nc.vector.tensor_copy(out=b2_rows_f32[:], in_=b2_rows[:])
+            b2_bank = psum.tile([P, P], F32, tag="bank")
+            nc.tensor.transpose(b2_bank[:], b2_rows_f32[:], ident[:])
+            half_b2_col = resident.tile([P, MODE_TILES], F32)
+            nc.vector.tensor_scalar(
+                out=half_b2_col[:], in0=b2_bank[:, 0:MODE_TILES], scalar1=0.5, scalar2=None, op0=ALU.mult
+            )
+
+            pull = resident.tile([P, MODES], F32)
+            for half in range(HALVES):
+                cols = slice(half * BANK, (half + 1) * BANK)
+                stiffness_bank = psum.tile([P, BANK], F32, tag="bank")
+                nc.tensor.matmul(
+                    out=stiffness_bank[:], lhsT=pick_stiffness[:], rhs=stiffness_rows[:, cols], start=True, stop=True
+                )
+                nc.vector.tensor_scalar(
+                    out=pull[:, cols], in0=stiffness_bank[:], scalar1=minus_dt[:, 0:1], scalar2=None, op0=ALU.mult
+                )
+            S_['half_b2_col'] = half_b2_col
+            S_['b1_col'] = b1_col
+            S_['pull'] = pull
+        F(0, 0)
+        CONST(0)
+        QF(0)
+        W1(0, 1)
         SP(0)
-        SP(1)
-        new_planes(0)
-        grouped_w1 = group_w1(0)
-        for n in range(W1_UNITS):
-            quantise_w1(n, grouped_w1)
-            if n + 1 < W1_UNITS:
-                grouped_w1 = group_w1(n + 1)
-            else:
-                grouped_drive = group_b()
-            HID(0, n)
-            if n == 2:
-                RG(0, 0, VC)
-        f[1] = group_feats(1)
-        QH(0, 0)
-        quantise_b(grouped_drive)
-        RG(0, 1, SC)
+        QW1(0)
+        W1(1, 1)
+        QW1(1)
+        HID(0, 0)
+        W1(2, 1)
+        QW1(2)
+        W1(3, 1)
+        HID(0, 1)
+        QW1(3)
+        B(0, 1)
+        RG(0, 0, VC)
+        QB(0)
+        V(0, 1)
+        HID(0, 2)
         DR(0)
-        quantise_feats(1, f[1])
-        v[0] = group_w2(0)
-        DR(1)
-        new_planes(1)
-        HID(1, 0)
+        F(1, 0)
+        QV(0)
+        QF(1)
+        V(1, 1)
+        SP(1)
+        HID(0, 3)
+        F(2, 0)
+        RG(0, 1, VC)
+        QV(1)
+        QH(0, 0)
         QH(0, 1)
-        v[1] = group_w2(1)
-        quantise_w2(0, v[0])
+        DR(1)
+        HID(1, 0)
         HID(1, 1)
         SP(2)
-        RG(1, 0, SC)
-        quantise_w2(1, v[1])
-        t_cols = damping_net(0)
         SP(3)
+        DM(0)
+        RG(1, 0, SC)
         HID(1, 2)
-        DR(2)
-        f[2] = group_feats(2)
-        HID(1, 3)
-        DR(3)
+        SP(4)
+        QF(2)
         QH(1, 0)
-        G(0, t_cols)
-        RG(1, 1, SC)
-        G(1, t_cols)
-        quantise_feats(2, f[2])
-        QH(1, 1)
-        new_planes(2)
+        G(0)
+        G(1)
+        SP(5)
+        DR(2)
+        HID(1, 3)
         W(0)
         W(1)
+        RG(1, 1, SC)
         HID(2, 0)
-        SP(4)
         Z(0)
-        Z(1)
+        F(3, 0)
         HID(2, 1)
+        Z(1)
         RG(2, 0, SC)
-        DR(4)
-        Y(0)
-        Y(1)
-        t_cols = damping_net(1)
-        QH(2, 0)
-        f[3] = group_feats(3)
+        QH(1, 1)
+        DR(3)
         HID(2, 2)
-        SP(5)
-        DR(5)
+        Y(0)
+        QH(2, 0)
+        DM(1)
         HID(2, 3)
+        Y(1)
         RG(2, 1, SC)
-        G(2, t_cols)
-        quantise_feats(3, f[3])
+        QF(3)
+        DR(4)
+        G(2)
+        G(3)
         QH(2, 1)
-        G(3, t_cols)
-        W(2)
-        W(3)
-        new_planes(3)
-        HID(3, 0)
+        DR(5)
         SP(6)
-        Z(2)
-        Z(3)
+        HID(3, 0)
         HID(3, 1)
         RG(3, 0, SC)
-        DR(6)
-        Y(2)
-        Y(3)
-        t_cols = damping_net(2)
+        W(2)
+        W(3)
+        SP(7)
+        DM(2)
+        Z(2)
         QH(3, 0)
         HID(3, 2)
-        SP(7)
+        Z(3)
         HID(3, 3)
         RG(3, 1, SC)
-        DR(7)
-        G(4, t_cols)
+        DR(6)
+        G(4)
+        Y(2)
+        G(5)
         QH(3, 1)
-        G(5, t_cols)
+        DR(7)
+        Y(3)
         W(4)
         W(5)
-        t_cols = damping_net(3)
+        DM(3)
         Z(4)
         Z(5)
+        G(6)
+        G(7)
         Y(4)
         Y(5)
-        G(6, t_cols)
-        G(7, t_cols)
         W(6)
         W(7)
         Z(6)

@@ -78,17 +78,16 @@ def tile_instrumentedlocmblock_pa_kernel(
             nc.sync.dma_start(out=u_sb[:, tiles, :], in_=u_rows[:, tiles, :])
 
         w1_rows = dmlp_w1.rearrange("(n p e) f -> n p e f", p=P, e=2)
-        b_rows = B_tilde.rearrange("(i p) k -> p i k", p=P)
-        w2_rows = dmlp_w2.rearrange("(i p) k -> p i k", p=P)
+        b_rows = B_tilde.rearrange("(p i) k -> p i k", i=MODE_TILES)
+        w2_rows = dmlp_w2.rearrange("(p i) k -> p i k", i=MODE_TILES)
 
         dt_bf = resident.tile([P, 1], BF16)
         nc.scalar.dma_start(out=dt_bf[:], in_=dt.partition_broadcast(P))
         b1_rows = resident.tile([P, 2 * P], BF16)
         nc.vector.memset(b1_rows[:], 0.0)
         nc.scalar.dma_start(out=b1_rows[0:W1_UNITS, :], in_=dmlp_b1.rearrange("(n w) -> n w", n=W1_UNITS))
-        b2_rows = resident.tile([P, P], BF16)
-        nc.vector.memset(b2_rows[:], 0.0)
-        nc.scalar.dma_start(out=b2_rows[0:MODE_TILES, :], in_=dmlp_b2.rearrange("(i p) -> i p", p=P))
+        b2_bf = resident.tile([P, MODE_TILES], BF16)
+        nc.scalar.dma_start(out=b2_bf[:], in_=dmlp_b2.rearrange("(p i) -> p i", i=MODE_TILES))
         stiffness_rows = resident.tile([P, MODES], BF16)
         nc.vector.memset(stiffness_rows[:], 0.0)
         nc.scalar.dma_start(out=stiffness_rows[0:1, :], in_=omega_sq.rearrange("(o r) -> o r", o=1))
@@ -108,9 +107,7 @@ def tile_instrumentedlocmblock_pa_kernel(
             nc.sync.dma_start(out=raw[:], in_=w2_rows[:, part * PART_TILES : (part + 1) * PART_TILES, :])
             w2_raw.append(raw)
 
-        for half in range(HALVES):
-            cols = slice(half * BANK, (half + 1) * BANK)
-            nc.sync.dma_start(out=y_sb[:, 0:2, cols], in_=y_rows[:, 0:2, cols])
+        load_y(0)
         load_zu(0)
         for n in range(W1_UNITS):
             load_w1(n)
@@ -280,6 +277,9 @@ def tile_instrumentedlocmblock_pa_kernel(
             nc.vector.tensor_tensor(out=z_next[:], in0=S_['pull'][:], in1=y_sb[:, j, :], op=ALU.mult)
             return z_next
 
+        def modes_of(rows, half):
+            return rows[:].rearrange("b (p i) -> b p i", i=MODE_TILES)[:, :, half * TILES_IN_BANK : (half + 1) * TILES_IN_BANK]
+
         def drive(j, z_next):
             rows = slice(j * P, (j + 1) * P)
             for half in range(HALVES):
@@ -294,9 +294,10 @@ def tile_instrumentedlocmblock_pa_kernel(
                     start=True,
                     stop=True,
                 )
+                force = modes_of(z_next, half)
                 nc.vector.scalar_tensor_tensor(
-                    out=z_next[:, cols], in0=acc[:], scalar=dt_col[:, 0:1], in1=z_next[:, cols],
-                    op0=ALU.mult, op1=ALU.add,
+                    out=force, in0=acc[:].rearrange("b (q p) -> b p q", q=TILES_IN_BANK), scalar=dt_col[:, 0:1],
+                    in1=force, op0=ALU.mult, op1=ALU.add,
                 )
 
         def damping_net(c):
@@ -327,7 +328,7 @@ def tile_instrumentedlocmblock_pa_kernel(
                 for q in range(TILES_IN_BANK):
                     nc.tensor.transpose(bank[:, q, :], t_cols[:, half * TILES_IN_BANK + q, rows], ident[:])
                 nc.scalar.activation(
-                    out=gamma[:, half * BANK : (half + 1) * BANK], in_=bank[:].rearrange("p q r -> p (q r)"),
+                    out=modes_of(gamma, half), in_=bank[:].rearrange("b q p -> b p q"),
                     func=ACT.Identity, bias=1.0, scale=1.0,
                 )
             nc.scalar.dma_start(out=gamma_rows[:, j, :], in_=gamma[:])
@@ -396,14 +397,8 @@ def tile_instrumentedlocmblock_pa_kernel(
             b1_col = resident.tile([P, 2 * W1_UNITS], F32)
             nc.vector.tensor_copy(out=b1_col[:], in_=b1_words[:].bitcast(BF16))
 
-            b2_rows_f32 = resident.tile([P, P], F32)
-            nc.vector.tensor_copy(out=b2_rows_f32[:], in_=b2_rows[:])
-            b2_bank = psum.tile([P, P], F32, tag="bank")
-            nc.tensor.transpose(b2_bank[:], b2_rows_f32[:], ident[:])
             half_b2_col = resident.tile([P, MODE_TILES], F32)
-            nc.vector.tensor_scalar(
-                out=half_b2_col[:], in0=b2_bank[:, 0:MODE_TILES], scalar1=0.5, scalar2=None, op0=ALU.mult
-            )
+            nc.vector.tensor_scalar(out=half_b2_col[:], in0=b2_bf[:], scalar1=0.5, scalar2=None, op0=ALU.mult)
 
             pull = resident.tile([P, MODES], F32)
             for half in range(HALVES):

@@ -16,8 +16,6 @@ PACK = 4
 K_PASS = P * PACK
 WORDS = K_PASS // 2
 BANK = 512
-PSUM_BANKS = 8
-DRIVE_BANKS = 2
 PAIR = 2 * P
 
 BATCH = 1024
@@ -26,19 +24,22 @@ DRIVE = 512
 HIDDEN = 1024
 FEATS = 2 * MODES + DRIVE
 ROW_TILES = BATCH // P
-MODE_TILES = MODES // P
 CHUNKS = BATCH // PAIR
 FEAT_PASSES = FEATS // K_PASS
 HID_PASSES = HIDDEN // K_PASS
 W1_UNITS = HIDDEN // PAIR
-W2_PARTS = 2
-PART_TILES = MODE_TILES // W2_PARTS
 HALVES = MODES // BANK
-TILES_IN_BANK = BANK // P
+HALF_TILES = BANK // P
+MODE_TILES = HALVES * HALF_TILES
+B_PASSES = MODES // PAIR
+W2_BANKS = HID_PASSES * HALF_TILES // 2
 
+DRIVE_BANKS = 2
+SHARED_BANKS = 8 - DRIVE_BANKS
 RAW_SLOTS = 3
 STAGE_SLOTS = 2 * FEAT_PASSES
-FORCE_SLOTS = 8
+GAMMA_SLOTS = 3
+KEPT_SLOTS = 4
 
 FLOPS = 2 * BATCH * (HIDDEN * FEATS + MODES * DRIVE + MODES * HIDDEN)
 
@@ -53,8 +54,8 @@ def tile_instrumentedlocmblock_pa_kernel(
         weights_in = ctx.enter_context(tc.tile_pool(name="weights_in", bufs=RAW_SLOTS))
         stage = ctx.enter_context(tc.tile_pool(name="stage", bufs=STAGE_SLOTS))
         hidden = ctx.enter_context(tc.tile_pool(name="hidden", bufs=2))
-        update = ctx.enter_context(tc.tile_pool(name="update", bufs=2))
-        psum = ctx.enter_context(tc.psum_pool(name="psum", bufs=PSUM_BANKS - DRIVE_BANKS))
+        update = ctx.enter_context(tc.tile_pool(name="update", bufs=KEPT_SLOTS))
+        psum = ctx.enter_context(tc.psum_pool(name="psum", bufs=SHARED_BANKS))
         drive_psum = ctx.enter_context(tc.psum_pool(name="drive_psum", bufs=DRIVE_BANKS))
         ctx.enter_context(tc.manual_schedule())
 
@@ -78,43 +79,41 @@ def tile_instrumentedlocmblock_pa_kernel(
             nc.sync.dma_start(out=u_sb[:, tiles, :], in_=u_rows[:, tiles, :])
 
         w1_rows = dmlp_w1.rearrange("(n p e) f -> n p e f", p=P, e=2)
-        b_rows = B_tilde.rearrange("(p i) k -> p i k", i=MODE_TILES)
-        w2_rows = dmlp_w2.rearrange("(p i) k -> p i k", i=MODE_TILES)
-
-        dt_bf = resident.tile([P, 1], BF16)
-        nc.scalar.dma_start(out=dt_bf[:], in_=dt.partition_broadcast(P))
-        b1_rows = resident.tile([P, 2 * P], BF16)
-        nc.vector.memset(b1_rows[:], 0.0)
-        nc.scalar.dma_start(out=b1_rows[0:W1_UNITS, :], in_=dmlp_b1.rearrange("(n w) -> n w", n=W1_UNITS))
-        b2_bf = resident.tile([P, MODE_TILES], BF16)
-        nc.scalar.dma_start(out=b2_bf[:], in_=dmlp_b2.rearrange("(p i) -> p i", i=MODE_TILES))
-        stiffness_rows = resident.tile([P, MODES], BF16)
-        nc.vector.memset(stiffness_rows[:], 0.0)
-        nc.scalar.dma_start(out=stiffness_rows[0:1, :], in_=omega_sq.rearrange("(o r) -> o r", o=1))
-        nc.scalar.dma_start(out=stiffness_rows[32:33, :], in_=alpha_lambda.rearrange("(o r) -> o r", o=1))
-
+        b_rows = B_tilde.rearrange("(h p q) k -> p h q k", p=P, q=HALF_TILES)
+        w2_rows = dmlp_w2.rearrange("(h p q) k -> p h q k", p=P, q=HALF_TILES)
         w1_raw = []
+        w2_raw = []
 
         def load_w1(n):
             raw = weights_in.tile([P, 2, FEATS], BF16, tag="raw", name="w1_raw%d" % n)
             nc.sync.dma_start(out=raw[:], in_=w1_rows[n])
             w1_raw.append(raw)
 
-        w2_raw = []
-
-        def load_w2(part):
-            raw = weights_in.tile([P, PART_TILES, HIDDEN], BF16, tag="raw", name="w2_raw%d" % part)
-            nc.sync.dma_start(out=raw[:], in_=w2_rows[:, part * PART_TILES : (part + 1) * PART_TILES, :])
+        def load_w2(h):
+            raw = weights_in.tile([P, HALF_TILES, HIDDEN], BF16, tag="raw", name="w2_raw%d" % h)
+            nc.sync.dma_start(out=raw[:], in_=w2_rows[:, h])
             w2_raw.append(raw)
+
+        dt_bf = resident.tile([P, 1], BF16)
+        nc.scalar.dma_start(out=dt_bf[:], in_=dt.partition_broadcast(P))
+        b1_rows = resident.tile([P, 2 * P], BF16)
+        nc.vector.memset(b1_rows[:], 0.0)
+        nc.scalar.dma_start(out=b1_rows[0:W1_UNITS, :], in_=dmlp_b1.rearrange("(n w) -> n w", n=W1_UNITS))
+        b2_bf = resident.tile([P, HALVES, HALF_TILES], BF16)
+        nc.scalar.dma_start(out=b2_bf[:], in_=dmlp_b2.rearrange("(h p q) -> p h q", p=P, q=HALF_TILES))
+        stiffness_rows = resident.tile([P, MODES], BF16)
+        nc.vector.memset(stiffness_rows[:], 0.0)
+        nc.scalar.dma_start(out=stiffness_rows[0:1, :], in_=omega_sq.rearrange("(o r) -> o r", o=1))
+        nc.scalar.dma_start(out=stiffness_rows[32:33, :], in_=alpha_lambda.rearrange("(o r) -> o r", o=1))
 
         load_y(0)
         load_zu(0)
         for n in range(W1_UNITS):
             load_w1(n)
         b_raw = weights_in.tile([P, MODE_TILES, DRIVE], BF16, tag="raw")
-        nc.sync.dma_start(out=b_raw[:], in_=b_rows)
-        load_w2(0)
-        load_w2(1)
+        nc.sync.dma_start(out=b_raw[:].rearrange("p (h q) k -> p h q k", q=HALF_TILES), in_=b_rows)
+        for h in range(HALVES):
+            load_w2(h)
         for c in range(1, CHUNKS):
             load_y(c)
             load_zu(c)
@@ -145,6 +144,29 @@ def tile_instrumentedlocmblock_pa_kernel(
         nc.vector.tensor_tensor(out=minus_step[:], in0=minus_dt[:], in1=tiny_step[:], op=ALU.subtract)
         nc.vector.reciprocal(out=minus_rate[:], in_=minus_step[:])
 
+        half_b2_col = resident.tile([P, MODE_TILES], F32)
+        nc.vector.tensor_scalar(
+            out=half_b2_col[:], in0=b2_bf[:].rearrange("p h q -> p (h q)"), scalar1=0.5, scalar2=None, op0=ALU.mult
+        )
+        b1_words = resident.tile([P, W1_UNITS], F32)
+        b1_col = resident.tile([P, 2 * W1_UNITS], F32)
+        pull = resident.tile([P, MODES], F32)
+
+        def constants_by_tensor():
+            b1_bank = psum.tile([P, P], F32, tag="bank")
+            nc.tensor.transpose(b1_bank[:], b1_rows[:].bitcast(F32), ident[:])
+            nc.vector.tensor_copy(out=b1_words[:], in_=b1_bank[:, 0:W1_UNITS])
+            nc.vector.tensor_copy(out=b1_col[:], in_=b1_words[:].bitcast(BF16))
+            for h in range(HALVES):
+                cols = slice(h * BANK, (h + 1) * BANK)
+                stiffness_bank = psum.tile([P, BANK], F32, tag="bank")
+                nc.tensor.matmul(
+                    out=stiffness_bank[:], lhsT=pick_stiffness[:], rhs=stiffness_rows[:, cols], start=True, stop=True
+                )
+                nc.vector.tensor_scalar(
+                    out=pull[:, cols], in0=stiffness_bank[:], scalar1=minus_dt[:, 0:1], scalar2=None, op0=ALU.mult
+                )
+
         feat_codes = resident.tile([P, FEAT_PASSES, BATCH], U32, align_bytes=64)
         feat_scales = resident.tile([P, FEAT_PASSES, BATCH], U8, align_bytes=64)
         w1_codes = resident.tile([P, W1_UNITS, FEAT_PASSES, PAIR], U32, align_bytes=64)
@@ -153,20 +175,15 @@ def tile_instrumentedlocmblock_pa_kernel(
         b_scales = resident.tile([P, MODES], U8, align_bytes=64)
         w2_codes = resident.tile([P, HID_PASSES, MODES], U32, align_bytes=64)
         w2_scales = resident.tile([P, HID_PASSES, MODES], U8, align_bytes=64)
-        h_codes = {}
-        h_scales = {}
 
-        def transpose_and_group(rows_a, rows_b, on_vector=False):
+        def transpose_and_group(rows_a, rows_b, by_vector):
             bank = psum.tile([P, 2, PAIR], F32, tag="bank")
             for s, rows in enumerate((rows_a, rows_b)):
                 for w in range(2):
                     nc.tensor.transpose(bank[:, w, s * P : (s + 1) * P], rows[:, w * P : (w + 1) * P], ident[:])
             grouped = stage.tile([P, PAIR, PACK], BF16, align_bytes=64)
-            words = bank[:].rearrange("p w c -> p c w")
-            if on_vector:
-                nc.vector.tensor_copy(out=grouped[:].bitcast(F32), in_=words)
-            else:
-                nc.scalar.copy(out=grouped[:].bitcast(F32), in_=words)
+            copy = nc.vector.tensor_copy if by_vector else nc.scalar.copy
+            copy(out=grouped[:].bitcast(F32), in_=bank[:].rearrange("p w c -> p c w"))
             return grouped
 
         def quantise(grouped, codes, scales):
@@ -178,68 +195,73 @@ def tile_instrumentedlocmblock_pa_kernel(
         z_words = z_sb[:].bitcast(F32)
         u_words = u_sb[:].bitcast(F32)
         feat_sources = ((y_words, 0), (y_words, 1), (z_words, 0), (z_words, 1), (u_words, 0))
+        feats_grouped = {}
+        w1_grouped = {}
+        b_grouped = []
+        w2_grouped = {}
 
-        def group_feats(c, k):
-            grouped = []
+        def transpose_feats(c, vector_banks):
+            feats_grouped[c] = []
             for g, (words, part) in enumerate(feat_sources):
                 k_words = slice(part * WORDS, (part + 1) * WORDS)
-                grouped.append(transpose_and_group(words[:, 2 * c, k_words], words[:, 2 * c + 1, k_words], on_vector=(g >= FEAT_PASSES - k)))
-            return grouped
+                feats_grouped[c].append(transpose_and_group(
+                    words[:, 2 * c, k_words], words[:, 2 * c + 1, k_words], g >= FEAT_PASSES - vector_banks
+                ))
 
-        def quantise_feats(c, grouped):
+        def quantise_feats(c):
             cols = slice(c * PAIR, (c + 1) * PAIR)
-            for g in range(FEAT_PASSES):
-                quantise(grouped[g], feat_codes[:, g, cols], feat_scales[:, g, cols])
+            for g, grouped in enumerate(feats_grouped[c]):
+                quantise(grouped, feat_codes[:, g, cols], feat_scales[:, g, cols])
 
-        def group_w1(n, k):
+        def transpose_w1(n, vector_banks):
             words = w1_raw[n][:].bitcast(F32)
-            grouped = []
+            w1_grouped[n] = []
             for g in range(FEAT_PASSES):
                 k_words = slice(g * WORDS, (g + 1) * WORDS)
-                grouped.append(
-                    transpose_and_group(words[:, 0, k_words], words[:, 1, k_words], on_vector=(g >= FEAT_PASSES - k))
-                )
-            return grouped
+                w1_grouped[n].append(transpose_and_group(
+                    words[:, 0, k_words], words[:, 1, k_words], g >= FEAT_PASSES - vector_banks
+                ))
 
-        def quantise_w1(n, grouped):
-            for g in range(FEAT_PASSES):
-                quantise(grouped[g], w1_codes[:, n, g, :], w1_scales[:, n, g, :])
+        def quantise_w1(n):
+            for g, grouped in enumerate(w1_grouped[n]):
+                quantise(grouped, w1_codes[:, n, g, :], w1_scales[:, n, g, :])
 
-        def group_b(k):
+        def transpose_b(vector_banks):
             words = b_raw[:].bitcast(F32)
-            grouped = []
-            for q in range(MODES // PAIR):
-                grouped.append(transpose_and_group(words[:, 2 * q, :], words[:, 2 * q + 1, :], on_vector=(q >= 4 - k)))
-            return grouped
+            for i in range(B_PASSES):
+                b_grouped.append(transpose_and_group(
+                    words[:, 2 * i, :], words[:, 2 * i + 1, :], i >= B_PASSES - vector_banks
+                ))
 
-        def quantise_b(grouped):
-            for q in range(MODES // PAIR):
-                cols = slice(q * PAIR, (q + 1) * PAIR)
-                quantise(grouped[q], b_codes[:, cols], b_scales[:, cols])
+        def quantise_b():
+            for i, grouped in enumerate(b_grouped):
+                cols = slice(i * PAIR, (i + 1) * PAIR)
+                quantise(grouped, b_codes[:, cols], b_scales[:, cols])
 
-        def group_w2(part, k):
-            words = w2_raw[part][:].bitcast(F32)
-            grouped = []
+        def transpose_w2(h, vector_banks):
+            words = w2_raw[h][:].bitcast(F32)
+            w2_grouped[h] = []
             for g in range(HID_PASSES):
                 k_words = slice(g * WORDS, (g + 1) * WORDS)
-                for q in range(PART_TILES // 2):
-                    last = 2 * g + q >= 4 - k
-                    grouped.append(transpose_and_group(words[:, 2 * q, k_words], words[:, 2 * q + 1, k_words], on_vector=last))
-            return grouped
+                for q in range(0, HALF_TILES, 2):
+                    by_vector = len(w2_grouped[h]) >= W2_BANKS - vector_banks
+                    w2_grouped[h].append(transpose_and_group(words[:, q, k_words], words[:, q + 1, k_words], by_vector))
 
-        def quantise_w2(part, grouped):
-            pairs = PART_TILES // 2
-            for g in range(HID_PASSES):
-                for q in range(pairs):
-                    cols = slice((pairs * part + q) * PAIR, (pairs * part + q + 1) * PAIR)
-                    quantise(grouped[pairs * g + q], w2_codes[:, g, cols], w2_scales[:, g, cols])
+        def quantise_w2(h):
+            for i, grouped in enumerate(w2_grouped[h]):
+                g, first = i // 2, h * BANK + (i % 2) * PAIR
+                cols = slice(first, first + PAIR)
+                quantise(grouped, w2_codes[:, g, cols], w2_scales[:, g, cols])
 
-        def new_h_planes():
-            h_planes = hidden.tile([P, PACK, PAIR], BF16)
-            return h_planes
+        h_planes = {}
+        h_grouped = {}
+        h_codes = {}
+        h_scales = {}
 
-        def hidden_layer(c, n, h_planes):
+        def hidden_units(c, n):
             cols = slice(c * PAIR, (c + 1) * PAIR)
+            if n % 2 == 0:
+                h_planes[c, n // 2] = hidden.tile([P, PACK, PAIR], BF16, tag="planes", name="planes%d_%d" % (c, n // 2))
             for e in range(2):
                 units = slice(e * P, (e + 1) * P)
                 acc = psum.tile([P, PAIR], F32, tag="bank")
@@ -254,55 +276,59 @@ def tile_instrumentedlocmblock_pa_kernel(
                         stop=(g == FEAT_PASSES - 1),
                     )
                 nc.scalar.activation(
-                    out=h_planes[:, 2 * (n % 2) + e, :], in_=acc[:], func=ACT.Tanh,
-                    bias=S_['b1_col'][:, 2 * n + e : 2 * n + e + 1], scale=1.0,
+                    out=h_planes[c, n // 2][:, 2 * (n % 2) + e, :], in_=acc[:], func=ACT.Tanh,
+                    bias=b1_col[:, 2 * n + e : 2 * n + e + 1], scale=1.0,
                 )
 
-        def regroup_hidden(h_planes, copy):
-            h_grouped = hidden.tile([P, PAIR, PACK], BF16, tag="h_grouped", bufs=2, align_bytes=64)
+        def regroup_hidden(c, g, copy):
+            grouped = hidden.tile([P, PAIR, PACK], BF16, tag="grouped", align_bytes=64)
             copy(
-                out=h_grouped[:].rearrange("p (c i) t -> p c t i", i=4),
-                in_=h_planes[:].rearrange("p t (c i) -> p c t i", i=4),
+                out=grouped[:].rearrange("p (c i) t -> p c t i", i=4),
+                in_=h_planes[c, g][:].rearrange("p t (c i) -> p c t i", i=4),
             )
-            return h_grouped
+            h_grouped[c, g] = grouped
 
-        def quantise_hidden(c, g, h_grouped):
+        def quantise_hidden(c, g):
             if g == 0:
-                h_codes[c] = hidden.tile([P, HID_PASSES, PAIR], U32, tag="h_codes", bufs=2, align_bytes=64, name="h_codes%d" % c)
-                h_scales[c] = hidden.tile([P, HID_PASSES, PAIR], U8, tag="h_scales", bufs=2, align_bytes=64, name="h_scales%d" % c)
-            quantise(h_grouped, h_codes[c][:, g, :], h_scales[c][:, g, :])
+                h_codes[c] = hidden.tile([P, HID_PASSES, PAIR], U32, tag="codes", align_bytes=64, name="h_codes%d" % c)
+                h_scales[c] = hidden.tile([P, HID_PASSES, PAIR], U8, tag="scales", align_bytes=64, name="h_scales%d" % c)
+            quantise(h_grouped[c, g], h_codes[c][:, g, :], h_scales[c][:, g, :])
+
+        z_next = {}
+        t_cols = {}
+        gammas = {}
+        kept = {}
+
+        def columns(h):
+            return slice(0, MODES) if h is None else slice(h * BANK, (h + 1) * BANK)
 
         def spring(j):
-            z_next = update.tile([P, MODES], F32, tag="z_next", bufs=FORCE_SLOTS, name="z_next%d" % j)
-            nc.vector.tensor_tensor(out=z_next[:], in0=S_['pull'][:], in1=y_sb[:, j, :], op=ALU.mult)
-            return z_next
+            z_next[j] = update.tile([P, MODES], F32, tag="z_next", bufs=ROW_TILES, name="z_next%d" % j)
+            nc.vector.tensor_tensor(out=z_next[j][:], in0=pull[:], in1=y_sb[:, j, :], op=ALU.mult)
 
-        def modes_of(rows, half):
-            return rows[:].rearrange("b (p i) -> b p i", i=MODE_TILES)[:, :, half * TILES_IN_BANK : (half + 1) * TILES_IN_BANK]
-
-        def drive(j, z_next):
+        def drive(j):
             rows = slice(j * P, (j + 1) * P)
-            for half in range(HALVES):
-                cols = slice(half * BANK, (half + 1) * BANK)
+            for h in range(HALVES):
                 acc = drive_psum.tile([P, BANK], F32, tag="drive")
                 nc.tensor.matmul_mx(
                     out=acc[:],
                     lhsT=feat_codes[:, FEAT_PASSES - 1, rows].bitcast(FP8X4),
                     lhsT_scale=feat_scales[:, FEAT_PASSES - 1, rows],
-                    rhs=b_codes[:, cols].bitcast(FP8X4),
-                    rhs_scale=b_scales[:, cols],
+                    rhs=b_codes[:, columns(h)].bitcast(FP8X4),
+                    rhs_scale=b_scales[:, columns(h)],
                     start=True,
                     stop=True,
                 )
-                force = modes_of(z_next, half)
+                force = z_next[j][:, columns(h)].rearrange("b (p q) -> b p q", q=HALF_TILES)
                 nc.vector.scalar_tensor_tensor(
-                    out=force, in0=acc[:].rearrange("b (q p) -> b p q", q=TILES_IN_BANK), scalar=dt_col[:, 0:1],
+                    out=force, in0=acc[:].rearrange("b (q p) -> b p q", q=HALF_TILES), scalar=dt_col[:, 0:1],
                     in1=force, op0=ALU.mult, op1=ALU.add,
                 )
 
-        def damping_net(c):
-            t_cols = weights_in.tile([P, MODE_TILES, PAIR], F32, tag="raw", name="t_cols%d" % c)
-            for i in range(MODE_TILES):
+        def damping_net(c, h):
+            if h == 0:
+                t_cols[c] = weights_in.tile([P, MODE_TILES, PAIR], F32, tag="raw", name="t_cols%d" % c)
+            for i in range(h * HALF_TILES, (h + 1) * HALF_TILES):
                 modes = slice(i * P, (i + 1) * P)
                 acc = psum.tile([P, PAIR], F32, tag="bank")
                 for g in range(HID_PASSES):
@@ -316,207 +342,178 @@ def tile_instrumentedlocmblock_pa_kernel(
                         stop=(g == HID_PASSES - 1),
                     )
                 nc.scalar.activation(
-                    out=t_cols[:, i, :], in_=acc[:], func=ACT.Tanh, bias=S_['half_b2_col'][:, i : i + 1], scale=0.5
+                    out=t_cols[c][:, i, :], in_=acc[:], func=ACT.Tanh, bias=half_b2_col[:, i : i + 1], scale=0.5
                 )
-            return t_cols
 
-        def damping_of(j, t_cols):
+        def gamma_half(j, h):
             rows = slice((j % 2) * P, (j % 2 + 1) * P)
-            gamma = update.tile([P, MODES], F32, tag="gamma", name="gamma%d" % j)
-            for half in range(HALVES):
-                bank = psum.tile([P, TILES_IN_BANK, P], F32, tag="bank")
-                for q in range(TILES_IN_BANK):
-                    nc.tensor.transpose(bank[:, q, :], t_cols[:, half * TILES_IN_BANK + q, rows], ident[:])
-                nc.scalar.activation(
-                    out=modes_of(gamma, half), in_=bank[:].rearrange("b q p -> b p q"),
-                    func=ACT.Identity, bias=1.0, scale=1.0,
-                )
-            nc.scalar.dma_start(out=gamma_rows[:, j, :], in_=gamma[:])
-            return gamma
-
-        def damp(j, gamma):
-            kept = update.tile([P, MODES], F32, tag="kept", bufs=4, name="kept%d" % j)
-            nc.vector.scalar_tensor_tensor(
-                out=kept[:], in0=gamma[:], scalar=minus_rate[:, 0:1], in1=z_sb[:, j, :], op0=ALU.add, op1=ALU.mult
+            if h == 0:
+                gammas[j] = update.tile([P, MODES], F32, tag="gamma", bufs=GAMMA_SLOTS, name="gamma%d" % j)
+            bank = psum.tile([P, HALF_TILES, P], F32, tag="bank")
+            for q in range(HALF_TILES):
+                nc.tensor.transpose(bank[:, q, :], t_cols[j // 2][:, h * HALF_TILES + q, rows], ident[:])
+            nc.scalar.activation(
+                out=gammas[j][:, columns(h)].rearrange("b (p q) -> b p q", q=HALF_TILES),
+                in_=bank[:].rearrange("b q p -> b p q"), func=ACT.Identity, bias=1.0, scale=1.0,
             )
-            return kept
 
-        def new_velocity(j, kept, z_next):
+        def store_gamma(j, h=None):
+            nc.sync.dma_start(out=gamma_rows[:, j, columns(h)], in_=gammas[j][:, columns(h)])
+
+        def damp(j, h=None):
+            if j not in kept:
+                kept[j] = update.tile([P, MODES], F32, tag="kept", name="kept%d" % j)
             nc.vector.scalar_tensor_tensor(
-                out=z_next[:], in0=kept[:], scalar=minus_step[:, 0:1], in1=z_next[:], op0=ALU.mult, op1=ALU.add
+                out=kept[j][:, columns(h)], in0=gammas[j][:, columns(h)], scalar=minus_rate[:, 0:1],
+                in1=z_sb[:, j, columns(h)], op0=ALU.add, op1=ALU.mult,
             )
-            nc.sync.dma_start(out=z_next_rows[:, j, :], in_=z_next[:])
 
-        def new_position(j, kept, z_next):
-            y_next = kept
+        def new_velocity(j, h=None):
             nc.vector.scalar_tensor_tensor(
-                out=y_next[:], in0=z_next[:], scalar=dt_col[:, 0:1], in1=y_sb[:, j, :], op0=ALU.mult, op1=ALU.add
+                out=z_next[j][:, columns(h)], in0=kept[j][:, columns(h)], scalar=minus_step[:, 0:1],
+                in1=z_next[j][:, columns(h)], op0=ALU.mult, op1=ALU.add,
             )
-            nc.sync.dma_start(out=y_next_rows[:, j, :], in_=y_next[:])
+            nc.sync.dma_start(out=z_next_rows[:, j, columns(h)], in_=z_next[j][:, columns(h)])
 
+        def new_position(j, h=None):
+            nc.vector.scalar_tensor_tensor(
+                out=kept[j][:, columns(h)], in0=z_next[j][:, columns(h)], scalar=dt_col[:, 0:1],
+                in1=y_sb[:, j, columns(h)], op0=ALU.mult, op1=ALU.add,
+            )
+            nc.sync.dma_start(out=y_next_rows[:, j, columns(h)], in_=kept[j][:, columns(h)])
 
-        forces = {}
-        planes = {}
-        kept = {}
-        gamma = {}
-        hg = {}
-        f = {}
-        w = {}
-        v = {}
-        t_cols = {}
-        bb = {}
-        VC = nc.vector.tensor_copy
-        SC = nc.scalar.copy
-        def F(c, k): f[c] = group_feats(c, k)
-        def QF(c): quantise_feats(c, f[c])
-        def W1(n, k): w[n] = group_w1(n, k)
-        def QW1(n): quantise_w1(n, w[n])
-        def B(i, k): bb[0] = group_b(k)
-        def QB(i): quantise_b(bb[0])
-        def V(i, k): v[i] = group_w2(i, k)
-        def QV(i): quantise_w2(i, v[i])
-        def SP(j): forces[j] = spring(j)
-        def DR(j): drive(j, forces[j])
-        def DM(c): t_cols[c] = damping_net(c)
-        def G(j): gamma[j] = damping_of(j, t_cols[j // 2])
-        def W(j): kept[j] = damp(j, gamma[j])
-        def Z(j): new_velocity(j, kept[j], forces[j])
-        def Y(j): new_position(j, kept[j], forces[j])
-        def HID(c, n):
-            if (c, n // 2) not in planes:
-                planes[c, n // 2] = new_h_planes()
-            hidden_layer(c, n, planes[c, n // 2])
-        def RG(c, g, e): hg[c, g] = regroup_hidden(planes[c, g], e)
-        def QH(c, g): quantise_hidden(c, g, hg[c, g])
-        S_ = {}
-        def CONST(i):
-            b1_bank = psum.tile([P, P], F32, tag="bank")
-            nc.tensor.transpose(b1_bank[:], b1_rows[:].bitcast(F32), ident[:])
-            b1_words = resident.tile([P, W1_UNITS], F32)
-            nc.vector.tensor_copy(out=b1_words[:], in_=b1_bank[:, 0:W1_UNITS])
-            b1_col = resident.tile([P, 2 * W1_UNITS], F32)
-            nc.vector.tensor_copy(out=b1_col[:], in_=b1_words[:].bitcast(BF16))
-
-            half_b2_col = resident.tile([P, MODE_TILES], F32)
-            nc.vector.tensor_scalar(out=half_b2_col[:], in0=b2_bf[:], scalar1=0.5, scalar2=None, op0=ALU.mult)
-
-            pull = resident.tile([P, MODES], F32)
-            for half in range(HALVES):
-                cols = slice(half * BANK, (half + 1) * BANK)
-                stiffness_bank = psum.tile([P, BANK], F32, tag="bank")
-                nc.tensor.matmul(
-                    out=stiffness_bank[:], lhsT=pick_stiffness[:], rhs=stiffness_rows[:, cols], start=True, stop=True
-                )
-                nc.vector.tensor_scalar(
-                    out=pull[:, cols], in0=stiffness_bank[:], scalar1=minus_dt[:, 0:1], scalar2=None, op0=ALU.mult
-                )
-            S_['half_b2_col'] = half_b2_col
-            S_['b1_col'] = b1_col
-            S_['pull'] = pull
-        F(0, 0)
-        CONST(0)
-        QF(0)
-        W1(0, 1)
-        SP(0)
-        QW1(0)
-        W1(1, 1)
-        QW1(1)
-        HID(0, 0)
-        W1(2, 1)
-        QW1(2)
-        W1(3, 1)
-        HID(0, 1)
-        QW1(3)
-        B(0, 1)
-        RG(0, 0, VC)
-        QB(0)
-        V(0, 1)
-        HID(0, 2)
-        DR(0)
-        F(1, 0)
-        QV(0)
-        QF(1)
-        V(1, 1)
-        SP(1)
-        HID(0, 3)
-        F(2, 0)
-        RG(0, 1, VC)
-        QV(1)
-        QH(0, 0)
-        QH(0, 1)
-        DR(1)
-        HID(1, 0)
-        HID(1, 1)
-        SP(2)
-        SP(3)
-        DM(0)
-        RG(1, 0, SC)
-        HID(1, 2)
-        SP(4)
-        QF(2)
-        QH(1, 0)
-        G(0)
-        G(1)
-        SP(5)
-        DR(2)
-        HID(1, 3)
-        W(0)
-        W(1)
-        RG(1, 1, SC)
-        HID(2, 0)
-        Z(0)
-        F(3, 0)
-        HID(2, 1)
-        Z(1)
-        RG(2, 0, SC)
-        QH(1, 1)
-        DR(3)
-        HID(2, 2)
-        Y(0)
-        QH(2, 0)
-        DM(1)
-        HID(2, 3)
-        Y(1)
-        RG(2, 1, SC)
-        QF(3)
-        DR(4)
-        G(2)
-        G(3)
-        QH(2, 1)
-        DR(5)
-        SP(6)
-        HID(3, 0)
-        HID(3, 1)
-        RG(3, 0, SC)
-        W(2)
-        W(3)
-        SP(7)
-        DM(2)
-        Z(2)
-        QH(3, 0)
-        HID(3, 2)
-        Z(3)
-        HID(3, 3)
-        RG(3, 1, SC)
-        DR(6)
-        G(4)
-        Y(2)
-        G(5)
-        QH(3, 1)
-        DR(7)
-        Y(3)
-        W(4)
-        W(5)
-        DM(3)
-        Z(4)
-        Z(5)
-        G(6)
-        G(7)
-        Y(4)
-        Y(5)
-        W(6)
-        W(7)
-        Z(6)
-        Z(7)
-        Y(6)
-        Y(7)
+        transpose_feats(0, 0)
+        constants_by_tensor()
+        quantise_feats(0)
+        transpose_w1(0, 1)
+        quantise_w1(0)
+        transpose_w1(1, 1)
+        quantise_w1(1)
+        hidden_units(0, 0)
+        spring(0)
+        transpose_w1(2, 1)
+        quantise_w1(2)
+        spring(1)
+        transpose_w1(3, 1)
+        hidden_units(0, 1)
+        quantise_w1(3)
+        transpose_b(0)
+        hidden_units(0, 2)
+        regroup_hidden(0, 0, nc.vector.tensor_copy)
+        quantise_b()
+        transpose_w2(0, 0)
+        drive(0)
+        transpose_feats(1, 1)
+        quantise_w2(0)
+        hidden_units(0, 3)
+        quantise_hidden(0, 0)
+        quantise_feats(1)
+        transpose_w2(1, 1)
+        regroup_hidden(0, 1, nc.scalar.copy)
+        drive(1)
+        transpose_feats(2, 1)
+        quantise_w2(1)
+        spring(2)
+        quantise_hidden(0, 1)
+        hidden_units(1, 0)
+        hidden_units(1, 1)
+        quantise_feats(2)
+        regroup_hidden(1, 0, nc.scalar.copy)
+        spring(3)
+        hidden_units(1, 2)
+        damping_net(0, 0)
+        damping_net(0, 1)
+        drive(2)
+        hidden_units(1, 3)
+        gamma_half(0, 0)
+        gamma_half(0, 1)
+        store_gamma(0)
+        quantise_hidden(1, 0)
+        gamma_half(1, 0)
+        gamma_half(1, 1)
+        store_gamma(1)
+        spring(4)
+        regroup_hidden(1, 1, nc.scalar.copy)
+        spring(5)
+        hidden_units(2, 0)
+        hidden_units(2, 1)
+        damp(0)
+        damp(1)
+        new_velocity(0)
+        new_velocity(1)
+        quantise_hidden(1, 1)
+        transpose_feats(3, 0)
+        drive(3)
+        new_position(0)
+        hidden_units(2, 2)
+        regroup_hidden(2, 0, nc.scalar.copy)
+        damping_net(1, 0)
+        damping_net(1, 1)
+        new_position(1)
+        quantise_hidden(2, 0)
+        quantise_feats(3)
+        hidden_units(2, 3)
+        drive(4)
+        gamma_half(2, 0)
+        gamma_half(2, 1)
+        store_gamma(2)
+        gamma_half(3, 0)
+        gamma_half(3, 1)
+        store_gamma(3)
+        spring(6)
+        spring(7)
+        regroup_hidden(2, 1, nc.scalar.copy)
+        hidden_units(3, 0)
+        hidden_units(3, 1)
+        damp(2)
+        damp(3)
+        regroup_hidden(3, 0, nc.scalar.copy)
+        drive(5)
+        hidden_units(3, 2)
+        quantise_hidden(2, 1)
+        new_velocity(2)
+        hidden_units(3, 3)
+        new_velocity(3)
+        damping_net(2, 0)
+        damping_net(2, 1)
+        quantise_hidden(3, 0)
+        new_position(2)
+        regroup_hidden(3, 1, nc.scalar.copy)
+        new_position(3)
+        quantise_hidden(3, 1)
+        drive(6)
+        gamma_half(4, 0)
+        gamma_half(4, 1)
+        store_gamma(4)
+        gamma_half(5, 0)
+        gamma_half(5, 1)
+        store_gamma(5)
+        damping_net(3, 0)
+        damp(4)
+        damp(5)
+        gamma_half(6, 0)
+        gamma_half(7, 0)
+        damping_net(3, 1)
+        store_gamma(6, 0)
+        store_gamma(7, 0)
+        new_velocity(4)
+        new_velocity(5)
+        drive(7)
+        gamma_half(6, 1)
+        gamma_half(7, 1)
+        store_gamma(6, 1)
+        store_gamma(7, 1)
+        new_position(4)
+        new_position(5)
+        damp(6, 0)
+        damp(7, 0)
+        new_velocity(6, 0)
+        new_velocity(7, 0)
+        new_position(6, 0)
+        new_position(7, 0)
+        damp(6, 1)
+        damp(7, 1)
+        new_velocity(6, 1)
+        new_velocity(7, 1)
+        new_position(6, 1)
+        new_position(7, 1)

@@ -31,13 +31,11 @@ W1_UNITS = HIDDEN // PAIR
 HALVES = MODES // BANK
 HALF_TILES = BANK // P
 MODE_TILES = HALVES * HALF_TILES
-B_PASSES = MODES // PAIR
-W2_BANKS = HID_PASSES * HALF_TILES // 2
 
 DRIVE_BANKS = 2
 SHARED_BANKS = 8 - DRIVE_BANKS
 RAW_SLOTS = 3
-STAGE_SLOTS = 2 * FEAT_PASSES
+STAGE_SLOTS = (2, 4)
 GAMMA_SLOTS = 3
 KEPT_SLOTS = 4
 
@@ -52,7 +50,7 @@ def tile_instrumentedlocmblock_pa_kernel(
     with ExitStack() as ctx:
         resident = ctx.enter_context(tc.tile_pool(name="resident", bufs=1))
         weights_in = ctx.enter_context(tc.tile_pool(name="weights_in", bufs=RAW_SLOTS))
-        stage = ctx.enter_context(tc.tile_pool(name="stage", bufs=STAGE_SLOTS))
+        stage = ctx.enter_context(tc.tile_pool(name="stage", bufs=2))
         hidden = ctx.enter_context(tc.tile_pool(name="hidden", bufs=2))
         update = ctx.enter_context(tc.tile_pool(name="update", bufs=KEPT_SLOTS))
         psum = ctx.enter_context(tc.psum_pool(name="psum", bufs=SHARED_BANKS))
@@ -93,6 +91,9 @@ def tile_instrumentedlocmblock_pa_kernel(
             raw = weights_in.tile([P, HALF_TILES, HIDDEN], BF16, tag="raw", name="w2_raw%d" % h)
             nc.sync.dma_start(out=raw[:], in_=w2_rows[:, h])
             w2_raw.append(raw)
+
+        idle_rows = resident.tile([P, BANK], BF16)
+        nc.vector.memset(idle_rows[:], 0.0)
 
         dt_bf = resident.tile([P, 1], BF16)
         nc.scalar.dma_start(out=dt_bf[:], in_=dt.partition_broadcast(P))
@@ -167,8 +168,11 @@ def tile_instrumentedlocmblock_pa_kernel(
                     out=pull[:, cols], in0=stiffness_bank[:], scalar1=minus_dt[:, 0:1], scalar2=None, op0=ALU.mult
                 )
 
-        feat_codes = resident.tile([P, FEAT_PASSES, BATCH], U32, align_bytes=64)
-        feat_scales = resident.tile([P, FEAT_PASSES, BATCH], U8, align_bytes=64)
+        def columns(h):
+            return slice(0, MODES) if h is None else slice(h * BANK, (h + 1) * BANK)
+
+        feat_codes = resident.tile([P, CHUNKS, FEAT_PASSES, PAIR], U32, align_bytes=64)
+        feat_scales = resident.tile([P, CHUNKS, FEAT_PASSES, PAIR], U8, align_bytes=64)
         w1_codes = resident.tile([P, W1_UNITS, FEAT_PASSES, PAIR], U32, align_bytes=64)
         w1_scales = resident.tile([P, W1_UNITS, FEAT_PASSES, PAIR], U8, align_bytes=64)
         b_codes = resident.tile([P, MODES], U32, align_bytes=64)
@@ -176,82 +180,93 @@ def tile_instrumentedlocmblock_pa_kernel(
         w2_codes = resident.tile([P, HID_PASSES, MODES], U32, align_bytes=64)
         w2_scales = resident.tile([P, HID_PASSES, MODES], U8, align_bytes=64)
 
-        def transpose_and_group(rows_a, rows_b, by_vector):
-            bank = psum.tile([P, 2, PAIR], F32, tag="bank")
-            for s, rows in enumerate((rows_a, rows_b)):
-                for w in range(2):
-                    nc.tensor.transpose(bank[:, w, s * P : (s + 1) * P], rows[:, w * P : (w + 1) * P], ident[:])
-            grouped = stage.tile([P, PAIR, PACK], BF16, align_bytes=64)
-            copy = nc.vector.tensor_copy if by_vector else nc.scalar.copy
-            copy(out=grouped[:].bitcast(F32), in_=bank[:].rearrange("p w c -> p c w"))
-            return grouped
+        def transpose_and_group(passes, vector_banks):
+            staged = []
+            for i, pair in enumerate(passes):
+                if i % 2 == 0:
+                    count = min(2, len(passes) - i)
+                    staged.append(stage.tile(
+                        [P, count, PAIR, PACK], BF16, tag="staged%d" % count, bufs=STAGE_SLOTS[count - 1], align_bytes=64,
+                        name="staged",
+                    ))
+                bank = psum.tile([P, 2, PAIR], F32, tag="bank")
+                for s, rows in enumerate(pair):
+                    for w in range(2):
+                        nc.tensor.transpose(bank[:, w, s * P : (s + 1) * P], rows[:, w * P : (w + 1) * P], ident[:])
+                copy = nc.vector.tensor_copy if i >= len(passes) - vector_banks else nc.scalar.copy
+                copy(out=staged[-1][:, i % 2].bitcast(F32), in_=bank[:].rearrange("p w c -> p c w"))
+            return staged
 
-        def quantise(grouped, codes, scales):
+        def quantise(staged, codes, scales):
             nc.vector.quantize_mx(
-                out=codes.bitcast(FP8X4), scales=scales, in_=grouped[:].rearrange("p c t -> p (c t)")
+                out=codes.bitcast(FP8X4), scales=scales, in_=staged[:].rearrange("p s c t -> p (s c t)")
             )
+
+        def quantise_passes(staged, codes, scales):
+            for i, tile in enumerate(staged):
+                both = slice(2 * i, min(2 * i + 2, codes.shape[1]))
+                quantise(
+                    tile, codes[:, both, :].rearrange("p s c -> p (s c)"), scales[:, both, :].rearrange("p s c -> p (s c)")
+                )
 
         y_words = y_sb[:].bitcast(F32)
         z_words = z_sb[:].bitcast(F32)
         u_words = u_sb[:].bitcast(F32)
         feat_sources = ((y_words, 0), (y_words, 1), (z_words, 0), (z_words, 1), (u_words, 0))
-        feats_grouped = {}
-        w1_grouped = {}
-        b_grouped = []
-        w2_grouped = {}
+        feats_staged = {}
+        w1_staged = {}
+        b_staged = []
+        w2_staged = {}
+
+        def k_words(g):
+            return slice(g * WORDS, (g + 1) * WORDS)
 
         def transpose_feats(c, vector_banks):
-            feats_grouped[c] = []
-            for g, (words, part) in enumerate(feat_sources):
-                k_words = slice(part * WORDS, (part + 1) * WORDS)
-                feats_grouped[c].append(transpose_and_group(
-                    words[:, 2 * c, k_words], words[:, 2 * c + 1, k_words], g >= FEAT_PASSES - vector_banks
-                ))
+            feats_staged[c] = transpose_and_group(
+                [(words[:, 2 * c, k_words(g)], words[:, 2 * c + 1, k_words(g)]) for words, g in feat_sources], vector_banks
+            )
 
         def quantise_feats(c):
-            cols = slice(c * PAIR, (c + 1) * PAIR)
-            for g, grouped in enumerate(feats_grouped[c]):
-                quantise(grouped, feat_codes[:, g, cols], feat_scales[:, g, cols])
+            quantise_passes(feats_staged[c], feat_codes[:, c], feat_scales[:, c])
 
         def transpose_w1(n, vector_banks):
             words = w1_raw[n][:].bitcast(F32)
-            w1_grouped[n] = []
-            for g in range(FEAT_PASSES):
-                k_words = slice(g * WORDS, (g + 1) * WORDS)
-                w1_grouped[n].append(transpose_and_group(
-                    words[:, 0, k_words], words[:, 1, k_words], g >= FEAT_PASSES - vector_banks
-                ))
+            w1_staged[n] = transpose_and_group(
+                [(words[:, 0, k_words(g)], words[:, 1, k_words(g)]) for g in range(FEAT_PASSES)], vector_banks
+            )
 
         def quantise_w1(n):
-            for g, grouped in enumerate(w1_grouped[n]):
-                quantise(grouped, w1_codes[:, n, g, :], w1_scales[:, n, g, :])
+            quantise_passes(w1_staged[n], w1_codes[:, n], w1_scales[:, n])
 
         def transpose_b(vector_banks):
             words = b_raw[:].bitcast(F32)
-            for i in range(B_PASSES):
-                b_grouped.append(transpose_and_group(
-                    words[:, 2 * i, :], words[:, 2 * i + 1, :], i >= B_PASSES - vector_banks
-                ))
+            b_staged.extend(transpose_and_group(
+                [(words[:, i, :], words[:, i + 1, :]) for i in range(0, MODE_TILES, 2)], vector_banks
+            ))
 
         def quantise_b():
-            for i, grouped in enumerate(b_grouped):
-                cols = slice(i * PAIR, (i + 1) * PAIR)
-                quantise(grouped, b_codes[:, cols], b_scales[:, cols])
+            for h, staged in enumerate(b_staged):
+                quantise(staged, b_codes[:, columns(h)], b_scales[:, columns(h)])
 
         def transpose_w2(h, vector_banks):
             words = w2_raw[h][:].bitcast(F32)
-            w2_grouped[h] = []
-            for g in range(HID_PASSES):
-                k_words = slice(g * WORDS, (g + 1) * WORDS)
-                for q in range(0, HALF_TILES, 2):
-                    by_vector = len(w2_grouped[h]) >= W2_BANKS - vector_banks
-                    w2_grouped[h].append(transpose_and_group(words[:, q, k_words], words[:, q + 1, k_words], by_vector))
+            w2_staged[h] = transpose_and_group(
+                [
+                    (words[:, q, k_words(g)], words[:, q + 1, k_words(g)])
+                    for g in range(HID_PASSES)
+                    for q in range(0, HALF_TILES, 2)
+                ],
+                vector_banks,
+            )
 
         def quantise_w2(h):
-            for i, grouped in enumerate(w2_grouped[h]):
-                g, first = i // 2, h * BANK + (i % 2) * PAIR
-                cols = slice(first, first + PAIR)
-                quantise(grouped, w2_codes[:, g, cols], w2_scales[:, g, cols])
+            for g, staged in enumerate(w2_staged[h]):
+                quantise(staged, w2_codes[:, g, columns(h)], w2_scales[:, g, columns(h)])
+
+        def idle_products(count):
+            bank = psum.tile([P, BANK], F32, tag="bank")
+            for i in range(count):
+                nc.tensor.matmul(out=bank[:], lhsT=idle_rows[:, 0:P], rhs=idle_rows[:], start=True, stop=True)
 
         h_planes = {}
         h_grouped = {}
@@ -259,7 +274,6 @@ def tile_instrumentedlocmblock_pa_kernel(
         h_scales = {}
 
         def hidden_units(c, n):
-            cols = slice(c * PAIR, (c + 1) * PAIR)
             if n % 2 == 0:
                 h_planes[c, n // 2] = hidden.tile([P, PACK, PAIR], BF16, tag="planes", name="planes%d_%d" % (c, n // 2))
             for e in range(2):
@@ -270,8 +284,8 @@ def tile_instrumentedlocmblock_pa_kernel(
                         out=acc[:],
                         lhsT=w1_codes[:, n, g, units].bitcast(FP8X4),
                         lhsT_scale=w1_scales[:, n, g, units],
-                        rhs=feat_codes[:, g, cols].bitcast(FP8X4),
-                        rhs_scale=feat_scales[:, g, cols],
+                        rhs=feat_codes[:, c, g, :].bitcast(FP8X4),
+                        rhs_scale=feat_scales[:, c, g, :],
                         start=(g == 0),
                         stop=(g == FEAT_PASSES - 1),
                     )
@@ -281,9 +295,9 @@ def tile_instrumentedlocmblock_pa_kernel(
                 )
 
         def regroup_hidden(c, g, copy):
-            grouped = hidden.tile([P, PAIR, PACK], BF16, tag="grouped", align_bytes=64)
+            grouped = hidden.tile([P, 1, PAIR, PACK], BF16, tag="grouped", align_bytes=64)
             copy(
-                out=grouped[:].rearrange("p (c i) t -> p c t i", i=4),
+                out=grouped[:, 0].rearrange("p (c i) t -> p c t i", i=4),
                 in_=h_planes[c, g][:].rearrange("p t (c i) -> p c t i", i=4),
             )
             h_grouped[c, g] = grouped
@@ -299,21 +313,18 @@ def tile_instrumentedlocmblock_pa_kernel(
         gammas = {}
         kept = {}
 
-        def columns(h):
-            return slice(0, MODES) if h is None else slice(h * BANK, (h + 1) * BANK)
-
         def spring(j):
             z_next[j] = update.tile([P, MODES], F32, tag="z_next", bufs=ROW_TILES, name="z_next%d" % j)
             nc.vector.tensor_tensor(out=z_next[j][:], in0=pull[:], in1=y_sb[:, j, :], op=ALU.mult)
 
         def drive(j):
-            rows = slice(j * P, (j + 1) * P)
+            c, rows = j // 2, slice((j % 2) * P, (j % 2 + 1) * P)
             for h in range(HALVES):
                 acc = drive_psum.tile([P, BANK], F32, tag="drive")
                 nc.tensor.matmul_mx(
                     out=acc[:],
-                    lhsT=feat_codes[:, FEAT_PASSES - 1, rows].bitcast(FP8X4),
-                    lhsT_scale=feat_scales[:, FEAT_PASSES - 1, rows],
+                    lhsT=feat_codes[:, c, FEAT_PASSES - 1, rows].bitcast(FP8X4),
+                    lhsT_scale=feat_scales[:, c, FEAT_PASSES - 1, rows],
                     rhs=b_codes[:, columns(h)].bitcast(FP8X4),
                     rhs_scale=b_scales[:, columns(h)],
                     start=True,
@@ -382,16 +393,20 @@ def tile_instrumentedlocmblock_pa_kernel(
             )
             nc.sync.dma_start(out=y_next_rows[:, j, columns(h)], in_=kept[j][:, columns(h)])
 
+        idle_products(6)
         transpose_feats(0, 0)
         constants_by_tensor()
         quantise_feats(0)
+        idle_products(3)
         transpose_w1(0, 1)
         quantise_w1(0)
+        idle_products(3)
         transpose_w1(1, 1)
         quantise_w1(1)
         hidden_units(0, 0)
         spring(0)
         transpose_w1(2, 1)
+        idle_products(2)
         quantise_w1(2)
         spring(1)
         transpose_w1(3, 1)

@@ -412,63 +412,64 @@ def tile_instrumentedlocmblock_pa_kernel(
         transpose_w1(3, 1)
         hidden_units(0, 1)
         quantise_w1(3)
-        transpose_b(0)
-        hidden_units(0, 2)
+        transpose_b(1)
         regroup_hidden(0, 0, nc.vector.tensor_copy)
         quantise_b()
-        transpose_w2(0, 0)
+        transpose_w2(0, 1)
+        hidden_units(0, 2)
         drive(0)
-        transpose_feats(1, 1)
-        quantise_w2(0)
         hidden_units(0, 3)
-        quantise_hidden(0, 0)
+        quantise_w2(0)
+        transpose_feats(1, 1)
+        spring(2)
         quantise_feats(1)
-        transpose_w2(1, 1)
+        transpose_w2(1, 0)
+        quantise_hidden(0, 0)
         regroup_hidden(0, 1, nc.scalar.copy)
         drive(1)
-        transpose_feats(2, 1)
+        transpose_feats(2, 0)
         quantise_w2(1)
-        spring(2)
-        quantise_hidden(0, 1)
         hidden_units(1, 0)
         hidden_units(1, 1)
-        quantise_feats(2)
-        regroup_hidden(1, 0, nc.scalar.copy)
         spring(3)
-        hidden_units(1, 2)
+        quantise_hidden(0, 1)
+        drive(2)
+        regroup_hidden(1, 0, nc.vector.tensor_copy)
         damping_net(0, 0)
         damping_net(0, 1)
-        drive(2)
+        hidden_units(1, 2)
+        spring(4)
         hidden_units(1, 3)
+        quantise_feats(2)
+        drive(3)
         gamma_half(0, 0)
         gamma_half(0, 1)
         store_gamma(0)
-        quantise_hidden(1, 0)
         gamma_half(1, 0)
         gamma_half(1, 1)
         store_gamma(1)
-        spring(4)
-        regroup_hidden(1, 1, nc.scalar.copy)
         spring(5)
-        hidden_units(2, 0)
-        hidden_units(2, 1)
+        quantise_hidden(1, 0)
+        regroup_hidden(1, 1, nc.vector.tensor_copy)
+        transpose_feats(3, 0)
         damp(0)
         damp(1)
-        new_velocity(0)
-        new_velocity(1)
         quantise_hidden(1, 1)
-        transpose_feats(3, 0)
-        drive(3)
-        new_position(0)
-        hidden_units(2, 2)
+        hidden_units(2, 0)
+        new_velocity(0)
+        hidden_units(2, 1)
+        quantise_feats(3)
+        new_velocity(1)
+        drive(4)
         regroup_hidden(2, 0, nc.scalar.copy)
+        hidden_units(2, 2)
         damping_net(1, 0)
         damping_net(1, 1)
-        new_position(1)
+        new_position(0)
         quantise_hidden(2, 0)
-        quantise_feats(3)
+        new_position(1)
         hidden_units(2, 3)
-        drive(4)
+        drive(5)
         gamma_half(2, 0)
         gamma_half(2, 1)
         store_gamma(2)
@@ -476,26 +477,24 @@ def tile_instrumentedlocmblock_pa_kernel(
         gamma_half(3, 1)
         store_gamma(3)
         spring(6)
-        spring(7)
-        regroup_hidden(2, 1, nc.scalar.copy)
-        hidden_units(3, 0)
-        hidden_units(3, 1)
         damp(2)
         damp(3)
-        regroup_hidden(3, 0, nc.scalar.copy)
-        drive(5)
-        hidden_units(3, 2)
-        quantise_hidden(2, 1)
+        regroup_hidden(2, 1, nc.scalar.copy)
+        hidden_units(3, 0)
         new_velocity(2)
-        hidden_units(3, 3)
+        quantise_hidden(2, 1)
+        hidden_units(3, 1)
         new_velocity(3)
+        regroup_hidden(3, 0, nc.scalar.copy)
+        spring(7)
+        hidden_units(3, 2)
+        hidden_units(3, 3)
+        new_position(2)
+        quantise_hidden(3, 0)
         damping_net(2, 0)
         damping_net(2, 1)
-        quantise_hidden(3, 0)
-        new_position(2)
-        regroup_hidden(3, 1, nc.scalar.copy)
         new_position(3)
-        quantise_hidden(3, 1)
+        regroup_hidden(3, 1, nc.scalar.copy)
         drive(6)
         gamma_half(4, 0)
         gamma_half(4, 1)
@@ -503,23 +502,24 @@ def tile_instrumentedlocmblock_pa_kernel(
         gamma_half(5, 0)
         gamma_half(5, 1)
         store_gamma(5)
+        quantise_hidden(3, 1)
         damping_net(3, 0)
         damp(4)
         damp(5)
-        gamma_half(6, 0)
-        gamma_half(7, 0)
-        damping_net(3, 1)
-        store_gamma(6, 0)
-        store_gamma(7, 0)
         new_velocity(4)
         new_velocity(5)
         drive(7)
+        gamma_half(6, 0)
+        gamma_half(7, 0)
+        store_gamma(6, 0)
+        store_gamma(7, 0)
+        damping_net(3, 1)
+        new_position(4)
+        new_position(5)
         gamma_half(6, 1)
         gamma_half(7, 1)
         store_gamma(6, 1)
         store_gamma(7, 1)
-        new_position(4)
-        new_position(5)
         damp(6, 0)
         damp(7, 0)
         new_velocity(6, 0)

@@ -171,14 +171,14 @@ def tile_instrumentedlocmblock_pa_kernel(
         def columns(h):
             return slice(0, MODES) if h is None else slice(h * BANK, (h + 1) * BANK)
 
-        feat_codes = resident.tile([P, CHUNKS, FEAT_PASSES, PAIR], U32, align_bytes=64)
-        feat_scales = resident.tile([P, CHUNKS, FEAT_PASSES, PAIR], U8, align_bytes=64)
-        w1_codes = resident.tile([P, W1_UNITS, FEAT_PASSES, PAIR], U32, align_bytes=64)
-        w1_scales = resident.tile([P, W1_UNITS, FEAT_PASSES, PAIR], U8, align_bytes=64)
-        b_codes = resident.tile([P, MODES], U32, align_bytes=64)
-        b_scales = resident.tile([P, MODES], U8, align_bytes=64)
-        w2_codes = resident.tile([P, HID_PASSES, MODES], U32, align_bytes=64)
-        w2_scales = resident.tile([P, HID_PASSES, MODES], U8, align_bytes=64)
+        feat_codes = resident.tile([P, CHUNKS, FEAT_PASSES, PAIR], U32, align_bytes=256)
+        feat_scales = resident.tile([P, CHUNKS, FEAT_PASSES, PAIR], U8, align_bytes=256)
+        w1_codes = resident.tile([P, W1_UNITS, FEAT_PASSES, PAIR], U32, align_bytes=256)
+        w1_scales = resident.tile([P, W1_UNITS, FEAT_PASSES, PAIR], U8, align_bytes=256)
+        b_codes = resident.tile([P, MODES], U32, align_bytes=256)
+        b_scales = resident.tile([P, MODES], U8, align_bytes=256)
+        w2_codes = resident.tile([P, HID_PASSES, MODES], U32, align_bytes=256)
+        w2_scales = resident.tile([P, HID_PASSES, MODES], U8, align_bytes=256)
 
         def transpose_and_group(passes, vector_banks):
             staged = []
@@ -304,8 +304,8 @@ def tile_instrumentedlocmblock_pa_kernel(
 
         def quantise_hidden(c, g):
             if g == 0:
-                h_codes[c] = hidden.tile([P, HID_PASSES, PAIR], U32, tag="codes", align_bytes=64, name="h_codes%d" % c)
-                h_scales[c] = hidden.tile([P, HID_PASSES, PAIR], U8, tag="scales", align_bytes=64, name="h_scales%d" % c)
+                h_codes[c] = hidden.tile([P, HID_PASSES, PAIR], U32, tag="codes", align_bytes=256, name="h_codes%d" % c)
+                h_scales[c] = hidden.tile([P, HID_PASSES, PAIR], U8, tag="scales", align_bytes=256, name="h_scales%d" % c)
             quantise(h_grouped[c, g], h_codes[c][:, g, :], h_scales[c][:, g, :])
 
         z_next = {}
@@ -418,9 +418,9 @@ def tile_instrumentedlocmblock_pa_kernel(
         transpose_w2(0, 1)
         hidden_units(0, 2)
         drive(0)
-        hidden_units(0, 3)
         quantise_w2(0)
         transpose_feats(1, 1)
+        hidden_units(0, 3)
         spring(2)
         quantise_feats(1)
         transpose_w2(1, 0)
@@ -439,23 +439,25 @@ def tile_instrumentedlocmblock_pa_kernel(
         damping_net(0, 1)
         hidden_units(1, 2)
         spring(4)
+        spring(5)
         hidden_units(1, 3)
         quantise_feats(2)
         drive(3)
+        spring(6)
         gamma_half(0, 0)
         gamma_half(0, 1)
         store_gamma(0)
         gamma_half(1, 0)
         gamma_half(1, 1)
         store_gamma(1)
-        spring(5)
         quantise_hidden(1, 0)
         regroup_hidden(1, 1, nc.vector.tensor_copy)
+        spring(7)
+        hidden_units(2, 0)
         transpose_feats(3, 0)
         damp(0)
         damp(1)
         quantise_hidden(1, 1)
-        hidden_units(2, 0)
         new_velocity(0)
         hidden_units(2, 1)
         quantise_feats(3)
@@ -476,7 +478,6 @@ def tile_instrumentedlocmblock_pa_kernel(
         gamma_half(3, 0)
         gamma_half(3, 1)
         store_gamma(3)
-        spring(6)
         damp(2)
         damp(3)
         regroup_hidden(2, 1, nc.scalar.copy)
@@ -486,7 +487,6 @@ def tile_instrumentedlocmblock_pa_kernel(
         hidden_units(3, 1)
         new_velocity(3)
         regroup_hidden(3, 0, nc.scalar.copy)
-        spring(7)
         hidden_units(3, 2)
         hidden_units(3, 3)
         new_position(2)

@@ -433,17 +433,17 @@ def tile_instrumentedlocmblock_pa_kernel(
         hidden_units(1, 1)
         spring(3)
         quantise_hidden(0, 1)
+        spring(4)
         drive(2)
         regroup_hidden(1, 0, nc.vector.tensor_copy)
         damping_net(0, 0)
         damping_net(0, 1)
         hidden_units(1, 2)
-        spring(4)
         spring(5)
         hidden_units(1, 3)
         quantise_feats(2)
-        drive(3)
         spring(6)
+        drive(3)
         gamma_half(0, 0)
         gamma_half(0, 1)
         store_gamma(0)
@@ -494,7 +494,7 @@ def tile_instrumentedlocmblock_pa_kernel(
         damping_net(2, 0)
         damping_net(2, 1)
         new_position(3)
-        regroup_hidden(3, 1, nc.scalar.copy)
+        regroup_hidden(3, 1, nc.vector.tensor_copy)
         drive(6)
         gamma_half(4, 0)
         gamma_half(4, 1)

from contextlib import ExitStack

import concourse.mybir as mybir
from concourse.masks import make_identity

BF16 = mybir.dt.bfloat16
F32 = mybir.dt.float32
U32 = mybir.dt.uint32
U8 = mybir.dt.uint8
FP8X4 = mybir.dt.float8_e4m3fn_x4
ALU = mybir.AluOpType
ACT = mybir.ActivationFunctionType

P = 128
PACK = 4
K_PASS = P * PACK
WORDS = K_PASS // 2
BANK = 512
PAIR = 2 * P

BATCH = 1024
MODES = 1024
DRIVE = 512
HIDDEN = 1024
FEATS = 2 * MODES + DRIVE
ROW_TILES = BATCH // P
CHUNKS = BATCH // PAIR
FEAT_PASSES = FEATS // K_PASS
HID_PASSES = HIDDEN // K_PASS
W1_UNITS = HIDDEN // PAIR
HALVES = MODES // BANK
HALF_TILES = BANK // P
MODE_TILES = HALVES * HALF_TILES

DRIVE_BANKS = 2
SHARED_BANKS = 8 - DRIVE_BANKS
RAW_SLOTS = 3
STAGE_SLOTS = (2, 4)
GAMMA_SLOTS = 3
KEPT_SLOTS = 4

FLOPS = 2 * BATCH * (HIDDEN * FEATS + MODES * DRIVE + MODES * HIDDEN)


def tile_instrumentedlocmblock_pa_kernel(
    tc, y_tilde, z_tilde, u, dt, omega_sq, alpha_lambda, B_tilde, dmlp_w1, dmlp_b1, dmlp_w2, dmlp_b2,
    out_0, out_1, out_2,
):
    nc = tc.nc
    with ExitStack() as ctx:
        resident = ctx.enter_context(tc.tile_pool(name="resident", bufs=1))
        weights_in = ctx.enter_context(tc.tile_pool(name="weights_in", bufs=RAW_SLOTS))
        stage = ctx.enter_context(tc.tile_pool(name="stage", bufs=2))
        hidden = ctx.enter_context(tc.tile_pool(name="hidden", bufs=2))
        update = ctx.enter_context(tc.tile_pool(name="update", bufs=KEPT_SLOTS))
        psum = ctx.enter_context(tc.psum_pool(name="psum", bufs=SHARED_BANKS))
        drive_psum = ctx.enter_context(tc.psum_pool(name="drive_psum", bufs=DRIVE_BANKS))
        ctx.enter_context(tc.manual_schedule())

        y_rows = y_tilde.rearrange("(p j) r -> p j r", j=ROW_TILES)
        z_rows = z_tilde.rearrange("(p j) r -> p j r", j=ROW_TILES)
        u_rows = u.rearrange("(p j) k -> p j k", j=ROW_TILES)
        z_next_rows = out_0.rearrange("(p j) r -> p j r", j=ROW_TILES)
        gamma_rows = out_1.rearrange("(p j) r -> p j r", j=ROW_TILES)
        y_next_rows = out_2.rearrange("(p j) r -> p j r", j=ROW_TILES)
        y_sb = resident.tile([P, ROW_TILES, MODES], BF16)
        z_sb = resident.tile([P, ROW_TILES, MODES], BF16)
        u_sb = resident.tile([P, ROW_TILES, DRIVE], BF16)

        def load_y(c):
            tiles = slice(2 * c, 2 * c + 2)
            nc.sync.dma_start(out=y_sb[:, tiles, :], in_=y_rows[:, tiles, :])

        def load_zu(c):
            tiles = slice(2 * c, 2 * c + 2)
            nc.sync.dma_start(out=z_sb[:, tiles, :], in_=z_rows[:, tiles, :])
            nc.sync.dma_start(out=u_sb[:, tiles, :], in_=u_rows[:, tiles, :])

        w1_rows = dmlp_w1.rearrange("(n p e) f -> n p e f", p=P, e=2)
        b_rows = B_tilde.rearrange("(h p q) k -> p h q k", p=P, q=HALF_TILES)
        w2_rows = dmlp_w2.rearrange("(h p q) k -> p h q k", p=P, q=HALF_TILES)
        w1_raw = []
        w2_raw = []

        def load_w1(n):
            raw = weights_in.tile([P, 2, FEATS], BF16, tag="raw", name="w1_raw%d" % n)
            nc.sync.dma_start(out=raw[:], in_=w1_rows[n])
            w1_raw.append(raw)

        def load_w2(h):
            raw = weights_in.tile([P, HALF_TILES, HIDDEN], BF16, tag="raw", name="w2_raw%d" % h)
            nc.sync.dma_start(out=raw[:], in_=w2_rows[:, h])
            w2_raw.append(raw)

        idle_rows = resident.tile([P, BANK], BF16)
        nc.vector.memset(idle_rows[:], 0.0)

        dt_bf = resident.tile([P, 1], BF16)
        nc.scalar.dma_start(out=dt_bf[:], in_=dt.partition_broadcast(P))
        b1_rows = resident.tile([P, 2 * P], BF16)
        nc.vector.memset(b1_rows[:], 0.0)
        nc.scalar.dma_start(out=b1_rows[0:W1_UNITS, :], in_=dmlp_b1.rearrange("(n w) -> n w", n=W1_UNITS))
        b2_bf = resident.tile([P, HALVES, HALF_TILES], BF16)
        nc.scalar.dma_start(out=b2_bf[:], in_=dmlp_b2.rearrange("(h p q) -> p h q", p=P, q=HALF_TILES))
        stiffness_rows = resident.tile([P, MODES], BF16)
        nc.vector.memset(stiffness_rows[:], 0.0)
        nc.scalar.dma_start(out=stiffness_rows[0:1, :], in_=omega_sq.rearrange("(o r) -> o r", o=1))
        nc.scalar.dma_start(out=stiffness_rows[32:33, :], in_=alpha_lambda.rearrange("(o r) -> o r", o=1))

        load_y(0)
        load_zu(0)
        for n in range(W1_UNITS):
            load_w1(n)
        b_raw = weights_in.tile([P, MODE_TILES, DRIVE], BF16, tag="raw")
        nc.sync.dma_start(out=b_raw[:].rearrange("p (h q) k -> p h q k", q=HALF_TILES), in_=b_rows)
        for h in range(HALVES):
            load_w2(h)
        for c in range(1, CHUNKS):
            load_y(c)
            load_zu(c)
        ident = resident.tile([P, P], F32)
        make_identity(nc, ident[:])

        warm = resident.tile([P, 1], F32)
        nc.vector.memset(warm[:], 0.0)
        nc.scalar.activation(out=warm[:], in_=warm[:], func=ACT.Tanh)

        pick_stiffness = resident.tile([P, P], BF16)
        nc.vector.memset(pick_stiffness[:], 0.0)
        nc.vector.memset(pick_stiffness[0:32, :], 1.0)
        nc.vector.memset(pick_stiffness[32:64, :], -1.0)

        dt_col = resident.tile([P, 1], F32)
        minus_dt = resident.tile([P, 1], F32)
        dt_size = resident.tile([P, 1], F32)
        tiny_step = resident.tile([P, 1], F32)
        minus_step = resident.tile([P, 1], F32)
        minus_rate = resident.tile([P, 1], F32)
        nc.vector.tensor_copy(out=dt_col[:], in_=dt_bf[:])
        nc.vector.tensor_scalar(out=minus_dt[:], in0=dt_col[:], scalar1=-1.0, scalar2=None, op0=ALU.mult)
        nc.vector.tensor_tensor(out=dt_size[:], in0=dt_col[:], in1=minus_dt[:], op=ALU.max)
        nc.vector.tensor_scalar(
            out=tiny_step[:], in0=dt_size[:], scalar1=1e-20, scalar2=1e-20, op0=ALU.is_lt, op1=ALU.mult
        )
        nc.vector.tensor_tensor(out=minus_step[:], in0=minus_dt[:], in1=tiny_step[:], op=ALU.subtract)
        nc.vector.reciprocal(out=minus_rate[:], in_=minus_step[:])

        half_b2_col = resident.tile([P, MODE_TILES], F32)
        nc.vector.tensor_scalar(
            out=half_b2_col[:], in0=b2_bf[:].rearrange("p h q -> p (h q)"), scalar1=0.5, scalar2=None, op0=ALU.mult
        )
        b1_words = resident.tile([P, W1_UNITS], F32)
        b1_col = resident.tile([P, 2 * W1_UNITS], F32)
        pull = resident.tile([P, MODES], F32)

        def constants_by_tensor():
            b1_bank = psum.tile([P, P], F32, tag="bank")
            nc.tensor.transpose(b1_bank[:], b1_rows[:].bitcast(F32), ident[:])
            nc.vector.tensor_copy(out=b1_words[:], in_=b1_bank[:, 0:W1_UNITS])
            nc.vector.tensor_copy(out=b1_col[:], in_=b1_words[:].bitcast(BF16))
            for h in range(HALVES):
                cols = slice(h * BANK, (h + 1) * BANK)
                stiffness_bank = psum.tile([P, BANK], F32, tag="bank")
                nc.tensor.matmul(
                    out=stiffness_bank[:], lhsT=pick_stiffness[:], rhs=stiffness_rows[:, cols], start=True, stop=True
                )
                nc.vector.tensor_scalar(
                    out=pull[:, cols], in0=stiffness_bank[:], scalar1=minus_dt[:, 0:1], scalar2=None, op0=ALU.mult
                )

        def columns(h):
            return slice(0, MODES) if h is None else slice(h * BANK, (h + 1) * BANK)

        feat_codes = resident.tile([P, CHUNKS, FEAT_PASSES, PAIR], U32, align_bytes=256)
        feat_scales = resident.tile([P, CHUNKS, FEAT_PASSES, PAIR], U8, align_bytes=256)
        w1_codes = resident.tile([P, W1_UNITS, FEAT_PASSES, PAIR], U32, align_bytes=256)
        w1_scales = resident.tile([P, W1_UNITS, FEAT_PASSES, PAIR], U8, align_bytes=256)
        b_codes = resident.tile([P, MODES], U32, align_bytes=256)
        b_scales = resident.tile([P, MODES], U8, align_bytes=256)
        w2_codes = resident.tile([P, HID_PASSES, MODES], U32, align_bytes=256)
        w2_scales = resident.tile([P, HID_PASSES, MODES], U8, align_bytes=256)

        def transpose_and_group(passes, vector_banks):
            staged = []
            for i, pair in enumerate(passes):
                if i % 2 == 0:
                    count = min(2, len(passes) - i)
                    staged.append(stage.tile(
                        [P, count, PAIR, PACK], BF16, tag="staged%d" % count, bufs=STAGE_SLOTS[count - 1], align_bytes=64,
                        name="staged",
                    ))
                bank = psum.tile([P, 2, PAIR], F32, tag="bank")
                for s, rows in enumerate(pair):
                    for w in range(2):
                        nc.tensor.transpose(bank[:, w, s * P : (s + 1) * P], rows[:, w * P : (w + 1) * P], ident[:])
                copy = nc.vector.tensor_copy if i >= len(passes) - vector_banks else nc.scalar.copy
                copy(out=staged[-1][:, i % 2].bitcast(F32), in_=bank[:].rearrange("p w c -> p c w"))
            return staged

        def quantise(staged, codes, scales):
            nc.vector.quantize_mx(
                out=codes.bitcast(FP8X4), scales=scales, in_=staged[:].rearrange("p s c t -> p (s c t)")
            )

        def quantise_passes(staged, codes, scales):
            for i, tile in enumerate(staged):
                both = slice(2 * i, min(2 * i + 2, codes.shape[1]))
                quantise(
                    tile, codes[:, both, :].rearrange("p s c -> p (s c)"), scales[:, both, :].rearrange("p s c -> p (s c)")
                )

        y_words = y_sb[:].bitcast(F32)
        z_words = z_sb[:].bitcast(F32)
        u_words = u_sb[:].bitcast(F32)
        feat_sources = ((y_words, 0), (y_words, 1), (z_words, 0), (z_words, 1), (u_words, 0))
        feats_staged = {}
        w1_staged = {}
        b_staged = []
        w2_staged = {}

        def k_words(g):
            return slice(g * WORDS, (g + 1) * WORDS)

        def transpose_feats(c, vector_banks):
            feats_staged[c] = transpose_and_group(
                [(words[:, 2 * c, k_words(g)], words[:, 2 * c + 1, k_words(g)]) for words, g in feat_sources], vector_banks
            )

        def quantise_feats(c):
            quantise_passes(feats_staged[c], feat_codes[:, c], feat_scales[:, c])

        def transpose_w1(n, vector_banks):
            words = w1_raw[n][:].bitcast(F32)
            w1_staged[n] = transpose_and_group(
                [(words[:, 0, k_words(g)], words[:, 1, k_words(g)]) for g in range(FEAT_PASSES)], vector_banks
            )

        def quantise_w1(n):
            quantise_passes(w1_staged[n], w1_codes[:, n], w1_scales[:, n])

        def transpose_b(vector_banks):
            words = b_raw[:].bitcast(F32)
            b_staged.extend(transpose_and_group(
                [(words[:, i, :], words[:, i + 1, :]) for i in range(0, MODE_TILES, 2)], vector_banks
            ))

        def quantise_b():
            for h, staged in enumerate(b_staged):
                quantise(staged, b_codes[:, columns(h)], b_scales[:, columns(h)])

        def transpose_w2(h, vector_banks):
            words = w2_raw[h][:].bitcast(F32)
            w2_staged[h] = transpose_and_group(
                [
                    (words[:, q, k_words(g)], words[:, q + 1, k_words(g)])
                    for g in range(HID_PASSES)
                    for q in range(0, HALF_TILES, 2)
                ],
                vector_banks,
            )

        def quantise_w2(h):
            for g, staged in enumerate(w2_staged[h]):
                quantise(staged, w2_codes[:, g, columns(h)], w2_scales[:, g, columns(h)])

        def idle_products(count):
            bank = psum.tile([P, BANK], F32, tag="bank")
            for i in range(count):
                nc.tensor.matmul(out=bank[:], lhsT=idle_rows[:, 0:P], rhs=idle_rows[:], start=True, stop=True)

        h_planes = {}
        h_grouped = {}
        h_codes = {}
        h_scales = {}

        def hidden_units(c, n):
            if n % 2 == 0:
                h_planes[c, n // 2] = hidden.tile([P, PACK, PAIR], BF16, tag="planes", name="planes%d_%d" % (c, n // 2))
            for e in range(2):
                units = slice(e * P, (e + 1) * P)
                acc = psum.tile([P, PAIR], F32, tag="bank")
                for g in range(FEAT_PASSES):
                    nc.tensor.matmul_mx(
                        out=acc[:],
                        lhsT=w1_codes[:, n, g, units].bitcast(FP8X4),
                        lhsT_scale=w1_scales[:, n, g, units],
                        rhs=feat_codes[:, c, g, :].bitcast(FP8X4),
                        rhs_scale=feat_scales[:, c, g, :],
                        start=(g == 0),
                        stop=(g == FEAT_PASSES - 1),
                    )
                nc.scalar.activation(
                    out=h_planes[c, n // 2][:, 2 * (n % 2) + e, :], in_=acc[:], func=ACT.Tanh,
                    bias=b1_col[:, 2 * n + e : 2 * n + e + 1], scale=1.0,
                )

        def regroup_hidden(c, g, copy):
            grouped = hidden.tile([P, 1, PAIR, PACK], BF16, tag="grouped", align_bytes=64)
            copy(
                out=grouped[:, 0].rearrange("p (c i) t -> p c t i", i=4),
                in_=h_planes[c, g][:].rearrange("p t (c i) -> p c t i", i=4),
            )
            h_grouped[c, g] = grouped

        def quantise_hidden(c, g):
            if g == 0:
                h_codes[c] = hidden.tile([P, HID_PASSES, PAIR], U32, tag="codes", align_bytes=256, name="h_codes%d" % c)
                h_scales[c] = hidden.tile([P, HID_PASSES, PAIR], U8, tag="scales", align_bytes=256, name="h_scales%d" % c)
            quantise(h_grouped[c, g], h_codes[c][:, g, :], h_scales[c][:, g, :])

        z_next = {}
        t_cols = {}
        gammas = {}
        kept = {}

        def spring(j):
            z_next[j] = update.tile([P, MODES], F32, tag="z_next", bufs=ROW_TILES, name="z_next%d" % j)
            nc.vector.tensor_tensor(out=z_next[j][:], in0=pull[:], in1=y_sb[:, j, :], op=ALU.mult)

        def drive(j):
            c, rows = j // 2, slice((j % 2) * P, (j % 2 + 1) * P)
            for h in range(HALVES):
                acc = drive_psum.tile([P, BANK], F32, tag="drive")
                nc.tensor.matmul_mx(
                    out=acc[:],
                    lhsT=feat_codes[:, c, FEAT_PASSES - 1, rows].bitcast(FP8X4),
                    lhsT_scale=feat_scales[:, c, FEAT_PASSES - 1, rows],
                    rhs=b_codes[:, columns(h)].bitcast(FP8X4),
                    rhs_scale=b_scales[:, columns(h)],
                    start=True,
                    stop=True,
                )
                force = z_next[j][:, columns(h)].rearrange("b (p q) -> b p q", q=HALF_TILES)
                nc.vector.scalar_tensor_tensor(
                    out=force, in0=acc[:].rearrange("b (q p) -> b p q", q=HALF_TILES), scalar=dt_col[:, 0:1],
                    in1=force, op0=ALU.mult, op1=ALU.add,
                )

        def damping_net(c, h):
            if h == 0:
                t_cols[c] = weights_in.tile([P, MODE_TILES, PAIR], F32, tag="raw", name="t_cols%d" % c)
            for i in range(h * HALF_TILES, (h + 1) * HALF_TILES):
                modes = slice(i * P, (i + 1) * P)
                acc = psum.tile([P, PAIR], F32, tag="bank")
                for g in range(HID_PASSES):
                    nc.tensor.matmul_mx(
                        out=acc[:],
                        lhsT=w2_codes[:, g, modes].bitcast(FP8X4),
                        lhsT_scale=w2_scales[:, g, modes],
                        rhs=h_codes[c][:, g, :].bitcast(FP8X4),
                        rhs_scale=h_scales[c][:, g, :],
                        start=(g == 0),
                        stop=(g == HID_PASSES - 1),
                    )
                nc.scalar.activation(
                    out=t_cols[c][:, i, :], in_=acc[:], func=ACT.Tanh, bias=half_b2_col[:, i : i + 1], scale=0.5
                )

        def gamma_half(j, h):
            rows = slice((j % 2) * P, (j % 2 + 1) * P)
            if h == 0:
                gammas[j] = update.tile([P, MODES], F32, tag="gamma", bufs=GAMMA_SLOTS, name="gamma%d" % j)
            bank = psum.tile([P, HALF_TILES, P], F32, tag="bank")
            for q in range(HALF_TILES):
                nc.tensor.transpose(bank[:, q, :], t_cols[j // 2][:, h * HALF_TILES + q, rows], ident[:])
            nc.scalar.activation(
                out=gammas[j][:, columns(h)].rearrange("b (p q) -> b p q", q=HALF_TILES),
                in_=bank[:].rearrange("b q p -> b p q"), func=ACT.Identity, bias=1.0, scale=1.0,
            )

        def store_gamma(j, h=None):
            nc.sync.dma_start(out=gamma_rows[:, j, columns(h)], in_=gammas[j][:, columns(h)])

        def damp(j, h=None):
            if j not in kept:
                kept[j] = update.tile([P, MODES], F32, tag="kept", name="kept%d" % j)
            nc.vector.scalar_tensor_tensor(
                out=kept[j][:, columns(h)], in0=gammas[j][:, columns(h)], scalar=minus_rate[:, 0:1],
                in1=z_sb[:, j, columns(h)], op0=ALU.add, op1=ALU.mult,
            )

        def new_velocity(j, h=None):
            nc.vector.scalar_tensor_tensor(
                out=z_next[j][:, columns(h)], in0=kept[j][:, columns(h)], scalar=minus_step[:, 0:1],
                in1=z_next[j][:, columns(h)], op0=ALU.mult, op1=ALU.add,
            )
            nc.sync.dma_start(out=z_next_rows[:, j, columns(h)], in_=z_next[j][:, columns(h)])

        def new_position(j, h=None):
            nc.vector.scalar_tensor_tensor(
                out=kept[j][:, columns(h)], in0=z_next[j][:, columns(h)], scalar=dt_col[:, 0:1],
                in1=y_sb[:, j, columns(h)], op0=ALU.mult, op1=ALU.add,
            )
            nc.sync.dma_start(out=y_next_rows[:, j, columns(h)], in_=kept[j][:, columns(h)])

        idle_products(6)
        transpose_feats(0, 0)
        constants_by_tensor()
        quantise_feats(0)
        idle_products(3)
        transpose_w1(0, 1)
        quantise_w1(0)
        idle_products(3)
        transpose_w1(1, 1)
        quantise_w1(1)
        hidden_units(0, 0)
        spring(0)
        transpose_w1(2, 1)
        idle_products(2)
        quantise_w1(2)
        spring(1)
        transpose_w1(3, 1)
        hidden_units(0, 1)
        quantise_w1(3)
        transpose_b(1)
        regroup_hidden(0, 0, nc.vector.tensor_copy)
        quantise_b()
        transpose_w2(0, 1)
        hidden_units(0, 2)
        drive(0)
        quantise_w2(0)
        transpose_feats(1, 1)
        hidden_units(0, 3)
        spring(2)
        quantise_feats(1)
        transpose_w2(1, 0)
        quantise_hidden(0, 0)
        regroup_hidden(0, 1, nc.scalar.copy)
        drive(1)
        transpose_feats(2, 0)
        quantise_w2(1)
        hidden_units(1, 0)
        hidden_units(1, 1)
        spring(3)
        quantise_hidden(0, 1)
        spring(4)
        drive(2)
        regroup_hidden(1, 0, nc.vector.tensor_copy)
        damping_net(0, 0)
        damping_net(0, 1)
        hidden_units(1, 2)
        spring(5)
        hidden_units(1, 3)
        quantise_feats(2)
        spring(6)
        drive(3)
        gamma_half(0, 0)
        gamma_half(0, 1)
        store_gamma(0)
        gamma_half(1, 0)
        gamma_half(1, 1)
        store_gamma(1)
        quantise_hidden(1, 0)
        regroup_hidden(1, 1, nc.vector.tensor_copy)
        spring(7)
        hidden_units(2, 0)
        transpose_feats(3, 0)
        damp(0)
        damp(1)
        quantise_hidden(1, 1)
        new_velocity(0)
        hidden_units(2, 1)
        quantise_feats(3)
        new_velocity(1)
        drive(4)
        regroup_hidden(2, 0, nc.scalar.copy)
        hidden_units(2, 2)
        damping_net(1, 0)
        damping_net(1, 1)
        new_position(0)
        quantise_hidden(2, 0)
        new_position(1)
        hidden_units(2, 3)
        drive(5)
        gamma_half(2, 0)
        gamma_half(2, 1)
        store_gamma(2)
        gamma_half(3, 0)
        gamma_half(3, 1)
        store_gamma(3)
        damp(2)
        damp(3)
        regroup_hidden(2, 1, nc.scalar.copy)
        hidden_units(3, 0)
        new_velocity(2)
        quantise_hidden(2, 1)
        hidden_units(3, 1)
        new_velocity(3)
        regroup_hidden(3, 0, nc.scalar.copy)
        hidden_units(3, 2)
        hidden_units(3, 3)
        new_position(2)
        quantise_hidden(3, 0)
        damping_net(2, 0)
        damping_net(2, 1)
        new_position(3)
        regroup_hidden(3, 1, nc.vector.tensor_copy)
        drive(6)
        gamma_half(4, 0)
        gamma_half(4, 1)
        store_gamma(4)
        gamma_half(5, 0)
        gamma_half(5, 1)
        store_gamma(5)
        quantise_hidden(3, 1)
        damping_net(3, 0)
        damp(4)
        damp(5)
        new_velocity(4)
        new_velocity(5)
        drive(7)
        gamma_half(6, 0)
        gamma_half(7, 0)
        store_gamma(6, 0)
        store_gamma(7, 0)
        damping_net(3, 1)
        new_position(4)
        new_position(5)
        gamma_half(6, 1)
        gamma_half(7, 1)
        store_gamma(6, 1)
        store_gamma(7, 1)
        damp(6, 0)
        damp(7, 0)
        new_velocity(6, 0)
        new_velocity(7, 0)
        new_position(6, 0)
        new_position(7, 0)
        damp(6, 1)
        damp(7, 1)
        new_velocity(6, 1)
        new_velocity(7, 1)
        new_position(6, 1)
        new_position(7, 1)
